import numpy as np
import ml_dtypes


def mxq(x, axis, fmt="e4m3"):
    dtype, down = {"e4m3": (ml_dtypes.float8_e4m3fn, 7), "e5m2": (ml_dtypes.float8_e5m2, 14)}[fmt]
    v = np.moveaxis(np.asarray(x, np.float32).astype(ml_dtypes.bfloat16).astype(np.float64), axis, -1)
    blocks = v.reshape(v.shape[:-1] + (-1, 32))
    amax = np.abs(blocks).max(-1, keepdims=True)
    byte = np.maximum(np.where(amax > 0, np.frexp(amax)[1] - 1 + 127, 0) - down, 1)
    scale = np.exp2(byte - 127.0)
    codes = (blocks / scale).astype(np.float32).astype(dtype).astype(np.float64)
    return np.moveaxis((codes * scale).reshape(v.shape), -1, axis)


WIDE = False


def mx_kscale(k):
    if not WIDE:
        return np.ones(k)
    levels = np.array([10, -10, 5, -5, 0])
    a = np.random.permutation(np.resize(levels, k // 512 * 4)).reshape(k // 512, 4)
    idx = np.arange(k)
    return np.exp2(a[idx // 512, idx % 128 // 32])


BF16 = ml_dtypes.bfloat16


def bf(x):
    return np.asarray(x, np.float32).astype(BF16)


def f64(x):
    return np.asarray(x).astype(np.float64)


B, H, KVH, N, D, QB = 8, 4, 2, 512, 128, 512
MASK_VALUE = -float(np.finfo(np.float32).max)
QC = 4.0
BLK = 32


def setup_inputs():
    s = np.array(mx_kscale(N), dtype=np.float64)
    s[:BLK] = s.max()
    q = np.random.standard_normal((B, H, N, D)) * 1.5
    k = np.random.standard_normal((B, KVH, N, D)) * 1.5
    v = np.random.standard_normal((B, KVH, N, D))
    q[..., 0] = QC
    k[..., 0] += np.log2(s) * np.log(2.0) * np.sqrt(D) / QC
    v *= (s.max() / s)[:, None]
    return {"q": bf(q), "k": bf(k), "v": bf(v)}


def rep(a):
    return np.reshape(np.broadcast_to(a[:, None], (B, H // KVH, KVH, N, D)), (B, H, N, D))


def reference(q, k, v):
    q = f64(q)
    k = rep(f64(k))
    vq = rep(mxq(f64(v), 2, "e4m3"))
    outs = []
    for g in range(N // QB):
        lo, hi = g * QB, (g + 1) * QB
        s = q[:, :, lo:hi] @ k[:, :, :hi].transpose(0, 1, 3, 2) * (1.0 / np.sqrt(D))
        mask = np.arange(hi)[None, :] > np.arange(lo, hi)[:, None]
        s = np.where(mask, MASK_VALUE, s)
        e = np.exp(s - s.max(-1, keepdims=True))
        outs.append((mxq(e, 3, "e4m3") @ vq[:, :, :hi]) / e.sum(-1, keepdims=True))
    return np.concatenate(outs, axis=2)

@@ -1,0 +1,206 @@
+import math
+from contextlib import ExitStack
+
+import concourse.mybir as mybir
+from concourse.masks import make_identity
+
+BF16 = mybir.dt.bfloat16
+F32 = mybir.dt.float32
+U32 = mybir.dt.uint32
+U8 = mybir.dt.uint8
+FP8X4 = mybir.dt.float8_e4m3fn_x4
+ALU = mybir.AluOpType
+ACT = mybir.ActivationFunctionType
+
+B, H, KVH, N, D = 8, 4, 2, 512, 128
+P = 128
+NT = N // P
+PACK = 4
+SCALE = 1.0 / math.sqrt(D)
+NEG = -1.0e30
+FLOPS = 4 * B * H * N * N * D
+
+ORD = [2, 0, 1, 3]
+UNITS = [[2, 0], [1], [3]]
+NE = 3
+VEC_EVERY = 8
+
+
+def tile_attend_t_kernel(tc, q, k, v, out):
+    nc = tc.nc
+    with ExitStack() as ctx:
+        const = ctx.enter_context(tc.tile_pool(name="const", bufs=1))
+        res = ctx.enter_context(tc.tile_pool(name="res", bufs=1))
+        qtp = ctx.enter_context(tc.tile_pool(name="qtp", bufs=3))
+        kvp = ctx.enter_context(tc.tile_pool(name="kvp", bufs=2))
+        ktp = ctx.enter_context(tc.tile_pool(name="ktp", bufs=4))
+        gp = ctx.enter_context(tc.tile_pool(name="gp", bufs=4))
+        cp = ctx.enter_context(tc.tile_pool(name="cp", bufs=6))
+        small = ctx.enter_context(tc.tile_pool(name="small", bufs=6))
+        obp = ctx.enter_context(tc.tile_pool(name="obp", bufs=3))
+        ps = ctx.enter_context(tc.psum_pool(name="ps", bufs=1))
+
+        qs, ks, vs = [], [], []
+        for b in range(B):
+            kb = res.tile([P, KVH, N], BF16, name="ks%d" % b)
+            qb = res.tile([P, H * NT, D], BF16, name="qs%d" % b)
+            vb = res.tile([P, KVH, N], BF16, name="vs%d" % b)
+            kview = k[b].rearrange("g (p t) d -> p g (t d)", t=PACK)
+            qview = q[b].rearrange("h (a p) d -> p (h a) d", p=P)
+            if b == 0:
+                nc.sync.dma_start(out=kb[:, 0:1, :], in_=kview[:, 0:1, :])
+                nc.sync.dma_start(out=qb[:, 0:NT, :], in_=qview[:, 0:NT, :])
+                nc.sync.dma_start(out=kb[:, 1:2, :], in_=kview[:, 1:2, :])
+                nc.sync.dma_start(out=qb[:, NT:H * NT, :], in_=qview[:, NT:H * NT, :])
+            else:
+                nc.sync.dma_start(out=kb[:], in_=kview)
+                nc.sync.dma_start(out=qb[:], in_=qview)
+            nc.sync.dma_start(out=vb[:], in_=v[b].rearrange("g (p t) d -> p g (t d)", t=PACK))
+            ks.append(kb)
+            qs.append(qb)
+            vs.append(vb)
+
+        ident = const.tile([P, P], BF16, name="ident")
+        make_identity(nc, ident[:])
+        m32 = const.tile([P, P], F32, name="m32")
+        nc.gpsimd.memset(m32[:], 0.0)
+        nc.gpsimd.affine_select(
+            out=m32[:], in_=m32[:], compare_op=ALU.is_ge, fill=NEG, base=0,
+            pattern=[[-1, P]], channel_multiplier=1,
+        )
+        maskb = const.tile([P, PACK, 32], BF16, name="maskb")
+        nc.vector.tensor_copy(out=maskb[:], in_=m32[:].rearrange("i (p t) -> i t p", t=PACK))
+        es = []
+        for j in range(NE):
+            et = const.tile([P, NT, PACK, P], BF16, name="e%d" % j)
+            if j == 0:
+                nc.vector.memset(et[:, 0:NT - 1], 0.0)
+            else:
+                nc.gpsimd.memset(et[:, 0:NT - 1], 0.0)
+            es.append(et)
+
+        st = {}
+
+        def prep_k(b, g):
+            tk = ps.tile([P, 2 * N], BF16, tag="t", bufs=3, name="tk")
+            for t in range(PACK):
+                nc.tensor.transpose(tk[:, t * P:(t + 1) * P], ks[b][:, g, t * D:(t + 1) * D], ident[:])
+            kt = ktp.tile([P, PACK, P], BF16, name="kt")
+            nc.vector.tensor_copy(out=kt[:].rearrange("d t p -> d (t p)"), in_=tk[:, 0:N])
+            st[("kt", b, g)] = kt
+
+        def prep_v(b):
+            vg = kvp.tile([P, KVH, D, PACK], BF16, name="vg", align_bytes=64)
+            nc.vector.tensor_copy(out=vg[:], in_=vs[b][:].rearrange("p g (t d) -> p g d t", t=PACK))
+            vc = kvp.tile([P, KVH * D], U32, name="vc", align_bytes=64)
+            vsc = kvp.tile([P, KVH * D], U8, name="vsc", align_bytes=64)
+            nc.vector.quantize_mx(
+                out=vc[:].bitcast(FP8X4), scales=vsc[:], in_=vg[:].rearrange("p g d t -> p (g d t)")
+            )
+            st[("kv", b)] = (vc, vsc)
+
+        def stage_a(n):
+            b, h = divmod(n, H)
+            if h < KVH:
+                prep_k(b, h)
+            tq = ps.tile([P, 2 * N], BF16, tag="t", bufs=3, name="tq")
+            for a in range(NT):
+                nc.tensor.transpose(tq[:, a * P:(a + 1) * P], qs[b][:, h * NT + a, :], ident[:])
+            qt = qtp.tile([P, N], BF16, name="qt")
+            nc.vector.tensor_copy(out=qt[:], in_=tq[:, 0:N])
+            st[("qt", n)] = qt
+            if h == 1:
+                prep_v(b)
+
+        def stage_b(n):
+            b, h = divmod(n, H)
+            g = h % KVH
+            kt = st[("kt", b, g)]
+            qt = st[("qt", n)]
+            et = es[n % NE]
+            mx = small.tile([P, NT], F32, name="mx")
+            nb = small.tile([P, NT], F32, name="nb")
+            rs = small.tile([P, NT], F32, name="rs")
+            c0 = 0
+            for unit in UNITS:
+                s = ps.tile([P, N], F32, tag="s", bufs=4, name="s")
+                regs = []
+                off = 0
+                for a in unit:
+                    w = 32 * (a + 1)
+                    flat = s[:, off:off + PACK * w]
+                    reg = flat.rearrange("i (t p) -> i t p", t=PACK)
+                    nc.tensor.matmul(out=reg, lhsT=qt[:, a * P:(a + 1) * P], rhs=kt[:, :, 0:w],
+                                     start=True, stop=False)
+                    nc.tensor.matmul(out=reg[:, :, 32 * a:32 * a + 32], lhsT=ident[:], rhs=maskb[:],
+                                     start=False, stop=True)
+                    regs.append((a, w, flat, reg))
+                    off += PACK * w
+                for i, (a, w, flat, reg) in enumerate(regs):
+                    nc.vector.tensor_reduce(out=mx[:, c0 + i:c0 + i + 1], in_=flat,
+                                            axis=mybir.AxisListType.X, op=ALU.max)
+                c1 = c0 + len(regs)
+                nc.vector.tensor_scalar(out=nb[:, c0:c1], in0=mx[:, c0:c1], scalar1=-SCALE, scalar2=None,
+                                        op0=ALU.mult)
+                for i, (a, w, flat, reg) in enumerate(regs):
+                    nc.scalar.activation(out=et[:, a, :, 0:w], in_=reg, func=ACT.Exp,
+                                         bias=nb[:, c0 + i:c0 + i + 1], scale=SCALE,
+                                         accum_out=rs[:, a:a + 1])
+                c0 = c1
+            st[("rs", n)] = rs
+
+        def stage_c(n):
+            et = es[n % NE]
+            lst = []
+            for j in range(2):
+                xt = ps.tile([P, 2, PACK, P], BF16, tag="t", bufs=3, name="xt")
+                for sl in range(2):
+                    a = ORD[2 * j + sl]
+                    for t in range(PACK):
+                        nc.tensor.transpose(xt[:, sl, t, :], et[:, a, t, :], ident[:])
+                gr = gp.tile([P, 2, P, PACK], BF16, name="gr", align_bytes=64)
+                if (2 * n + j) % VEC_EVERY == VEC_EVERY - 3:
+                    nc.vector.tensor_copy(out=gr[:], in_=xt[:].rearrange("p s t i -> p s i t"))
+                else:
+                    nc.scalar.copy(out=gr[:], in_=xt[:].rearrange("p s t i -> p s i t"))
+                ec = cp.tile([P, 2 * P], U32, name="ec", align_bytes=64)
+                esc = cp.tile([P, 2 * P], U8, name="esc", align_bytes=64)
+                nc.vector.quantize_mx(out=ec[:].bitcast(FP8X4), scales=esc[:],
+                                      in_=gr[:].rearrange("p s i t -> p (s i t)"))
+                lst.append((ec, esc))
+            st[("ec", n)] = lst
+
+        def stage_d(n):
+            b, h = divmod(n, H)
+            g = h % KVH
+            vc, vsc = st[("kv", b)]
+            lst = st[("ec", n)]
+            rs = st[("rs", n)]
+            o = ps.tile([P, NT, D], F32, tag="o", bufs=1, name="o")
+            for c in range(NT):
+                a = ORD[c]
+                ec, esc = lst[c // 2]
+                cols = slice((c % 2) * P, (c % 2) * P + P)
+                nc.tensor.matmul_mx(
+                    out=o[:, a, :],
+                    lhsT=ec[:, cols].bitcast(FP8X4), lhsT_scale=esc[:, cols],
+                    rhs=vc[:, g * D:(g + 1) * D].bitcast(FP8X4), rhs_scale=vsc[:, g * D:(g + 1) * D],
+                    start=True, stop=True,
+                )
+            rinv = small.tile([P, NT], F32, name="rinv")
+            nc.vector.reciprocal(out=rinv[:], in_=rs[:])
+            ob = obp.tile([P, NT, D], F32, name="ob")
+            nc.vector.tensor_tensor(out=ob[:], in0=o[:], in1=rinv[:].unsqueeze(2).to_broadcast([P, NT, D]),
+                                    op=ALU.mult)
+            nc.sync.dma_start(out=out[b, h].rearrange("(a p) d -> p a d", p=P), in_=ob[:])
+
+        nh = B * H
+        for it in range(nh + 3):
+            if it < nh:
+                stage_a(it)
+            if 0 <= it - 1 < nh:
+                stage_b(it - 1)
+            if 0 <= it - 2 < nh:
+                stage_c(it - 2)
+            if 0 <= it - 3 < nh:
+                stage_d(it - 3)

@@ -19,25 +19,27 @@ PACK = 4
 SCALE = 1.0 / math.sqrt(D)
 NEG = -1.0e30
 FLOPS = 4 * B * H * N * N * D
+NH = B * H
 
-ORD = [2, 0, 1, 3]
 UNITS = [[2, 0], [1], [3]]
+UCOL = [0, 2, 3]
+BANKS = [[2, 0], [1, 3]]
 NE = 3
-VEC_EVERY = 8
 
 
 def tile_attend_t_kernel(tc, q, k, v, out):
     nc = tc.nc
     with ExitStack() as ctx:
+        ctx.enter_context(tc.manual_schedule())
         const = ctx.enter_context(tc.tile_pool(name="const", bufs=1))
         res = ctx.enter_context(tc.tile_pool(name="res", bufs=1))
-        qtp = ctx.enter_context(tc.tile_pool(name="qtp", bufs=3))
-        kvp = ctx.enter_context(tc.tile_pool(name="kvp", bufs=2))
+        qtp = ctx.enter_context(tc.tile_pool(name="qtp", bufs=5))
         ktp = ctx.enter_context(tc.tile_pool(name="ktp", bufs=4))
-        gp = ctx.enter_context(tc.tile_pool(name="gp", bufs=4))
+        kvp = ctx.enter_context(tc.tile_pool(name="kvp", bufs=2))
+        gp = ctx.enter_context(tc.tile_pool(name="gp", bufs=1))
         cp = ctx.enter_context(tc.tile_pool(name="cp", bufs=6))
-        small = ctx.enter_context(tc.tile_pool(name="small", bufs=6))
-        obp = ctx.enter_context(tc.tile_pool(name="obp", bufs=3))
+        small = ctx.enter_context(tc.tile_pool(name="small", bufs=9))
+        obp = ctx.enter_context(tc.tile_pool(name="obp", bufs=4))
         ps = ctx.enter_context(tc.psum_pool(name="ps", bufs=1))
 
         qs, ks, vs = [], [], []
@@ -81,15 +83,37 @@ def tile_attend_t_kernel(tc, q, k, v, out):
 
         st = {}
 
-        def prep_k(b, g):
-            tk = ps.tile([P, 2 * N], BF16, tag="t", bufs=3, name="tk")
-            for t in range(PACK):
-                nc.tensor.transpose(tk[:, t * P:(t + 1) * P], ks[b][:, g, t * D:(t + 1) * D], ident[:])
-            kt = ktp.tile([P, PACK, P], BF16, name="kt")
-            nc.vector.tensor_copy(out=kt[:].rearrange("d t p -> d (t p)"), in_=tk[:, 0:N])
-            st[("kt", b, g)] = kt
+        def ok(n):
+            return 0 <= n < NH
 
-        def prep_v(b):
+        def qt_tr(n):
+            if not ok(n):
+                return
+            b, h = divmod(n, H)
+            tq = ps.tile([P, 2 * N], BF16, tag="tq", name="tq")
+            for a in range(NT):
+                nc.tensor.transpose(tq[:, a * P:(a + 1) * P], qs[b][:, h * NT + a, :], ident[:])
+            if h < KVH:
+                for t in range(PACK):
+                    nc.tensor.transpose(tq[:, N + t * P:N + (t + 1) * P], ks[b][:, h, t * D:(t + 1) * D], ident[:])
+            st[("tq", n)] = tq
+
+        def qt_cp(n):
+            if not ok(n):
+                return
+            b, h = divmod(n, H)
+            tq = st[("tq", n)]
+            qt = qtp.tile([P, N], BF16, name="qt")
+            nc.vector.tensor_copy(out=qt[:], in_=tq[:, 0:N])
+            st[("qt", n)] = qt
+            if h < KVH:
+                kt = ktp.tile([P, PACK, P], BF16, name="kt")
+                nc.vector.tensor_copy(out=kt[:].rearrange("d t p -> d (t p)"), in_=tq[:, N:2 * N])
+                st[("kt", b, h)] = kt
+
+        def v_prep(b):
+            if not 0 <= b < B:
+                return
             vg = kvp.tile([P, KVH, D, PACK], BF16, name="vg", align_bytes=64)
             nc.vector.tensor_copy(out=vg[:], in_=vs[b][:].rearrange("p g (t d) -> p g d t", t=PACK))
             vc = kvp.tile([P, KVH * D], U32, name="vc", align_bytes=64)
@@ -99,94 +123,114 @@ def tile_attend_t_kernel(tc, q, k, v, out):
             )
             st[("kv", b)] = (vc, vsc)
 
-        def stage_a(n):
+        def qk(n, u):
+            if not ok(n):
+                return
             b, h = divmod(n, H)
-            if h < KVH:
-                prep_k(b, h)
-            tq = ps.tile([P, 2 * N], BF16, tag="t", bufs=3, name="tq")
-            for a in range(NT):
-                nc.tensor.transpose(tq[:, a * P:(a + 1) * P], qs[b][:, h * NT + a, :], ident[:])
-            qt = qtp.tile([P, N], BF16, name="qt")
-            nc.vector.tensor_copy(out=qt[:], in_=tq[:, 0:N])
-            st[("qt", n)] = qt
-            if h == 1:
-                prep_v(b)
-
-        def stage_b(n):
-            b, h = divmod(n, H)
-            g = h % KVH
-            kt = st[("kt", b, g)]
+            kt = st[("kt", b, h % KVH)]
             qt = st[("qt", n)]
-            et = es[n % NE]
-            mx = small.tile([P, NT], F32, name="mx")
-            nb = small.tile([P, NT], F32, name="nb")
-            rs = small.tile([P, NT], F32, name="rs")
-            c0 = 0
-            for unit in UNITS:
-                s = ps.tile([P, N], F32, tag="s", bufs=4, name="s")
-                regs = []
-                off = 0
-                for a in unit:
-                    w = 32 * (a + 1)
-                    flat = s[:, off:off + PACK * w]
-                    reg = flat.rearrange("i (t p) -> i t p", t=PACK)
-                    nc.tensor.matmul(out=reg, lhsT=qt[:, a * P:(a + 1) * P], rhs=kt[:, :, 0:w],
-                                     start=True, stop=False)
-                    nc.tensor.matmul(out=reg[:, :, 32 * a:32 * a + 32], lhsT=ident[:], rhs=maskb[:],
-                                     start=False, stop=True)
-                    regs.append((a, w, flat, reg))
-                    off += PACK * w
-                for i, (a, w, flat, reg) in enumerate(regs):
-                    nc.vector.tensor_reduce(out=mx[:, c0 + i:c0 + i + 1], in_=flat,
-                                            axis=mybir.AxisListType.X, op=ALU.max)
-                c1 = c0 + len(regs)
-                nc.vector.tensor_scalar(out=nb[:, c0:c1], in0=mx[:, c0:c1], scalar1=-SCALE, scalar2=None,
-                                        op0=ALU.mult)
-                for i, (a, w, flat, reg) in enumerate(regs):
-                    nc.scalar.activation(out=et[:, a, :, 0:w], in_=reg, func=ACT.Exp,
-                                         bias=nb[:, c0 + i:c0 + i + 1], scale=SCALE,
-                                         accum_out=rs[:, a:a + 1])
-                c0 = c1
-            st[("rs", n)] = rs
+            if u == 0:
+                mx = small.tile([P, NT], F32, name="mx")
+                nb = small.tile([P, NT], F32, name="nb")
+                rs = small.tile([P, NT], F32, name="rs")
+                st[("sm", n)] = (mx, nb, rs)
+            s = ps.tile([P, N], F32, tag="s%d" % ((3 * n + u) % 4), name="s")
+            regs = []
+            off = 0
+            for a in UNITS[u]:
+                w = 32 * (a + 1)
+                flat = s[:, off:off + PACK * w]
+                reg = flat.rearrange("i (t p) -> i t p", t=PACK)
+                nc.tensor.matmul(out=reg, lhsT=qt[:, a * P:(a + 1) * P], rhs=kt[:, :, 0:w],
+                                 start=True, stop=False)
+                nc.tensor.matmul(out=reg[:, :, 32 * a:32 * a + 32], lhsT=ident[:], rhs=maskb[:],
+                                 start=False, stop=True)
+                regs.append((a, w, flat, reg))
+                off += PACK * w
+            st[("s", n, u)] = regs
 
-        def stage_c(n):
-            et = es[n % NE]
-            lst = []
-            for j in range(2):
-                xt = ps.tile([P, 2, PACK, P], BF16, tag="t", bufs=3, name="xt")
-                for sl in range(2):
-                    a = ORD[2 * j + sl]
-                    for t in range(PACK):
-                        nc.tensor.transpose(xt[:, sl, t, :], et[:, a, t, :], ident[:])
-                gr = gp.tile([P, 2, P, PACK], BF16, name="gr", align_bytes=64)
-                if (2 * n + j) % VEC_EVERY == VEC_EVERY - 3:
-                    nc.vector.tensor_copy(out=gr[:], in_=xt[:].rearrange("p s t i -> p s i t"))
-                else:
-                    nc.scalar.copy(out=gr[:], in_=xt[:].rearrange("p s t i -> p s i t"))
-                ec = cp.tile([P, 2 * P], U32, name="ec", align_bytes=64)
-                esc = cp.tile([P, 2 * P], U8, name="esc", align_bytes=64)
-                nc.vector.quantize_mx(out=ec[:].bitcast(FP8X4), scales=esc[:],
-                                      in_=gr[:].rearrange("p s i t -> p (s i t)"))
-                lst.append((ec, esc))
-            st[("ec", n)] = lst
+        def mxr(n, u):
+            if not ok(n):
+                return
+            mx, nb, rs = st[("sm", n)]
+            regs = st[("s", n, u)]
+            c0 = UCOL[u]
+            for i, (a, w, flat, reg) in enumerate(regs):
+                nc.vector.tensor_reduce(out=mx[:, c0 + i:c0 + i + 1], in_=flat,
+                                        axis=mybir.AxisListType.X, op=ALU.max)
+            c1 = c0 + len(regs)
+            nc.vector.tensor_scalar(out=nb[:, c0:c1], in0=mx[:, c0:c1], scalar1=-SCALE, scalar2=None,
+                                    op0=ALU.mult)
 
-        def stage_d(n):
+        def ex(n, u):
+            if not ok(n):
+                return
+            mx, nb, rs = st[("sm", n)]
+            et = es[n % NE]
+            c0 = UCOL[u]
+            for i, (a, w, flat, reg) in enumerate(st[("s", n, u)]):
+                nc.scalar.activation(out=et[:, a, :, 0:w], in_=reg, func=ACT.Exp,
+                                     bias=nb[:, c0 + i:c0 + i + 1], scale=SCALE,
+                                     accum_out=rs[:, a:a + 1])
+
+        def tr(n, j):
+            if not ok(n):
+                return
+            et = es[n % NE]
+            xt = ps.tile([P, 2, PACK, P], BF16, tag="xt%d" % j, name="xt")
+            for sl in range(2):
+                a = BANKS[j][sl]
+                for t in range(PACK):
+                    nc.tensor.transpose(xt[:, sl, t, :], et[:, a, t, :], ident[:])
+            st[("xt", n, j)] = xt
+
+        def cpo(n, j):
+            if not ok(n):
+                return
+            xt = st[("xt", n, j)]
+            gr = gp.tile([P, 2, P, PACK], BF16, name="gr", tag="gr%d_%d" % (j, n % 2), align_bytes=64)
+            if False:
+                nc.vector.tensor_copy(out=gr[:], in_=xt[:].rearrange("p s t i -> p s i t"))
+            else:
+                nc.scalar.copy(out=gr[:], in_=xt[:].rearrange("p s t i -> p s i t"))
+            st[("gr", n, j)] = gr
+
+        def qz(n, j):
+            if not ok(n):
+                return
+            gr = st[("gr", n, j)]
+            ec = cp.tile([P, 2 * P], U32, name="ec", align_bytes=64)
+            esc = cp.tile([P, 2 * P], U8, name="esc", align_bytes=64)
+            nc.vector.quantize_mx(out=ec[:].bitcast(FP8X4), scales=esc[:],
+                                  in_=gr[:].rearrange("p s i t -> p (s i t)"))
+            st[("ec", n, j)] = (ec, esc)
+
+        def pv(n):
+            if not ok(n):
+                return
             b, h = divmod(n, H)
             g = h % KVH
             vc, vsc = st[("kv", b)]
-            lst = st[("ec", n)]
-            rs = st[("rs", n)]
-            o = ps.tile([P, NT, D], F32, tag="o", bufs=1, name="o")
-            for c in range(NT):
-                a = ORD[c]
-                ec, esc = lst[c // 2]
-                cols = slice((c % 2) * P, (c % 2) * P + P)
-                nc.tensor.matmul_mx(
-                    out=o[:, a, :],
-                    lhsT=ec[:, cols].bitcast(FP8X4), lhsT_scale=esc[:, cols],
-                    rhs=vc[:, g * D:(g + 1) * D].bitcast(FP8X4), rhs_scale=vsc[:, g * D:(g + 1) * D],
-                    start=True, stop=True,
-                )
+            o = ps.tile([P, NT, D], F32, tag="o", name="o")
+            for j in range(2):
+                ec, esc = st[("ec", n, j)]
+                for sl in range(2):
+                    a = BANKS[j][sl]
+                    cols = slice(sl * P, sl * P + P)
+                    nc.tensor.matmul_mx(
+                        out=o[:, a, :],
+                        lhsT=ec[:, cols].bitcast(FP8X4), lhsT_scale=esc[:, cols],
+                        rhs=vc[:, g * D:(g + 1) * D].bitcast(FP8X4), rhs_scale=vsc[:, g * D:(g + 1) * D],
+                        start=True, stop=True,
+                    )
+            st[("o", n)] = o
+
+        def nrm(n):
+            if not ok(n):
+                return
+            b, h = divmod(n, H)
+            o = st[("o", n)]
+            rs = st[("sm", n)][2]
             rinv = small.tile([P, NT], F32, name="rinv")
             nc.vector.reciprocal(out=rinv[:], in_=rs[:])
             ob = obp.tile([P, NT, D], F32, name="ob")
@@ -194,13 +238,25 @@ def tile_attend_t_kernel(tc, q, k, v, out):
                                     op=ALU.mult)
             nc.sync.dma_start(out=out[b, h].rearrange("(a p) d -> p a d", p=P), in_=ob[:])
 
-        nh = B * H
-        for it in range(nh + 3):
-            if it < nh:
-                stage_a(it)
-            if 0 <= it - 1 < nh:
-                stage_b(it - 1)
-            if 0 <= it - 2 < nh:
-                stage_c(it - 2)
-            if 0 <= it - 3 < nh:
-                stage_d(it - 3)
+        for kk in range(-3, NH + 3):
+            ex(kk, 2)
+            nrm(kk - 3)
+            qz(kk - 2, 1)
+            mxr(kk + 1, 0)
+            qt_cp(kk + 2)
+            if (kk + 2) % H == 2:
+                v_prep((kk + 2) // H)
+            cpo(kk - 1, 1)
+            pv(kk - 2)
+            mxr(kk + 1, 1)
+            tr(kk, 0)
+            qz(kk - 1, 0)
+            ex(kk + 1, 0)
+            ex(kk + 1, 1)
+            qk(kk + 2, 0)
+            qt_tr(kk + 3)
+            tr(kk, 1)
+            cpo(kk, 0)
+            mxr(kk + 1, 2)
+            qk(kk + 2, 1)
+            qk(kk + 2, 2)

@@ -6,11 +6,13 @@ from concourse.masks import make_identity
 
 BF16 = mybir.dt.bfloat16
 F32 = mybir.dt.float32
+I32 = mybir.dt.int32
 U32 = mybir.dt.uint32
 U8 = mybir.dt.uint8
 FP8X4 = mybir.dt.float8_e4m3fn_x4
 ALU = mybir.AluOpType
 ACT = mybir.ActivationFunctionType
+AX = mybir.AxisListType
 
 B, H, KVH, N, D = 8, 4, 2, 512, 128
 P = 128
@@ -19,48 +21,47 @@ PACK = 4
 SCALE = 1.0 / math.sqrt(D)
 NEG = -1.0e30
 FLOPS = 4 * B * H * N * N * D
-NH = B * H
+NP = B * KVH
+NV = 4
 
-UNITS = [[2, 0], [1], [3]]
-UCOL = [0, 2, 3]
-BANKS = [[2, 0], [1, 3]]
-NE = 3
+UNITS = [[(0, 2), (0, 0)], [(1, 2), (1, 0)], [(0, 1), (1, 1)], [(0, 3)], [(1, 3)]]
+DEST = {(0, 2): (0, 0), (0, 0): (0, 96), (1, 2): (1, 0), (1, 0): (1, 96),
+        (0, 1): (2, 0), (1, 1): (2, 64), (0, 3): (3, 0), (1, 3): (4, 0)}
+RCOL = {(0, 0): 0, (0, 2): 1, (1, 0): 2, (1, 2): 3, (0, 1): 4, (1, 1): 5, (0, 3): 6, (1, 3): 7}
+BANKS = [[0, 1], [2, 3], [4]]
 
 
 def tile_attend_t_kernel(tc, q, k, v, out):
     nc = tc.nc
     with ExitStack() as ctx:
-        ctx.enter_context(tc.manual_schedule())
         const = ctx.enter_context(tc.tile_pool(name="const", bufs=1))
-        res = ctx.enter_context(tc.tile_pool(name="res", bufs=1))
-        qtp = ctx.enter_context(tc.tile_pool(name="qtp", bufs=5))
-        ktp = ctx.enter_context(tc.tile_pool(name="ktp", bufs=4))
-        kvp = ctx.enter_context(tc.tile_pool(name="kvp", bufs=2))
-        gp = ctx.enter_context(tc.tile_pool(name="gp", bufs=1))
-        cp = ctx.enter_context(tc.tile_pool(name="cp", bufs=6))
-        small = ctx.enter_context(tc.tile_pool(name="small", bufs=9))
+        ld = ctx.enter_context(tc.tile_pool(name="ld", bufs=3))
+        qtp = ctx.enter_context(tc.tile_pool(name="qtp", bufs=3))
+        vgp = ctx.enter_context(tc.tile_pool(name="vgp", bufs=2))
+        ep = ctx.enter_context(tc.tile_pool(name="ep", bufs=3))
+        gp = ctx.enter_context(tc.tile_pool(name="gp", bufs=2))
+        cp = ctx.enter_context(tc.tile_pool(name="cp", bufs=3))
+        small = ctx.enter_context(tc.tile_pool(name="small", bufs=5))
         obp = ctx.enter_context(tc.tile_pool(name="obp", bufs=4))
         ps = ctx.enter_context(tc.psum_pool(name="ps", bufs=1))
 
-        qs, ks, vs = [], [], []
-        for b in range(B):
-            kb = res.tile([P, KVH, N], BF16, name="ks%d" % b)
-            qb = res.tile([P, H * NT, D], BF16, name="qs%d" % b)
-            vb = res.tile([P, KVH, N], BF16, name="vs%d" % b)
+        st = {}
+
+        def load(b):
+            if b >= B:
+                return
+            eng = nc.sync if b == 0 else nc.gpsimd
+            kb = ld.tile([P, KVH, N], BF16, name="kb")
+            qb = ld.tile([P, H * NT, D], BF16, name="qb")
+            vb = ld.tile([P, KVH, N], BF16, name="vb")
             kview = k[b].rearrange("g (p t) d -> p g (t d)", t=PACK)
             qview = q[b].rearrange("h (a p) d -> p (h a) d", p=P)
-            if b == 0:
-                nc.sync.dma_start(out=kb[:, 0:1, :], in_=kview[:, 0:1, :])
-                nc.sync.dma_start(out=qb[:, 0:NT, :], in_=qview[:, 0:NT, :])
-                nc.sync.dma_start(out=kb[:, 1:2, :], in_=kview[:, 1:2, :])
-                nc.sync.dma_start(out=qb[:, NT:H * NT, :], in_=qview[:, NT:H * NT, :])
-            else:
-                nc.sync.dma_start(out=kb[:], in_=kview)
-                nc.sync.dma_start(out=qb[:], in_=qview)
-            nc.sync.dma_start(out=vb[:], in_=v[b].rearrange("g (p t) d -> p g (t d)", t=PACK))
-            ks.append(kb)
-            qs.append(qb)
-            vs.append(vb)
+            eng.dma_start(out=kb[:], in_=kview)
+            eng.dma_start(out=qb[:], in_=qview)
+            eng.dma_start(out=vb[:], in_=v[b].rearrange("g (p t) d -> p g (t d)", t=PACK))
+            st[("ld", b)] = (kb, qb, vb)
+
+        load(0)
 
         ident = const.tile([P, P], BF16, name="ident")
         make_identity(nc, ident[:])
@@ -72,191 +73,147 @@ def tile_attend_t_kernel(tc, q, k, v, out):
         )
         maskb = const.tile([P, PACK, 32], BF16, name="maskb")
         nc.vector.tensor_copy(out=maskb[:], in_=m32[:].rearrange("i (p t) -> i t p", t=PACK))
-        es = []
-        for j in range(NE):
-            et = const.tile([P, NT, PACK, P], BF16, name="e%d" % j)
-            if j == 0:
-                nc.vector.memset(et[:, 0:NT - 1], 0.0)
-            else:
-                nc.gpsimd.memset(et[:, 0:NT - 1], 0.0)
-            es.append(et)
+        load(1)
 
-        st = {}
+        vsets = []
+        for j in range(NV):
+            vc = const.tile([P, D], U32, name="vc%d" % j, align_bytes=64)
+            vsc = const.tile([P, D], U8, name="vsc%d" % j, align_bytes=64)
+            r20c = const.tile([P, 2 * D], U32, name="r20c%d" % j, align_bytes=64)
+            r20s = const.tile([P, 2 * D], U8, name="r20s%d" % j, align_bytes=64)
+            r11c = const.tile([P, 2 * D], U32, name="r11c%d" % j, align_bytes=64)
+            r11s = const.tile([P, 2 * D], U8, name="r11s%d" % j, align_bytes=64)
+            for t in (vsc, r20c, r20s, r11c, r11s):
+                nc.vector.memset(t[:].bitcast(I32), 0)
+            vsets.append((vc, vsc, r20c, r20s, r11c, r11s))
 
-        def ok(n):
-            return 0 <= n < NH
+        def move(dst, src):
+            nc.sync.dma_start(out=dst.bitcast(I32), in_=src.bitcast(I32))
 
-        def qt_tr(n):
-            if not ok(n):
-                return
-            b, h = divmod(n, H)
-            tq = ps.tile([P, 2 * N], BF16, tag="tq", name="tq")
-            for a in range(NT):
-                nc.tensor.transpose(tq[:, a * P:(a + 1) * P], qs[b][:, h * NT + a, :], ident[:])
-            if h < KVH:
-                for t in range(PACK):
-                    nc.tensor.transpose(tq[:, N + t * P:N + (t + 1) * P], ks[b][:, h, t * D:(t + 1) * D], ident[:])
-            st[("tq", n)] = tq
+        def stage_a(pi):
+            b, g = divmod(pi, KVH)
+            if g == 0:
+                load(b + 2)
+            kb, qb, vb = st[("ld", b)]
+            tk = ps.tile([P, 2 * N], BF16, tag="t", bufs=3, name="tk")
+            for t in range(PACK):
+                nc.tensor.transpose(tk[:, t * P:(t + 1) * P], kb[:, g, t * D:(t + 1) * D], ident[:])
+            kt = qtp.tile([P, PACK, P], BF16, name="kt")
+            nc.vector.tensor_copy(out=kt[:].rearrange("d t p -> d (t p)"), in_=tk[:, 0:N])
+            tq = ps.tile([P, 2 * N], BF16, tag="t", bufs=3, name="tq")
+            for x in range(2):
+                for a in range(NT):
+                    j = x * NT + a
+                    nc.tensor.transpose(tq[:, j * P:(j + 1) * P], qb[:, (g + KVH * x) * NT + a, :], ident[:])
+            qt = qtp.tile([P, 2, NT, P], BF16, name="qt")
+            nc.vector.tensor_copy(out=qt[:].rearrange("d x a i -> d (x a i)"), in_=tq[:])
+            st[("qk", pi)] = (qt, kt)
+            vc, vsc, r20c, r20s, r11c, r11s = vsets[pi % NV]
+            vg = vgp.tile([P, D, PACK], BF16, name="vg", align_bytes=64)
+            nc.vector.tensor_copy(out=vg[:], in_=vb[:, g, :].rearrange("p (t d) -> p d t", t=PACK))
+            nc.vector.quantize_mx(out=vc[:].bitcast(FP8X4), scales=vsc[:], in_=vg[:].rearrange("p d t -> p (d t)"))
+            for cod, r20, r11 in ((vc, r20c, r11c), (vsc, r20s, r11s)):
+                move(r20[96:128, 0:D], cod[0:32, :])
+                move(r20[0:96, D:2 * D], cod[0:96, :])
+                move(r11[0:64, 0:D], cod[0:64, :])
+                move(r11[64:128, D:2 * D], cod[0:64, :])
 
-        def qt_cp(n):
-            if not ok(n):
-                return
-            b, h = divmod(n, H)
-            tq = st[("tq", n)]
-            qt = qtp.tile([P, N], BF16, name="qt")
-            nc.vector.tensor_copy(out=qt[:], in_=tq[:, 0:N])
-            st[("qt", n)] = qt
-            if h < KVH:
-                kt = ktp.tile([P, PACK, P], BF16, name="kt")
-                nc.vector.tensor_copy(out=kt[:].rearrange("d t p -> d (t p)"), in_=tq[:, N:2 * N])
-                st[("kt", b, h)] = kt
+        def stage_b(pi):
+            qt, kt = st[("qk", pi)]
+            mx = small.tile([P, 8], F32, name="mx")
+            nb = small.tile([P, 8], F32, name="nb")
+            rs = small.tile([P, 8], F32, name="rs")
+            ets = []
+            for j in range(5):
+                ets.append(ep.tile([P, PACK, P], BF16, name="et%d" % j))
+            c0 = 0
+            for unit in UNITS:
+                s = ps.tile([P, N], F32, tag="s", bufs=4, name="s")
+                regs = []
+                off = 0
+                for (x, a) in unit:
+                    w = 32 * (a + 1)
+                    flat = s[:, off:off + PACK * w]
+                    reg = flat.rearrange("i (t p) -> i t p", t=PACK)
+                    nc.tensor.matmul(out=reg, lhsT=qt[:, x, a, :], rhs=kt[:, :, 0:w], start=True, stop=False)
+                    nc.tensor.matmul(out=reg[:, :, 32 * a:32 * a + 32], lhsT=ident[:], rhs=maskb[:],
+                                     start=False, stop=True)
+                    regs.append((x, a, w, flat, reg))
+                    off += PACK * w
+                c1 = c0 + len(regs)
+                if len(regs) == 2 and regs[0][2] == regs[1][2]:
+                    nc.vector.tensor_reduce(out=mx[:, c0:c1], in_=s[:].rearrange("i (x c) -> i x c", x=2),
+                                            axis=AX.X, op=ALU.max)
+                else:
+                    for i, (x, a, w, flat, reg) in enumerate(regs):
+                        nc.vector.tensor_reduce(out=mx[:, c0 + i:c0 + i + 1], in_=flat, axis=AX.X, op=ALU.max)
+                nc.vector.tensor_scalar(out=nb[:, c0:c1], in0=mx[:, c0:c1], scalar1=-SCALE, scalar2=None,
+                                        op0=ALU.mult)
+                for i, (x, a, w, flat, reg) in enumerate(regs):
+                    j, col = DEST[(x, a)]
+                    r = RCOL[(x, a)]
+                    nc.scalar.activation(out=ets[j][:, :, col:col + w], in_=reg, func=ACT.Exp,
+                                         bias=nb[:, c0 + i:c0 + i + 1], scale=SCALE, accum_out=rs[:, r:r + 1])
+                c0 = c1
+            st[("e", pi)] = (ets, rs)
 
-        def v_prep(b):
-            if not 0 <= b < B:
-                return
-            vg = kvp.tile([P, KVH, D, PACK], BF16, name="vg", align_bytes=64)
-            nc.vector.tensor_copy(out=vg[:], in_=vs[b][:].rearrange("p g (t d) -> p g d t", t=PACK))
-            vc = kvp.tile([P, KVH * D], U32, name="vc", align_bytes=64)
-            vsc = kvp.tile([P, KVH * D], U8, name="vsc", align_bytes=64)
-            nc.vector.quantize_mx(
-                out=vc[:].bitcast(FP8X4), scales=vsc[:], in_=vg[:].rearrange("p g d t -> p (g d t)")
-            )
-            st[("kv", b)] = (vc, vsc)
+        def stage_c(pi):
+            ets = st[("e", pi)][0]
+            codes = {}
+            for bi, bank in enumerate(BANKS):
+                nb_t = len(bank)
+                xt = ps.tile([P, 2, PACK, P], BF16, tag="t", bufs=3, name="xt")
+                for sl, j in enumerate(bank):
+                    for t in range(PACK):
+                        nc.tensor.transpose(xt[:, sl, t, :], ets[j][:, t, :], ident[:])
+                gr = gp.tile([P, 2, P, PACK], BF16, name="gr%d" % bi, align_bytes=64)
+                nc.scalar.copy(out=gr[:, 0:nb_t], in_=xt[:, 0:nb_t].rearrange("p s t i -> p s i t"))
+                ec = cp.tile([P, 2 * P], U32, name="ec%d" % bi, align_bytes=64)
+                esc = cp.tile([P, 2 * P], U8, name="esc%d" % bi, align_bytes=64)
+                nc.vector.quantize_mx(out=ec[:, 0:nb_t * P].bitcast(FP8X4), scales=esc[:, 0:nb_t * P],
+                                      in_=gr[:, 0:nb_t].rearrange("p s i t -> p (s i t)"))
+                for sl, j in enumerate(bank):
+                    codes[j] = (ec[:, sl * P:(sl + 1) * P], esc[:, sl * P:(sl + 1) * P])
+            st[("c", pi)] = codes
 
-        def qk(n, u):
-            if not ok(n):
-                return
-            b, h = divmod(n, H)
-            kt = st[("kt", b, h % KVH)]
-            qt = st[("qt", n)]
-            if u == 0:
-                mx = small.tile([P, NT], F32, name="mx")
-                nb = small.tile([P, NT], F32, name="nb")
-                rs = small.tile([P, NT], F32, name="rs")
-                st[("sm", n)] = (mx, nb, rs)
-            s = ps.tile([P, N], F32, tag="s%d" % ((3 * n + u) % 4), name="s")
-            regs = []
-            off = 0
-            for a in UNITS[u]:
-                w = 32 * (a + 1)
-                flat = s[:, off:off + PACK * w]
-                reg = flat.rearrange("i (t p) -> i t p", t=PACK)
-                nc.tensor.matmul(out=reg, lhsT=qt[:, a * P:(a + 1) * P], rhs=kt[:, :, 0:w],
-                                 start=True, stop=False)
-                nc.tensor.matmul(out=reg[:, :, 32 * a:32 * a + 32], lhsT=ident[:], rhs=maskb[:],
-                                 start=False, stop=True)
-                regs.append((a, w, flat, reg))
-                off += PACK * w
-            st[("s", n, u)] = regs
-
-        def mxr(n, u):
-            if not ok(n):
-                return
-            mx, nb, rs = st[("sm", n)]
-            regs = st[("s", n, u)]
-            c0 = UCOL[u]
-            for i, (a, w, flat, reg) in enumerate(regs):
-                nc.vector.tensor_reduce(out=mx[:, c0 + i:c0 + i + 1], in_=flat,
-                                        axis=mybir.AxisListType.X, op=ALU.max)
-            c1 = c0 + len(regs)
-            nc.vector.tensor_scalar(out=nb[:, c0:c1], in0=mx[:, c0:c1], scalar1=-SCALE, scalar2=None,
-                                    op0=ALU.mult)
-
-        def ex(n, u):
-            if not ok(n):
-                return
-            mx, nb, rs = st[("sm", n)]
-            et = es[n % NE]
-            c0 = UCOL[u]
-            for i, (a, w, flat, reg) in enumerate(st[("s", n, u)]):
-                nc.scalar.activation(out=et[:, a, :, 0:w], in_=reg, func=ACT.Exp,
-                                     bias=nb[:, c0 + i:c0 + i + 1], scale=SCALE,
-                                     accum_out=rs[:, a:a + 1])
-
-        def tr(n, j):
-            if not ok(n):
-                return
-            et = es[n % NE]
-            xt = ps.tile([P, 2, PACK, P], BF16, tag="xt%d" % j, name="xt")
-            for sl in range(2):
-                a = BANKS[j][sl]
-                for t in range(PACK):
-                    nc.tensor.transpose(xt[:, sl, t, :], et[:, a, t, :], ident[:])
-            st[("xt", n, j)] = xt
-
-        def cpo(n, j):
-            if not ok(n):
-                return
-            xt = st[("xt", n, j)]
-            gr = gp.tile([P, 2, P, PACK], BF16, name="gr", tag="gr%d_%d" % (j, n % 2), align_bytes=64)
-            if False:
-                nc.vector.tensor_copy(out=gr[:], in_=xt[:].rearrange("p s t i -> p s i t"))
-            else:
-                nc.scalar.copy(out=gr[:], in_=xt[:].rearrange("p s t i -> p s i t"))
-            st[("gr", n, j)] = gr
-
-        def qz(n, j):
-            if not ok(n):
-                return
-            gr = st[("gr", n, j)]
-            ec = cp.tile([P, 2 * P], U32, name="ec", align_bytes=64)
-            esc = cp.tile([P, 2 * P], U8, name="esc", align_bytes=64)
-            nc.vector.quantize_mx(out=ec[:].bitcast(FP8X4), scales=esc[:],
-                                  in_=gr[:].rearrange("p s i t -> p (s i t)"))
-            st[("ec", n, j)] = (ec, esc)
-
-        def pv(n):
-            if not ok(n):
-                return
-            b, h = divmod(n, H)
-            g = h % KVH
-            vc, vsc = st[("kv", b)]
-            o = ps.tile([P, NT, D], F32, tag="o", name="o")
-            for j in range(2):
-                ec, esc = st[("ec", n, j)]
-                for sl in range(2):
-                    a = BANKS[j][sl]
-                    cols = slice(sl * P, sl * P + P)
+        def stage_d(pi):
+            b, g = divmod(pi, KVH)
+            vc, vsc, r20c, r20s, r11c, r11s = vsets[pi % NV]
+            codes = st[("c", pi)]
+            rs = st[("e", pi)][1]
+            rinv = small.tile([P, 8], F32, name="rinv")
+            nc.vector.reciprocal(out=rinv[:], in_=rs[:])
+            plan = [
+                [(0, 0, r20c, r20s, 2 * D), (1, 2 * D, r20c, r20s, 2 * D)],
+                [(2, 0, r11c, r11s, 2 * D), (3, 2 * D, vc, vsc, D), (4, 3 * D, vc, vsc, D)],
+            ]
+            for half in range(2):
+                o = ps.tile([P, NT, D], F32, tag="o", bufs=1, name="o")
+                oflat = o[:].rearrange("i a d -> i (a d)")
+                for (j, col, rc, rsc, width) in plan[half]:
                     nc.tensor.matmul_mx(
-                        out=o[:, a, :],
-                        lhsT=ec[:, cols].bitcast(FP8X4), lhsT_scale=esc[:, cols],
-                        rhs=vc[:, g * D:(g + 1) * D].bitcast(FP8X4), rhs_scale=vsc[:, g * D:(g + 1) * D],
+                        out=oflat[:, col:col + width],
+                        lhsT=codes[j][0].bitcast(FP8X4), lhsT_scale=codes[j][1],
+                        rhs=rc[:, 0:width].bitcast(FP8X4), rhs_scale=rsc[:, 0:width],
                         start=True, stop=True,
                     )
-            st[("o", n)] = o
+                ob = obp.tile([P, NT, D], F32, name="ob")
+                nc.vector.tensor_tensor(
+                    out=ob[:], in0=o[:],
+                    in1=rinv[:, half * NT:(half + 1) * NT].unsqueeze(2).to_broadcast([P, NT, D]), op=ALU.mult)
+                for x in range(2):
+                    dst = out[b, g + KVH * x].rearrange("(a p) d -> p a d", p=P)
+                    if half == 0:
+                        nc.sync.dma_start(out=dst[:, 0:NT:2, :], in_=ob[:, 2 * x:2 * x + 2, :])
+                    else:
+                        nc.sync.dma_start(out=dst[:, 1:NT:2, :], in_=ob[:, x:NT:2, :])
 
-        def nrm(n):
-            if not ok(n):
-                return
-            b, h = divmod(n, H)
-            o = st[("o", n)]
-            rs = st[("sm", n)][2]
-            rinv = small.tile([P, NT], F32, name="rinv")
-            nc.vector.reciprocal(out=rinv[:], in_=rs[:])
-            ob = obp.tile([P, NT, D], F32, name="ob")
-            nc.vector.tensor_tensor(out=ob[:], in0=o[:], in1=rinv[:].unsqueeze(2).to_broadcast([P, NT, D]),
-                                    op=ALU.mult)
-            nc.sync.dma_start(out=out[b, h].rearrange("(a p) d -> p a d", p=P), in_=ob[:])
-
-        for kk in range(-3, NH + 3):
-            ex(kk, 2)
-            nrm(kk - 3)
-            qz(kk - 2, 1)
-            mxr(kk + 1, 0)
-            qt_cp(kk + 2)
-            if (kk + 2) % H == 2:
-                v_prep((kk + 2) // H)
-            cpo(kk - 1, 1)
-            pv(kk - 2)
-            mxr(kk + 1, 1)
-            tr(kk, 0)
-            qz(kk - 1, 0)
-            ex(kk + 1, 0)
-            ex(kk + 1, 1)
-            qk(kk + 2, 0)
-            qt_tr(kk + 3)
-            tr(kk, 1)
-            cpo(kk, 0)
-            mxr(kk + 1, 2)
-            qk(kk + 2, 1)
-            qk(kk + 2, 2)
+        for it in range(NP + 3):
+            if it < NP:
+                stage_a(it)
+            if 0 <= it - 1 < NP:
+                stage_b(it - 1)
+            if 0 <= it - 2 < NP:
+                stage_c(it - 2)
+            if 0 <= it - 3 < NP:
+                stage_d(it - 3)

@@ -25,8 +25,8 @@ NP = B * KVH
 NV = 4
 
 UNITS = [[(0, 2), (0, 0)], [(1, 2), (1, 0)], [(0, 1), (1, 1)], [(0, 3)], [(1, 3)]]
-DEST = {(0, 2): (0, 0), (0, 0): (0, 96), (1, 2): (1, 0), (1, 0): (1, 96),
-        (0, 1): (2, 0), (1, 1): (2, 64), (0, 3): (3, 0), (1, 3): (4, 0)}
+UCOL = [0, 2, 4, 6, 7]
+ECOL = {(0, 2): 0, (0, 0): 96, (1, 2): 0, (1, 0): 96, (0, 1): 0, (1, 1): 64, (0, 3): 0, (1, 3): 0}
 RCOL = {(0, 0): 0, (0, 2): 1, (1, 0): 2, (1, 2): 3, (0, 1): 4, (1, 1): 5, (0, 3): 6, (1, 3): 7}
 BANKS = [[0, 1], [2, 3], [4]]
 
@@ -34,34 +34,34 @@ BANKS = [[0, 1], [2, 3], [4]]
 def tile_attend_t_kernel(tc, q, k, v, out):
     nc = tc.nc
     with ExitStack() as ctx:
+        ctx.enter_context(tc.manual_schedule())
         const = ctx.enter_context(tc.tile_pool(name="const", bufs=1))
-        ld = ctx.enter_context(tc.tile_pool(name="ld", bufs=3))
         qtp = ctx.enter_context(tc.tile_pool(name="qtp", bufs=3))
         vgp = ctx.enter_context(tc.tile_pool(name="vgp", bufs=2))
         ep = ctx.enter_context(tc.tile_pool(name="ep", bufs=3))
         gp = ctx.enter_context(tc.tile_pool(name="gp", bufs=2))
-        cp = ctx.enter_context(tc.tile_pool(name="cp", bufs=3))
-        small = ctx.enter_context(tc.tile_pool(name="small", bufs=5))
+        cpl = ctx.enter_context(tc.tile_pool(name="cpl", bufs=3))
+        small = ctx.enter_context(tc.tile_pool(name="small", bufs=6))
         obp = ctx.enter_context(tc.tile_pool(name="obp", bufs=4))
         ps = ctx.enter_context(tc.psum_pool(name="ps", bufs=1))
 
         st = {}
 
-        def load(b):
-            if b >= B:
-                return
-            eng = nc.sync if b == 0 else nc.gpsimd
-            kb = ld.tile([P, KVH, N], BF16, name="kb")
-            qb = ld.tile([P, H * NT, D], BF16, name="qb")
-            vb = ld.tile([P, KVH, N], BF16, name="vb")
-            kview = k[b].rearrange("g (p t) d -> p g (t d)", t=PACK)
-            qview = q[b].rearrange("h (a p) d -> p (h a) d", p=P)
-            eng.dma_start(out=kb[:], in_=kview)
-            eng.dma_start(out=qb[:], in_=qview)
-            eng.dma_start(out=vb[:], in_=v[b].rearrange("g (p t) d -> p g (t d)", t=PACK))
-            st[("ld", b)] = (kb, qb, vb)
-
-        load(0)
+        lds = []
+        views = []
+        for b in range(B):
+            kb = const.tile([P, KVH, N], BF16, name="kb%d" % b)
+            qb = const.tile([P, H, NT, D], BF16, name="qb%d" % b)
+            vb = const.tile([P, KVH, N], BF16, name="vb%d" % b)
+            lds.append((kb, qb, vb))
+            views.append((k[b].rearrange("g (p t) d -> p g (t d)", t=PACK),
+                          q[b].rearrange("h (a p) d -> p h a d", p=P),
+                          v[b].rearrange("g (p t) d -> p g (t d)", t=PACK)))
+        for g in range(KVH):
+            nc.sync.dma_start(out=lds[0][0][:, g, :], in_=views[0][0][:, g, :])
+            nc.sync.dma_start(out=lds[0][2][:, g, :], in_=views[0][2][:, g, :])
+            nc.sync.dma_start(out=lds[0][1][:, g], in_=views[0][1][:, g])
+            nc.sync.dma_start(out=lds[0][1][:, g + KVH], in_=views[0][1][:, g + KVH])
 
         ident = const.tile([P, P], BF16, name="ident")
         make_identity(nc, ident[:])
@@ -71,10 +71,6 @@ def tile_attend_t_kernel(tc, q, k, v, out):
             out=m32[:], in_=m32[:], compare_op=ALU.is_ge, fill=NEG, base=0,
             pattern=[[-1, P]], channel_multiplier=1,
         )
-        maskb = const.tile([P, PACK, 32], BF16, name="maskb")
-        nc.vector.tensor_copy(out=maskb[:], in_=m32[:].rearrange("i (p t) -> i t p", t=PACK))
-        load(1)
-
         vsets = []
         for j in range(NV):
             vc = const.tile([P, D], U32, name="vc%d" % j, align_bytes=64)
@@ -87,30 +83,76 @@ def tile_attend_t_kernel(tc, q, k, v, out):
                 nc.vector.memset(t[:].bitcast(I32), 0)
             vsets.append((vc, vsc, r20c, r20s, r11c, r11s))
 
+        maskb = const.tile([P, PACK, 32], BF16, name="maskb")
+        nc.vector.tensor_copy(out=maskb[:], in_=m32[:].rearrange("i (p t) -> i t p", t=PACK))
+
+        for b in range(1, B):
+            nc.gpsimd.dma_start(out=lds[b][2][:], in_=views[b][2])
+            nc.gpsimd.dma_start(out=lds[b][0][:], in_=views[b][0])
+            nc.gpsimd.dma_start(out=lds[b][1][:].rearrange("p h a d -> p (h a) d"),
+                                in_=views[b][1].rearrange("p h a d -> p (h a) d"))
+
+        def ok(n):
+            return 0 <= n < NP
+
         def move(dst, src):
             nc.sync.dma_start(out=dst.bitcast(I32), in_=src.bitcast(I32))
 
-        def stage_a(pi):
-            b, g = divmod(pi, KVH)
-            if g == 0:
-                load(b + 2)
-            kb, qb, vb = st[("ld", b)]
-            tk = ps.tile([P, 2 * N], BF16, tag="t", bufs=3, name="tk")
+        def sm(n):
+            if ("sm", n) not in st:
+                mx = small.tile([P, 8], F32, name="mx")
+                nbt = small.tile([P, 8], F32, name="nbt")
+                rs = small.tile([P, 8], F32, name="rs")
+                st[("sm", n)] = (mx, nbt, rs)
+            return st[("sm", n)]
+
+        def kttr(n):
+            if not ok(n):
+                return
+            b, g = divmod(n, KVH)
+            tk = ps.tile([P, 2 * N], BF16, tag="tq", name="tk")
             for t in range(PACK):
-                nc.tensor.transpose(tk[:, t * P:(t + 1) * P], kb[:, g, t * D:(t + 1) * D], ident[:])
+                nc.tensor.transpose(tk[:, t * P:(t + 1) * P], lds[b][0][:, g, t * D:(t + 1) * D], ident[:])
+            st[("tk", n)] = tk
+
+        def ktcp(n):
+            if not ok(n):
+                return
             kt = qtp.tile([P, PACK, P], BF16, name="kt")
-            nc.vector.tensor_copy(out=kt[:].rearrange("d t p -> d (t p)"), in_=tk[:, 0:N])
-            tq = ps.tile([P, 2 * N], BF16, tag="t", bufs=3, name="tq")
+            nc.vector.tensor_copy(out=kt[:].rearrange("d t p -> d (t p)"), in_=st[("tk", n)][:, 0:N])
+            st[("kt", n)] = kt
+
+        def qttr(n):
+            if not ok(n):
+                return
+            b, g = divmod(n, KVH)
+            tq = ps.tile([P, 2 * N], BF16, tag="tq", name="tq")
             for x in range(2):
                 for a in range(NT):
                     j = x * NT + a
-                    nc.tensor.transpose(tq[:, j * P:(j + 1) * P], qb[:, (g + KVH * x) * NT + a, :], ident[:])
+                    nc.tensor.transpose(tq[:, j * P:(j + 1) * P], lds[b][1][:, g + KVH * x, a, :], ident[:])
+            st[("tq", n)] = tq
+
+        def qtcp(n):
+            if not ok(n):
+                return
             qt = qtp.tile([P, 2, NT, P], BF16, name="qt")
-            nc.vector.tensor_copy(out=qt[:].rearrange("d x a i -> d (x a i)"), in_=tq[:])
-            st[("qk", pi)] = (qt, kt)
-            vc, vsc, r20c, r20s, r11c, r11s = vsets[pi % NV]
+            nc.vector.tensor_copy(out=qt[:].rearrange("d x a i -> d (x a i)"), in_=st[("tq", n)][:])
+            st[("qt", n)] = qt
+
+        def vrg(n):
+            if not ok(n):
+                return
+            b, g = divmod(n, KVH)
             vg = vgp.tile([P, D, PACK], BF16, name="vg", align_bytes=64)
-            nc.vector.tensor_copy(out=vg[:], in_=vb[:, g, :].rearrange("p (t d) -> p d t", t=PACK))
+            nc.vector.tensor_copy(out=vg[:], in_=lds[b][2][:, g, :].rearrange("p (t d) -> p d t", t=PACK))
+            st[("vg", n)] = vg
+
+        def vqz(n):
+            if not ok(n):
+                return
+            vc, vsc, r20c, r20s, r11c, r11s = vsets[n % NV]
+            vg = st[("vg", n)]
             nc.vector.quantize_mx(out=vc[:].bitcast(FP8X4), scales=vsc[:], in_=vg[:].rearrange("p d t -> p (d t)"))
             for cod, r20, r11 in ((vc, r20c, r11c), (vsc, r20s, r11s)):
                 move(r20[96:128, 0:D], cod[0:32, :])
@@ -118,102 +160,171 @@ def tile_attend_t_kernel(tc, q, k, v, out):
                 move(r11[0:64, 0:D], cod[0:64, :])
                 move(r11[64:128, D:2 * D], cod[0:64, :])
 
-        def stage_b(pi):
-            qt, kt = st[("qk", pi)]
-            mx = small.tile([P, 8], F32, name="mx")
-            nb = small.tile([P, 8], F32, name="nb")
-            rs = small.tile([P, 8], F32, name="rs")
-            ets = []
-            for j in range(5):
-                ets.append(ep.tile([P, PACK, P], BF16, name="et%d" % j))
-            c0 = 0
-            for unit in UNITS:
-                s = ps.tile([P, N], F32, tag="s", bufs=4, name="s")
-                regs = []
-                off = 0
-                for (x, a) in unit:
-                    w = 32 * (a + 1)
-                    flat = s[:, off:off + PACK * w]
-                    reg = flat.rearrange("i (t p) -> i t p", t=PACK)
-                    nc.tensor.matmul(out=reg, lhsT=qt[:, x, a, :], rhs=kt[:, :, 0:w], start=True, stop=False)
-                    nc.tensor.matmul(out=reg[:, :, 32 * a:32 * a + 32], lhsT=ident[:], rhs=maskb[:],
-                                     start=False, stop=True)
-                    regs.append((x, a, w, flat, reg))
-                    off += PACK * w
-                c1 = c0 + len(regs)
-                if len(regs) == 2 and regs[0][2] == regs[1][2]:
-                    nc.vector.tensor_reduce(out=mx[:, c0:c1], in_=s[:].rearrange("i (x c) -> i x c", x=2),
-                                            axis=AX.X, op=ALU.max)
-                else:
-                    for i, (x, a, w, flat, reg) in enumerate(regs):
-                        nc.vector.tensor_reduce(out=mx[:, c0 + i:c0 + i + 1], in_=flat, axis=AX.X, op=ALU.max)
-                nc.vector.tensor_scalar(out=nb[:, c0:c1], in0=mx[:, c0:c1], scalar1=-SCALE, scalar2=None,
-                                        op0=ALU.mult)
+        def qk(n, u):
+            if not ok(n):
+                return
+            qt, kt = st[("qt", n)], st[("kt", n)]
+            s = ps.tile([P, N], F32, tag="s%d" % ((5 * n + u) % 4), name="s")
+            regs = []
+            off = 0
+            for (x, a) in UNITS[u]:
+                w = 32 * (a + 1)
+                flat = s[:, off:off + PACK * w]
+                reg = flat.rearrange("i (t p) -> i t p", t=PACK)
+                nc.tensor.matmul(out=reg, lhsT=qt[:, x, a, :], rhs=kt[:, :, 0:w], start=True, stop=False)
+                nc.tensor.matmul(out=reg[:, :, 32 * a:32 * a + 32], lhsT=ident[:], rhs=maskb[:],
+                                 start=False, stop=True)
+                regs.append((x, a, w, flat, reg))
+                off += PACK * w
+            st[("s", n, u)] = (s, regs)
+
+        def red(n, u):
+            if not ok(n):
+                return
+            mx = sm(n)[0]
+            s, regs = st[("s", n, u)]
+            c0 = UCOL[u]
+            if u == 2:
+                nc.vector.tensor_reduce(out=mx[:, c0:c0 + 2], in_=s[:].rearrange("i (x c) -> i x c", x=2),
+                                        axis=AX.X, op=ALU.max)
+            else:
                 for i, (x, a, w, flat, reg) in enumerate(regs):
-                    j, col = DEST[(x, a)]
-                    r = RCOL[(x, a)]
-                    nc.scalar.activation(out=ets[j][:, :, col:col + w], in_=reg, func=ACT.Exp,
-                                         bias=nb[:, c0 + i:c0 + i + 1], scale=SCALE, accum_out=rs[:, r:r + 1])
-                c0 = c1
-            st[("e", pi)] = (ets, rs)
+                    nc.vector.tensor_reduce(out=mx[:, c0 + i:c0 + i + 1], in_=flat, axis=AX.X, op=ALU.max)
 
-        def stage_c(pi):
-            ets = st[("e", pi)][0]
-            codes = {}
-            for bi, bank in enumerate(BANKS):
-                nb_t = len(bank)
-                xt = ps.tile([P, 2, PACK, P], BF16, tag="t", bufs=3, name="xt")
-                for sl, j in enumerate(bank):
-                    for t in range(PACK):
-                        nc.tensor.transpose(xt[:, sl, t, :], ets[j][:, t, :], ident[:])
-                gr = gp.tile([P, 2, P, PACK], BF16, name="gr%d" % bi, align_bytes=64)
-                nc.scalar.copy(out=gr[:, 0:nb_t], in_=xt[:, 0:nb_t].rearrange("p s t i -> p s i t"))
-                ec = cp.tile([P, 2 * P], U32, name="ec%d" % bi, align_bytes=64)
-                esc = cp.tile([P, 2 * P], U8, name="esc%d" % bi, align_bytes=64)
-                nc.vector.quantize_mx(out=ec[:, 0:nb_t * P].bitcast(FP8X4), scales=esc[:, 0:nb_t * P],
-                                      in_=gr[:, 0:nb_t].rearrange("p s i t -> p (s i t)"))
-                for sl, j in enumerate(bank):
-                    codes[j] = (ec[:, sl * P:(sl + 1) * P], esc[:, sl * P:(sl + 1) * P])
-            st[("c", pi)] = codes
+        def nb(n, u):
+            if not ok(n):
+                return
+            mx, nbt, rs = sm(n)
+            c0, c1 = UCOL[u], UCOL[u] + len(UNITS[u])
+            nc.vector.tensor_scalar(out=nbt[:, c0:c1], in0=mx[:, c0:c1], scalar1=-SCALE, scalar2=None,
+                                    op0=ALU.mult)
 
-        def stage_d(pi):
-            b, g = divmod(pi, KVH)
-            vc, vsc, r20c, r20s, r11c, r11s = vsets[pi % NV]
-            codes = st[("c", pi)]
-            rs = st[("e", pi)][1]
-            rinv = small.tile([P, 8], F32, name="rinv")
-            nc.vector.reciprocal(out=rinv[:], in_=rs[:])
+        def ex(n, u):
+            if not ok(n):
+                return
+            mx, nbt, rs = sm(n)
+            et = ep.tile([P, PACK, P], BF16, name="et%d" % u)
+            c0 = UCOL[u]
+            for i, (x, a, w, flat, reg) in enumerate(st[("s", n, u)][1]):
+                col = ECOL[(x, a)]
+                r = RCOL[(x, a)]
+                nc.scalar.activation(out=et[:, :, col:col + w], in_=reg, func=ACT.Exp,
+                                     bias=nbt[:, c0 + i:c0 + i + 1], scale=SCALE, accum_out=rs[:, r:r + 1])
+            st[("et", n, u)] = et
+
+        def tr(n, bi):
+            if not ok(n):
+                return
+            xt = ps.tile([P, 2, PACK, P], BF16, tag="x%d" % ((3 * n + bi) % 2), name="xt")
+            for sl, j in enumerate(BANKS[bi]):
+                et = st[("et", n, j)]
+                for t in range(PACK):
+                    nc.tensor.transpose(xt[:, sl, t, :], et[:, t, :], ident[:])
+            st[("xt", n, bi)] = xt
+
+        def cp(n, bi):
+            if not ok(n):
+                return
+            cnt = len(BANKS[bi])
+            xt = st[("xt", n, bi)]
+            gr = gp.tile([P, 2, P, PACK], BF16, name="gr%d" % bi, align_bytes=64)
+            nc.scalar.copy(out=gr[:, 0:cnt], in_=xt[:, 0:cnt].rearrange("p s t i -> p s i t"))
+            st[("gr", n, bi)] = gr
+
+        def qz(n, bi):
+            if not ok(n):
+                return
+            cnt = len(BANKS[bi])
+            gr = st[("gr", n, bi)]
+            ec = cpl.tile([P, 2 * P], U32, name="ec%d" % bi, align_bytes=64)
+            esc = cpl.tile([P, 2 * P], U8, name="esc%d" % bi, align_bytes=64)
+            nc.vector.quantize_mx(out=ec[:, 0:cnt * P].bitcast(FP8X4), scales=esc[:, 0:cnt * P],
+                                  in_=gr[:, 0:cnt].rearrange("p s i t -> p (s i t)"))
+            for sl, j in enumerate(BANKS[bi]):
+                st[("c", n, j)] = (ec[:, sl * P:(sl + 1) * P], esc[:, sl * P:(sl + 1) * P])
+
+        def pv(n, half):
+            if not ok(n):
+                return
+            vc, vsc, r20c, r20s, r11c, r11s = vsets[n % NV]
             plan = [
                 [(0, 0, r20c, r20s, 2 * D), (1, 2 * D, r20c, r20s, 2 * D)],
                 [(2, 0, r11c, r11s, 2 * D), (3, 2 * D, vc, vsc, D), (4, 3 * D, vc, vsc, D)],
             ]
-            for half in range(2):
-                o = ps.tile([P, NT, D], F32, tag="o", bufs=1, name="o")
-                oflat = o[:].rearrange("i a d -> i (a d)")
-                for (j, col, rc, rsc, width) in plan[half]:
-                    nc.tensor.matmul_mx(
-                        out=oflat[:, col:col + width],
-                        lhsT=codes[j][0].bitcast(FP8X4), lhsT_scale=codes[j][1],
-                        rhs=rc[:, 0:width].bitcast(FP8X4), rhs_scale=rsc[:, 0:width],
-                        start=True, stop=True,
-                    )
-                ob = obp.tile([P, NT, D], F32, name="ob")
-                nc.vector.tensor_tensor(
-                    out=ob[:], in0=o[:],
-                    in1=rinv[:, half * NT:(half + 1) * NT].unsqueeze(2).to_broadcast([P, NT, D]), op=ALU.mult)
-                for x in range(2):
-                    dst = out[b, g + KVH * x].rearrange("(a p) d -> p a d", p=P)
-                    if half == 0:
-                        nc.sync.dma_start(out=dst[:, 0:NT:2, :], in_=ob[:, 2 * x:2 * x + 2, :])
-                    else:
-                        nc.sync.dma_start(out=dst[:, 1:NT:2, :], in_=ob[:, x:NT:2, :])
+            o = ps.tile([P, NT, D], F32, tag="o", name="o")
+            oflat = o[:].rearrange("i a d -> i (a d)")
+            for (j, col, rc_, rsc, width) in plan[half]:
+                cod, sca = st[("c", n, j)]
+                nc.tensor.matmul_mx(
+                    out=oflat[:, col:col + width],
+                    lhsT=cod.bitcast(FP8X4), lhsT_scale=sca,
+                    rhs=rc_[:, 0:width].bitcast(FP8X4), rhs_scale=rsc[:, 0:width],
+                    start=True, stop=True,
+                )
+            st[("o", n, half)] = o
 
-        for it in range(NP + 3):
-            if it < NP:
-                stage_a(it)
-            if 0 <= it - 1 < NP:
-                stage_b(it - 1)
-            if 0 <= it - 2 < NP:
-                stage_c(it - 2)
-            if 0 <= it - 3 < NP:
-                stage_d(it - 3)
+        def rc(n):
+            if not ok(n):
+                return
+            rinv = small.tile([P, 8], F32, name="rinv")
+            nc.vector.reciprocal(out=rinv[:], in_=sm(n)[2][:])
+            st[("rinv", n)] = rinv
+
+        def nm(n, half):
+            if not ok(n):
+                return
+            b, g = divmod(n, KVH)
+            o = st[("o", n, half)]
+            rinv = st[("rinv", n)]
+            ob = obp.tile([P, NT, D], F32, name="ob")
+            nc.vector.tensor_tensor(
+                out=ob[:], in0=o[:],
+                in1=rinv[:, half * NT:(half + 1) * NT].unsqueeze(2).to_broadcast([P, NT, D]), op=ALU.mult)
+            for x in range(2):
+                dst = out[b, g + KVH * x].rearrange("(a p) d -> p a d", p=P)
+                if half == 0:
+                    nc.sync.dma_start(out=dst[:, 0:NT:2, :], in_=ob[:, 2 * x:2 * x + 2, :])
+                else:
+                    nc.sync.dma_start(out=dst[:, 1:NT:2, :], in_=ob[:, x:NT:2, :])
+
+        for kk in range(-2, NP + 2):
+            tr(kk - 1, 1)
+            nm(kk - 2, 1)
+            qk(kk, 2)
+            qttr(kk + 1)
+            nb(kk, 0)
+            ex(kk - 1, 4)
+            tr(kk - 1, 2)
+            cp(kk - 1, 1)
+            vrg(kk + 2)
+            ex(kk, 0)
+            red(kk, 2)
+            nb(kk, 1)
+            rc(kk - 1)
+            qtcp(kk + 1)
+            qk(kk, 3)
+            qz(kk - 1, 0)
+            kttr(kk + 2)
+            nb(kk, 2)
+            qk(kk, 4)
+            red(kk, 3)
+            qz(kk - 1, 1)
+            pv(kk - 1, 0)
+            ktcp(kk + 2)
+            nb(kk, 3)
+            cp(kk - 1, 2)
+            ex(kk, 1)
+            qk(kk + 1, 0)
+            tr(kk, 0)
+            ex(kk, 2)
+            qz(kk - 1, 2)
+            ex(kk, 3)
+            qk(kk + 1, 1)
+            red(kk, 4)
+            cp(kk, 0)
+            nm(kk - 1, 0)
+            vqz(kk + 1)
+            pv(kk - 1, 1)
+            nb(kk, 4)
+            red(kk + 1, 0)
+            red(kk + 1, 1)

@@ -38,6 +38,7 @@ def tile_attend_t_kernel(tc, q, k, v, out):
         const = ctx.enter_context(tc.tile_pool(name="const", bufs=1))
         qtp = ctx.enter_context(tc.tile_pool(name="qtp", bufs=3))
         vgp = ctx.enter_context(tc.tile_pool(name="vgp", bufs=2))
+        jp = ctx.enter_context(tc.tile_pool(name="jp", bufs=2))
         ep = ctx.enter_context(tc.tile_pool(name="ep", bufs=3))
         gp = ctx.enter_context(tc.tile_pool(name="gp", bufs=2))
         cpl = ctx.enter_context(tc.tile_pool(name="cpl", bufs=3))
@@ -86,11 +87,13 @@ def tile_attend_t_kernel(tc, q, k, v, out):
         maskb = const.tile([P, PACK, 32], BF16, name="maskb")
         nc.vector.tensor_copy(out=maskb[:], in_=m32[:].rearrange("i (p t) -> i t p", t=PACK))
 
-        for b in range(1, B):
-            nc.gpsimd.dma_start(out=lds[b][2][:], in_=views[b][2])
-            nc.gpsimd.dma_start(out=lds[b][0][:], in_=views[b][0])
-            nc.gpsimd.dma_start(out=lds[b][1][:].rearrange("p h a d -> p (h a) d"),
-                                in_=views[b][1].rearrange("p h a d -> p (h a) d"))
+        def load(b):
+            if not 1 <= b < B:
+                return
+            nc.sync.dma_start(out=lds[b][2][:], in_=views[b][2])
+            nc.sync.dma_start(out=lds[b][0][:], in_=views[b][0])
+            nc.sync.dma_start(out=lds[b][1][:].rearrange("p h a d -> p (h a) d"),
+                              in_=views[b][1].rearrange("p h a d -> p (h a) d"))
 
         def ok(n):
             return 0 <= n < NP
@@ -100,10 +103,9 @@ def tile_attend_t_kernel(tc, q, k, v, out):
 
         def sm(n):
             if ("sm", n) not in st:
-                mx = small.tile([P, 8], F32, name="mx")
                 nbt = small.tile([P, 8], F32, name="nbt")
                 rs = small.tile([P, 8], F32, name="rs")
-                st[("sm", n)] = (mx, nbt, rs)
+                st[("sm", n)] = (nbt, rs)
             return st[("sm", n)]
 
         def kttr(n):
@@ -145,7 +147,8 @@ def tile_attend_t_kernel(tc, q, k, v, out):
                 return
             b, g = divmod(n, KVH)
             vg = vgp.tile([P, D, PACK], BF16, name="vg", align_bytes=64)
-            nc.vector.tensor_copy(out=vg[:], in_=lds[b][2][:, g, :].rearrange("p (t d) -> p d t", t=PACK))
+            nc.gpsimd.tensor_scalar(out=vg[:], in0=lds[b][2][:, g, :].rearrange("p (t d) -> p d t", t=PACK),
+                                    scalar1=1.0, scalar2=0.0, op0=ALU.mult, op1=ALU.add)
             st[("vg", n)] = vg
 
         def vqz(n):
@@ -181,28 +184,18 @@ def tile_attend_t_kernel(tc, q, k, v, out):
         def red(n, u):
             if not ok(n):
                 return
-            mx = sm(n)[0]
+            nbt = sm(n)[0]
             s, regs = st[("s", n, u)]
             c0 = UCOL[u]
-            if u == 2:
-                nc.vector.tensor_reduce(out=mx[:, c0:c0 + 2], in_=s[:].rearrange("i (x c) -> i x c", x=2),
-                                        axis=AX.X, op=ALU.max)
-            else:
-                for i, (x, a, w, flat, reg) in enumerate(regs):
-                    nc.vector.tensor_reduce(out=mx[:, c0 + i:c0 + i + 1], in_=flat, axis=AX.X, op=ALU.max)
-
-        def nb(n, u):
-            if not ok(n):
-                return
-            mx, nbt, rs = sm(n)
-            c0, c1 = UCOL[u], UCOL[u] + len(UNITS[u])
-            nc.vector.tensor_scalar(out=nbt[:, c0:c1], in0=mx[:, c0:c1], scalar1=-SCALE, scalar2=None,
-                                    op0=ALU.mult)
+            for i, (x, a, w, flat, reg) in enumerate(regs):
+                junk = jp.tile([P, N], F32, name="junk")
+                nc.vector.tensor_scalar(out=junk[:, 0:PACK * w], in0=flat, scalar1=-SCALE, scalar2=None,
+                                        op0=ALU.mult, op1=ALU.min, accum_out=nbt[:, c0 + i:c0 + i + 1])
 
         def ex(n, u):
             if not ok(n):
                 return
-            mx, nbt, rs = sm(n)
+            nbt, rs = sm(n)
             et = ep.tile([P, PACK, P], BF16, name="et%d" % u)
             c0 = UCOL[u]
             for i, (x, a, w, flat, reg) in enumerate(st[("s", n, u)][1]):
@@ -267,7 +260,7 @@ def tile_attend_t_kernel(tc, q, k, v, out):
             if not ok(n):
                 return
             rinv = small.tile([P, 8], F32, name="rinv")
-            nc.vector.reciprocal(out=rinv[:], in_=sm(n)[2][:])
+            nc.vector.reciprocal(out=rinv[:], in_=sm(n)[1][:])
             st[("rinv", n)] = rinv
 
         def nm(n, half):
@@ -288,43 +281,40 @@ def tile_attend_t_kernel(tc, q, k, v, out):
                     nc.sync.dma_start(out=dst[:, 1:NT:2, :], in_=ob[:, x:NT:2, :])
 
         for kk in range(-2, NP + 2):
-            tr(kk - 1, 1)
-            nm(kk - 2, 1)
+            if (kk + 4) % 2 == 0:
+                load((kk + 4) // 2)
+            ex(kk - 1, 4)
             qk(kk, 2)
             qttr(kk + 1)
-            nb(kk, 0)
-            ex(kk - 1, 4)
-            tr(kk - 1, 2)
-            cp(kk - 1, 1)
-            vrg(kk + 2)
             ex(kk, 0)
-            red(kk, 2)
-            nb(kk, 1)
-            rc(kk - 1)
-            qtcp(kk + 1)
+            tr(kk - 1, 1)
             qk(kk, 3)
+            tr(kk - 1, 2)
+            nm(kk - 2, 1)
             qz(kk - 1, 0)
-            kttr(kk + 2)
-            nb(kk, 2)
-            qk(kk, 4)
-            red(kk, 3)
-            qz(kk - 1, 1)
-            pv(kk - 1, 0)
-            ktcp(kk + 2)
-            nb(kk, 3)
-            cp(kk - 1, 2)
             ex(kk, 1)
-            qk(kk + 1, 0)
-            tr(kk, 0)
-            ex(kk, 2)
-            qz(kk - 1, 2)
-            ex(kk, 3)
-            qk(kk + 1, 1)
+            qk(kk, 4)
+            red(kk, 2)
+            pv(kk - 1, 0)
+            qtcp(kk + 1)
+            red(kk, 3)
+            rc(kk - 1)
             red(kk, 4)
-            cp(kk, 0)
-            nm(kk - 1, 0)
+            cp(kk - 1, 1)
+            kttr(kk + 2)
             vqz(kk + 1)
-            pv(kk - 1, 1)
-            nb(kk, 4)
+            tr(kk, 0)
+            qk(kk + 1, 0)
+            cp(kk - 1, 2)
+            ktcp(kk + 2)
+            qz(kk - 1, 1)
+            ex(kk, 2)
+            ex(kk, 3)
+            qz(kk - 1, 2)
+            nm(kk - 1, 0)
+            vrg(kk + 2)
+            qk(kk + 1, 1)
             red(kk + 1, 0)
             red(kk + 1, 1)
+            pv(kk - 1, 1)
+            cp(kk, 0)

@@ -38,7 +38,6 @@ def tile_attend_t_kernel(tc, q, k, v, out):
         const = ctx.enter_context(tc.tile_pool(name="const", bufs=1))
         qtp = ctx.enter_context(tc.tile_pool(name="qtp", bufs=3))
         vgp = ctx.enter_context(tc.tile_pool(name="vgp", bufs=2))
-        jp = ctx.enter_context(tc.tile_pool(name="jp", bufs=2))
         ep = ctx.enter_context(tc.tile_pool(name="ep", bufs=3))
         gp = ctx.enter_context(tc.tile_pool(name="gp", bufs=2))
         cpl = ctx.enter_context(tc.tile_pool(name="cpl", bufs=3))
@@ -103,9 +102,10 @@ def tile_attend_t_kernel(tc, q, k, v, out):
 
         def sm(n):
             if ("sm", n) not in st:
+                mx = small.tile([P, 8], F32, name="mx")
                 nbt = small.tile([P, 8], F32, name="nbt")
                 rs = small.tile([P, 8], F32, name="rs")
-                st[("sm", n)] = (nbt, rs)
+                st[("sm", n)] = (mx, nbt, rs)
             return st[("sm", n)]
 
         def kttr(n):
@@ -184,18 +184,28 @@ def tile_attend_t_kernel(tc, q, k, v, out):
         def red(n, u):
             if not ok(n):
                 return
-            nbt = sm(n)[0]
+            mx = sm(n)[0]
             s, regs = st[("s", n, u)]
             c0 = UCOL[u]
-            for i, (x, a, w, flat, reg) in enumerate(regs):
-                junk = jp.tile([P, N], F32, name="junk")
-                nc.vector.tensor_scalar(out=junk[:, 0:PACK * w], in0=flat, scalar1=-SCALE, scalar2=None,
-                                        op0=ALU.mult, op1=ALU.min, accum_out=nbt[:, c0 + i:c0 + i + 1])
+            if u == 2:
+                nc.vector.tensor_reduce(out=mx[:, c0:c0 + 2], in_=s[:].rearrange("i (x c) -> i x c", x=2),
+                                        axis=AX.X, op=ALU.max)
+            else:
+                for i, (x, a, w, flat, reg) in enumerate(regs):
+                    nc.vector.tensor_reduce(out=mx[:, c0 + i:c0 + i + 1], in_=flat, axis=AX.X, op=ALU.max)
+
+        def nb(n, u):
+            if not ok(n):
+                return
+            mx, nbt, rs = sm(n)
+            c0, c1 = UCOL[u], UCOL[u] + len(UNITS[u])
+            nc.gpsimd.tensor_scalar(out=nbt[:, c0:c1], in0=mx[:, c0:c1], scalar1=-SCALE, scalar2=0.0,
+                                    op0=ALU.mult, op1=ALU.add)
 
         def ex(n, u):
             if not ok(n):
                 return
-            nbt, rs = sm(n)
+            mx, nbt, rs = sm(n)
             et = ep.tile([P, PACK, P], BF16, name="et%d" % u)
             c0 = UCOL[u]
             for i, (x, a, w, flat, reg) in enumerate(st[("s", n, u)][1]):
@@ -221,7 +231,10 @@ def tile_attend_t_kernel(tc, q, k, v, out):
             cnt = len(BANKS[bi])
             xt = st[("xt", n, bi)]
             gr = gp.tile([P, 2, P, PACK], BF16, name="gr%d" % bi, align_bytes=64)
-            nc.scalar.copy(out=gr[:, 0:cnt], in_=xt[:, 0:cnt].rearrange("p s t i -> p s i t"))
+            if bi == 2 and n % 4 == 3:
+                nc.vector.tensor_copy(out=gr[:, 0:cnt], in_=xt[:, 0:cnt].rearrange("p s t i -> p s i t"))
+            else:
+                nc.scalar.copy(out=gr[:, 0:cnt], in_=xt[:, 0:cnt].rearrange("p s t i -> p s i t"))
             st[("gr", n, bi)] = gr
 
         def qz(n, bi):
@@ -260,7 +273,7 @@ def tile_attend_t_kernel(tc, q, k, v, out):
             if not ok(n):
                 return
             rinv = small.tile([P, 8], F32, name="rinv")
-            nc.vector.reciprocal(out=rinv[:], in_=sm(n)[1][:])
+            nc.vector.reciprocal(out=rinv[:], in_=sm(n)[2][:])
             st[("rinv", n)] = rinv
 
         def nm(n, half):
@@ -283,38 +296,43 @@ def tile_attend_t_kernel(tc, q, k, v, out):
         for kk in range(-2, NP + 2):
             if (kk + 4) % 2 == 0:
                 load((kk + 4) // 2)
-            ex(kk - 1, 4)
-            qk(kk, 2)
-            qttr(kk + 1)
-            ex(kk, 0)
-            tr(kk - 1, 1)
-            qk(kk, 3)
-            tr(kk - 1, 2)
+            nb(kk, 0)
             nm(kk - 2, 1)
             qz(kk - 1, 0)
-            ex(kk, 1)
-            qk(kk, 4)
+            qk(kk, 2)
+            tr(kk - 1, 1)
+            qttr(kk + 1)
+            ex(kk - 1, 4)
+            nb(kk, 1)
+            qk(kk, 3)
             red(kk, 2)
-            pv(kk - 1, 0)
             qtcp(kk + 1)
             red(kk, 3)
-            rc(kk - 1)
-            red(kk, 4)
-            cp(kk - 1, 1)
-            kttr(kk + 2)
+            tr(kk - 1, 2)
             vqz(kk + 1)
-            tr(kk, 0)
-            qk(kk + 1, 0)
+            ex(kk, 0)
+            qk(kk, 4)
+            rc(kk - 1)
+            cp(kk - 1, 1)
+            ex(kk, 1)
             cp(kk - 1, 2)
-            ktcp(kk + 2)
+            red(kk, 4)
+            pv(kk - 1, 0)
             qz(kk - 1, 1)
-            ex(kk, 2)
-            ex(kk, 3)
-            qz(kk - 1, 2)
+            nb(kk, 2)
+            nb(kk, 3)
             nm(kk - 1, 0)
             vrg(kk + 2)
-            qk(kk + 1, 1)
+            qk(kk + 1, 0)
+            nb(kk, 4)
+            qz(kk - 1, 2)
+            ex(kk, 2)
+            ex(kk, 3)
             red(kk + 1, 0)
+            tr(kk, 0)
+            cp(kk, 0)
+            kttr(kk + 2)
+            ktcp(kk + 2)
+            qk(kk + 1, 1)
             red(kk + 1, 1)
             pv(kk - 1, 1)
-            cp(kk, 0)

@@ -65,6 +65,8 @@ def tile_attend_t_kernel(tc, q, k, v, out):
 
         ident = const.tile([P, P], BF16, name="ident")
         make_identity(nc, ident[:])
+        identf = const.tile([P, P], F32, name="identf")
+        make_identity(nc, identf[:])
         m32 = const.tile([P, P], F32, name="m32")
         nc.gpsimd.memset(m32[:], 0.0)
         nc.gpsimd.affine_select(
@@ -206,23 +208,24 @@ def tile_attend_t_kernel(tc, q, k, v, out):
             if not ok(n):
                 return
             mx, nbt, rs = sm(n)
-            et = ep.tile([P, PACK, P], BF16, name="et%d" % u)
+            et = ep.tile([P, 2, P, 2], BF16, name="et%d" % u)
             c0 = UCOL[u]
             for i, (x, a, w, flat, reg) in enumerate(st[("s", n, u)][1]):
                 col = ECOL[(x, a)]
                 r = RCOL[(x, a)]
-                nc.scalar.activation(out=et[:, :, col:col + w], in_=reg, func=ACT.Exp,
+                nc.scalar.activation(out=et[:, :, col:col + w, :],
+                                     in_=reg.rearrange("i (h e) p -> i h p e", e=2), func=ACT.Exp,
                                      bias=nbt[:, c0 + i:c0 + i + 1], scale=SCALE, accum_out=rs[:, r:r + 1])
             st[("et", n, u)] = et
 
         def tr(n, bi):
             if not ok(n):
                 return
-            xt = ps.tile([P, 2, PACK, P], BF16, tag="x%d" % ((3 * n + bi) % 2), name="xt")
+            xt = ps.tile([P, 2, 2, P], F32, tag="x%d" % ((3 * n + bi) % 2), name="xt")
             for sl, j in enumerate(BANKS[bi]):
-                et = st[("et", n, j)]
-                for t in range(PACK):
-                    nc.tensor.transpose(xt[:, sl, t, :], et[:, t, :], ident[:])
+                words = st[("et", n, j)][:].rearrange("i h p e -> i (h p e)").bitcast(F32)
+                for h in range(2):
+                    nc.tensor.transpose(xt[:, sl, h, :], words[:, h * P:(h + 1) * P], identf[:])
             st[("xt", n, bi)] = xt
 
         def cp(n, bi):
@@ -232,9 +235,9 @@ def tile_attend_t_kernel(tc, q, k, v, out):
             xt = st[("xt", n, bi)]
             gr = gp.tile([P, 2, P, PACK], BF16, name="gr%d" % bi, align_bytes=64)
             if bi == 2 and n % 4 == 3:
-                nc.vector.tensor_copy(out=gr[:, 0:cnt], in_=xt[:, 0:cnt].rearrange("p s t i -> p s i t"))
+                nc.vector.tensor_copy(out=gr[:, 0:cnt].bitcast(F32), in_=xt[:, 0:cnt].rearrange("p s h i -> p s i h"))
             else:
-                nc.scalar.copy(out=gr[:, 0:cnt], in_=xt[:, 0:cnt].rearrange("p s t i -> p s i t"))
+                nc.scalar.copy(out=gr[:, 0:cnt].bitcast(F32), in_=xt[:, 0:cnt].rearrange("p s h i -> p s i h"))
             st[("gr", n, bi)] = gr
 
         def qz(n, bi):

@@ -63,6 +63,10 @@ def tile_attend_t_kernel(tc, q, k, v, out):
             nc.sync.dma_start(out=lds[0][1][:, g], in_=views[0][1][:, g])
             nc.sync.dma_start(out=lds[0][1][:, g + KVH], in_=views[0][1][:, g + KVH])
 
+        warm = const.tile([P, 2], F32, name="warm")
+        nc.vector.memset(warm[:], 0.0)
+        nc.scalar.activation(out=warm[:, 1:2], in_=warm[:, 0:1], func=ACT.Exp)
+
         ident = const.tile([P, P], BF16, name="ident")
         make_identity(nc, ident[:])
         identf = const.tile([P, P], F32, name="identf")
@@ -96,6 +100,12 @@ def tile_attend_t_kernel(tc, q, k, v, out):
             nc.sync.dma_start(out=lds[b][1][:].rearrange("p h a d -> p (h a) d"),
                               in_=views[b][1].rearrange("p h a d -> p (h a) d"))
 
+        turns = []
+
+        def ttag():
+            turns.append(0)
+            return "t%d" % (len(turns) % 2)
+
         def ok(n):
             return 0 <= n < NP
 
@@ -114,7 +124,7 @@ def tile_attend_t_kernel(tc, q, k, v, out):
             if not ok(n):
                 return
             b, g = divmod(n, KVH)
-            tk = ps.tile([P, 2 * N], BF16, tag="tq", name="tk")
+            tk = ps.tile([P, 2 * N], BF16, tag=ttag(), name="tk")
             for t in range(PACK):
                 nc.tensor.transpose(tk[:, t * P:(t + 1) * P], lds[b][0][:, g, t * D:(t + 1) * D], ident[:])
             st[("tk", n)] = tk
@@ -130,7 +140,7 @@ def tile_attend_t_kernel(tc, q, k, v, out):
             if not ok(n):
                 return
             b, g = divmod(n, KVH)
-            tq = ps.tile([P, 2 * N], BF16, tag="tq", name="tq")
+            tq = ps.tile([P, 2 * N], BF16, tag=ttag(), name="tq")
             for x in range(2):
                 for a in range(NT):
                     j = x * NT + a
@@ -141,7 +151,7 @@ def tile_attend_t_kernel(tc, q, k, v, out):
             if not ok(n):
                 return
             qt = qtp.tile([P, 2, NT, P], BF16, name="qt")
-            nc.vector.tensor_copy(out=qt[:].rearrange("d x a i -> d (x a i)"), in_=st[("tq", n)][:])
+            nc.scalar.copy(out=qt[:].rearrange("d x a i -> d (x a i)"), in_=st[("tq", n)][:])
             st[("qt", n)] = qt
 
         def vrg(n):
@@ -169,7 +179,7 @@ def tile_attend_t_kernel(tc, q, k, v, out):
             if not ok(n):
                 return
             qt, kt = st[("qt", n)], st[("kt", n)]
-            s = ps.tile([P, N], F32, tag="s%d" % ((5 * n + u) % 4), name="s")
+            s = ps.tile([P, N], F32, tag="s%d" % u, name="s")
             regs = []
             off = 0
             for (x, a) in UNITS[u]:
@@ -221,7 +231,7 @@ def tile_attend_t_kernel(tc, q, k, v, out):
         def tr(n, bi):
             if not ok(n):
                 return
-            xt = ps.tile([P, 2, 2, P], F32, tag="x%d" % ((3 * n + bi) % 2), name="xt")
+            xt = ps.tile([P, 2, 2, P], F32, tag=ttag(), name="xt")
             for sl, j in enumerate(BANKS[bi]):
                 words = st[("et", n, j)][:].rearrange("i h p e -> i (h p e)").bitcast(F32)
                 for h in range(2):
@@ -234,10 +244,7 @@ def tile_attend_t_kernel(tc, q, k, v, out):
             cnt = len(BANKS[bi])
             xt = st[("xt", n, bi)]
             gr = gp.tile([P, 2, P, PACK], BF16, name="gr%d" % bi, align_bytes=64)
-            if bi == 2 and n % 4 == 3:
-                nc.vector.tensor_copy(out=gr[:, 0:cnt].bitcast(F32), in_=xt[:, 0:cnt].rearrange("p s h i -> p s i h"))
-            else:
-                nc.scalar.copy(out=gr[:, 0:cnt].bitcast(F32), in_=xt[:, 0:cnt].rearrange("p s h i -> p s i h"))
+            nc.scalar.copy(out=gr[:, 0:cnt].bitcast(F32), in_=xt[:, 0:cnt].rearrange("p s h i -> p s i h"))
             st[("gr", n, bi)] = gr
 
         def qz(n, bi):
@@ -296,46 +303,46 @@ def tile_attend_t_kernel(tc, q, k, v, out):
                 else:
                     nc.sync.dma_start(out=dst[:, 1:NT:2, :], in_=ob[:, x:NT:2, :])
 
-        for kk in range(-2, NP + 2):
-            if (kk + 4) % 2 == 0:
-                load((kk + 4) // 2)
-            nb(kk, 0)
-            nm(kk - 2, 1)
-            qz(kk - 1, 0)
-            qk(kk, 2)
-            tr(kk - 1, 1)
-            qttr(kk + 1)
-            ex(kk - 1, 4)
-            nb(kk, 1)
-            qk(kk, 3)
-            red(kk, 2)
-            qtcp(kk + 1)
-            red(kk, 3)
-            tr(kk - 1, 2)
-            vqz(kk + 1)
-            ex(kk, 0)
-            qk(kk, 4)
-            rc(kk - 1)
-            cp(kk - 1, 1)
-            ex(kk, 1)
-            cp(kk - 1, 2)
-            red(kk, 4)
-            pv(kk - 1, 0)
-            qz(kk - 1, 1)
-            nb(kk, 2)
-            nb(kk, 3)
-            nm(kk - 1, 0)
-            vrg(kk + 2)
-            qk(kk + 1, 0)
-            nb(kk, 4)
-            qz(kk - 1, 2)
-            ex(kk, 2)
-            ex(kk, 3)
-            red(kk + 1, 0)
-            tr(kk, 0)
-            cp(kk, 0)
-            kttr(kk + 2)
-            ktcp(kk + 2)
-            qk(kk + 1, 1)
-            red(kk + 1, 1)
-            pv(kk - 1, 1)
+        for n in range(-2, NP + 2):
+            if n % 2 == 0:
+                load(n // 2 + 2)
+            tr(n - 1, 1)
+            pv(n - 2, 1)
+            qk(n, 4)
+            ex(n, 0)
+            qtcp(n + 1)
+            qz(n - 1, 0)
+            red(n, 3)
+            nb(n, 3)
+            tr(n - 1, 2)
+            qk(n + 1, 0)
+            ex(n, 1)
+            cp(n - 1, 1)
+            nm(n - 2, 1)
+            red(n, 4)
+            nb(n, 4)
+            vrg(n + 2)
+            kttr(n + 2)
+            pv(n - 1, 0)
+            qk(n + 1, 1)
+            ex(n, 2)
+            cp(n - 1, 2)
+            rc(n - 1)
+            vqz(n + 1)
+            red(n + 1, 0)
+            nb(n + 1, 0)
+            tr(n, 0)
+            qk(n + 1, 2)
+            ex(n, 3)
+            ktcp(n + 2)
+            qz(n - 1, 1)
+            nm(n - 1, 0)
+            red(n + 1, 1)
+            nb(n + 1, 1)
+            qttr(n + 2)
+            qk(n + 1, 3)
+            ex(n, 4)
+            cp(n, 0)
+            qz(n - 1, 2)
+            red(n + 1, 2)
+            nb(n + 1, 2)

@@ -16,19 +16,35 @@ AX = mybir.AxisListType
 
 B, H, KVH, N, D = 8, 4, 2, 512, 128
 P = 128
-NT = N // P
 PACK = 4
 SCALE = 1.0 / math.sqrt(D)
 NEG = -1.0e30
 FLOPS = 4 * B * H * N * N * D
-NP = B * KVH
-NV = 4
+HQ = 64
+NM = N // HQ
+SL = HQ // PACK
+NSETS = 2
 
-UNITS = [[(0, 2), (0, 0)], [(1, 2), (1, 0)], [(0, 1), (1, 1)], [(0, 3)], [(1, 3)]]
-UCOL = [0, 2, 4, 6, 7]
-ECOL = {(0, 2): 0, (0, 0): 96, (1, 2): 0, (1, 0): 96, (0, 1): 0, (1, 1): 64, (0, 3): 0, (1, 3): 0}
-RCOL = {(0, 0): 0, (0, 2): 1, (1, 0): 2, (1, 2): 3, (0, 1): 4, (1, 1): 5, (0, 3): 6, (1, 3): 7}
-BANKS = [[0, 1], [2, 3], [4]]
+UNITS = [[(0, 0), (0, 6)], [(0, 2), (0, 4)], [(1, 0), (1, 6)], [(1, 2), (1, 4)], [(0, 1), (0, 5)], [(0, 7)],
+         [(1, 1), (1, 5)], [(1, 7)], [(0, 3), (1, 3)]]
+NU = len(UNITS)
+UCOL = [0, 2, 4, 6, 8, 10, 11, 13, 14]
+GROUPS = [[0, 1], [2, 3], [4, 5], [6, 7], [8]]
+QGROUP = [[0, 1], [2, 3], [4]]
+OBANK = [[0, 1], [2, 3], [4, 5, 8], [6, 7, 8]]
+NS = 5
+
+
+def width(m):
+    return SL * (m + 1)
+
+
+def shift(m):
+    return P - width(m) if m <= 3 else 0
+
+
+def plane_row(blk):
+    return 32 * (blk // 4) + blk % 4
 
 
 def tile_attend_t_kernel(tc, q, k, v, out):
@@ -36,36 +52,58 @@ def tile_attend_t_kernel(tc, q, k, v, out):
     with ExitStack() as ctx:
         ctx.enter_context(tc.manual_schedule())
         const = ctx.enter_context(tc.tile_pool(name="const", bufs=1))
-        qtp = ctx.enter_context(tc.tile_pool(name="qtp", bufs=3))
+        qtp = ctx.enter_context(tc.tile_pool(name="qtp", bufs=2))
         vgp = ctx.enter_context(tc.tile_pool(name="vgp", bufs=2))
-        ep = ctx.enter_context(tc.tile_pool(name="ep", bufs=3))
+        ep = ctx.enter_context(tc.tile_pool(name="ep", bufs=8))
         gp = ctx.enter_context(tc.tile_pool(name="gp", bufs=2))
-        cpl = ctx.enter_context(tc.tile_pool(name="cpl", bufs=3))
-        small = ctx.enter_context(tc.tile_pool(name="small", bufs=6))
-        obp = ctx.enter_context(tc.tile_pool(name="obp", bufs=4))
+        cpl = ctx.enter_context(tc.tile_pool(name="cpl", bufs=2))
+        small = ctx.enter_context(tc.tile_pool(name="small", bufs=4))
+        obp = ctx.enter_context(tc.tile_pool(name="obp", bufs=3))
         ps = ctx.enter_context(tc.psum_pool(name="ps", bufs=1))
 
         st = {}
+        turns = []
+
+        def ttag():
+            turns.append(0)
+            return "t%d" % (len(turns) % 2)
+
+        def ok(b):
+            return 0 <= b < B
 
         lds = []
-        views = []
         for b in range(B):
             kb = const.tile([P, KVH, N], BF16, name="kb%d" % b)
-            qb = const.tile([P, H, NT, D], BF16, name="qb%d" % b)
+            qb = const.tile([P, KVH, NM, D], BF16, name="qb%d" % b)
             vb = const.tile([P, KVH, N], BF16, name="vb%d" % b)
             lds.append((kb, qb, vb))
-            views.append((k[b].rearrange("g (p t) d -> p g (t d)", t=PACK),
-                          q[b].rearrange("h (a p) d -> p h a d", p=P),
-                          v[b].rearrange("g (p t) d -> p g (t d)", t=PACK)))
-        for g in range(KVH):
-            nc.sync.dma_start(out=lds[0][0][:, g, :], in_=views[0][0][:, g, :])
-            nc.sync.dma_start(out=lds[0][2][:, g, :], in_=views[0][2][:, g, :])
-            nc.sync.dma_start(out=lds[0][1][:, g], in_=views[0][1][:, g])
-            nc.sync.dma_start(out=lds[0][1][:, g + KVH], in_=views[0][1][:, g + KVH])
+
+        def load(b):
+            if not ok(b):
+                return
+            kb, qb, vb = lds[b]
+            nc.sync.dma_start(out=kb[:], in_=k[b].rearrange("g (p t) d -> p g (t d)", t=PACK))
+            for x in range(2):
+                nc.sync.dma_start(out=qb[HQ * x:HQ * (x + 1)].rearrange("i g m d -> i (g m) d"),
+                                  in_=q[b, KVH * x:KVH * (x + 1)].rearrange("g (m i) d -> i (g m) d", i=HQ))
+            nc.sync.dma_start(out=vb[:], in_=v[b].rearrange("g (p t) d -> p g (t d)", t=PACK))
+
+        load(0)
 
         warm = const.tile([P, 2], F32, name="warm")
         nc.vector.memset(warm[:], 0.0)
         nc.scalar.activation(out=warm[:, 1:2], in_=warm[:, 0:1], func=ACT.Exp)
+
+        vsets = []
+        for j in range(NSETS):
+            vc = const.tile([P, KVH, D], U32, name="vc%d" % j, align_bytes=64)
+            vsc = const.tile([P, KVH, D], U8, name="vsc%d" % j, align_bytes=64)
+            rcod = const.tile([P, NM, KVH, D], U32, name="rcod%d" % j, align_bytes=64)
+            rsca = const.tile([P, NM // 2, KVH, D], U8, name="rsca%d" % j, align_bytes=64)
+            nc.vector.memset(vsc[:].rearrange("p g d -> p (g d)").bitcast(I32), 0)
+            nc.vector.memset(rcod[:, 0:NM - 1].rearrange("p m g d -> p (m g d)").bitcast(I32), 0)
+            nc.vector.memset(rsca[:].rearrange("p m g d -> p (m g d)").bitcast(I32), 0)
+            vsets.append((vc, vsc, rcod, rsca))
 
         ident = const.tile([P, P], BF16, name="ident")
         make_identity(nc, ident[:])
@@ -77,272 +115,296 @@ def tile_attend_t_kernel(tc, q, k, v, out):
             out=m32[:], in_=m32[:], compare_op=ALU.is_ge, fill=NEG, base=0,
             pattern=[[-1, P]], channel_multiplier=1,
         )
-        vsets = []
-        for j in range(NV):
-            vc = const.tile([P, D], U32, name="vc%d" % j, align_bytes=64)
-            vsc = const.tile([P, D], U8, name="vsc%d" % j, align_bytes=64)
-            r20c = const.tile([P, 2 * D], U32, name="r20c%d" % j, align_bytes=64)
-            r20s = const.tile([P, 2 * D], U8, name="r20s%d" % j, align_bytes=64)
-            r11c = const.tile([P, 2 * D], U32, name="r11c%d" % j, align_bytes=64)
-            r11s = const.tile([P, 2 * D], U8, name="r11s%d" % j, align_bytes=64)
-            for t in (vsc, r20c, r20s, r11c, r11s):
-                nc.vector.memset(t[:].bitcast(I32), 0)
-            vsets.append((vc, vsc, r20c, r20s, r11c, r11s))
-
-        maskb = const.tile([P, PACK, 32], BF16, name="maskb")
-        nc.vector.tensor_copy(out=maskb[:], in_=m32[:].rearrange("i (p t) -> i t p", t=PACK))
-
-        def load(b):
-            if not 1 <= b < B:
-                return
-            nc.sync.dma_start(out=lds[b][2][:], in_=views[b][2])
-            nc.sync.dma_start(out=lds[b][0][:], in_=views[b][0])
-            nc.sync.dma_start(out=lds[b][1][:].rearrange("p h a d -> p (h a) d"),
-                              in_=views[b][1].rearrange("p h a d -> p (h a) d"))
-
-        turns = []
-
-        def ttag():
-            turns.append(0)
-            return "t%d" % (len(turns) % 2)
-
-        def ok(n):
-            return 0 <= n < NP
+        maskb = const.tile([P, PACK, SL], BF16, name="maskb")
+        for x in range(2):
+            rows = slice(HQ * x, HQ * (x + 1))
+            nc.vector.tensor_copy(out=maskb[rows], in_=m32[rows, HQ * x:HQ * (x + 1)].rearrange("i (p t) -> i t p", t=PACK))
 
         def move(dst, src):
             nc.sync.dma_start(out=dst.bitcast(I32), in_=src.bitcast(I32))
 
-        def sm(n):
-            if ("sm", n) not in st:
-                mx = small.tile([P, 8], F32, name="mx")
-                nbt = small.tile([P, 8], F32, name="nbt")
-                rs = small.tile([P, 8], F32, name="rs")
-                st[("sm", n)] = (mx, nbt, rs)
-            return st[("sm", n)]
+        def sm(b):
+            if ("sm", b) not in st:
+                mx = small.tile([P, 16], F32, name="mx")
+                nbt = small.tile([P, 16], F32, name="nbt")
+                rs = small.tile([P, 16], F32, name="rs")
+                rinv = small.tile([P, 16], F32, name="rinv")
+                st[("sm", b)] = (mx, nbt, rs, rinv)
+            return st[("sm", b)]
 
-        def kttr(n):
-            if not ok(n):
+        def kttr(b):
+            if not ok(b):
                 return
-            b, g = divmod(n, KVH)
-            tk = ps.tile([P, 2 * N], BF16, tag=ttag(), name="tk")
-            for t in range(PACK):
-                nc.tensor.transpose(tk[:, t * P:(t + 1) * P], lds[b][0][:, g, t * D:(t + 1) * D], ident[:])
-            st[("tk", n)] = tk
+            tk = ps.tile([P, KVH, PACK, P], BF16, tag=ttag(), name="tk")
+            for g in range(KVH):
+                for t in range(PACK):
+                    nc.tensor.transpose(tk[:, g, t, :], lds[b][0][:, g, t * D:(t + 1) * D], ident[:])
+            st[("tk", b)] = tk
 
-        def ktcp(n):
-            if not ok(n):
+        def ktcp(b):
+            if not ok(b):
                 return
-            kt = qtp.tile([P, PACK, P], BF16, name="kt")
-            nc.vector.tensor_copy(out=kt[:].rearrange("d t p -> d (t p)"), in_=st[("tk", n)][:, 0:N])
-            st[("kt", n)] = kt
+            kt = qtp.tile([P, KVH, PACK, P], BF16, name="kt")
+            KTCP(out=kt[:].rearrange("d g t p -> d (g t p)"), in_=st[("tk", b)][:].rearrange("d g t p -> d (g t p)"))
+            st[("kt", b)] = kt
 
-        def qttr(n):
-            if not ok(n):
+        def qttr(b, g):
+            if not ok(b):
                 return
-            b, g = divmod(n, KVH)
-            tq = ps.tile([P, 2 * N], BF16, tag=ttag(), name="tq")
-            for x in range(2):
-                for a in range(NT):
-                    j = x * NT + a
-                    nc.tensor.transpose(tq[:, j * P:(j + 1) * P], lds[b][1][:, g + KVH * x, a, :], ident[:])
-            st[("tq", n)] = tq
+            tq = ps.tile([P, NM, P], BF16, tag=ttag(), name="tq")
+            for m in range(NM):
+                nc.tensor.transpose(tq[:, m, :], lds[b][1][:, g, m, :], ident[:])
+            st[("tq", b, g)] = tq
 
-        def qtcp(n):
-            if not ok(n):
+        def qtcp(b, g):
+            if not ok(b):
                 return
-            qt = qtp.tile([P, 2, NT, P], BF16, name="qt")
-            nc.scalar.copy(out=qt[:].rearrange("d x a i -> d (x a i)"), in_=st[("tq", n)][:])
-            st[("qt", n)] = qt
+            qt = qtp.tile([P, NM, P], BF16, name="qt%d" % g)
+            nc.scalar.copy(out=qt[:].rearrange("d m i -> d (m i)"), in_=st[("tq", b, g)][:].rearrange("d m i -> d (m i)"))
+            st[("qt", b, g)] = qt
 
-        def vrg(n):
-            if not ok(n):
+        def vrg(b, g):
+            if not ok(b):
                 return
-            b, g = divmod(n, KVH)
-            vg = vgp.tile([P, D, PACK], BF16, name="vg", align_bytes=64)
-            nc.gpsimd.tensor_scalar(out=vg[:], in0=lds[b][2][:, g, :].rearrange("p (t d) -> p d t", t=PACK),
+            if g == 0:
+                vg = vgp.tile([P, KVH, D, PACK], BF16, name="vg", align_bytes=64)
+                st[("vg", b)] = vg
+            vg = st[("vg", b)]
+            nc.gpsimd.tensor_scalar(out=vg[:, g], in0=lds[b][2][:, g, :].rearrange("p (t d) -> p d t", t=PACK),
                                     scalar1=1.0, scalar2=0.0, op0=ALU.mult, op1=ALU.add)
-            st[("vg", n)] = vg
 
-        def vqz(n):
-            if not ok(n):
+        def vqz(b):
+            if not ok(b):
                 return
-            vc, vsc, r20c, r20s, r11c, r11s = vsets[n % NV]
-            vg = st[("vg", n)]
-            nc.vector.quantize_mx(out=vc[:].bitcast(FP8X4), scales=vsc[:], in_=vg[:].rearrange("p d t -> p (d t)"))
-            for cod, r20, r11 in ((vc, r20c, r11c), (vsc, r20s, r11s)):
-                move(r20[96:128, 0:D], cod[0:32, :])
-                move(r20[0:96, D:2 * D], cod[0:96, :])
-                move(r11[0:64, 0:D], cod[0:64, :])
-                move(r11[64:128, D:2 * D], cod[0:64, :])
+            vc, vsc, rcod, rsca = vsets[b % NSETS]
+            nc.vector.quantize_mx(out=vc[:].rearrange("p g d -> p (g d)").bitcast(FP8X4),
+                                  scales=vsc[:].rearrange("p g d -> p (g d)"),
+                                  in_=st[("vg", b)][:].rearrange("p g d t -> p (g d t)"))
+            for m in range(NM - 1):
+                w = width(m)
+                sh = shift(m)
+                for gs in ((slice(0, KVH),) if m != 3 else (slice(0, 1), slice(1, 2))):
+                    s_ = sh if (m != 3 or gs.start == 0) else 0
+                    move(rcod[s_:s_ + w, m, gs, :], vc[0:w, gs, :])
+                    blk = 0
+                    while s_ > 0 and blk < w // 8:
+                        cnt = 1
+                        while (blk + cnt < w // 8 and plane_row(blk + cnt) == plane_row(blk) + cnt
+                               and plane_row(blk + cnt + s_ // 8) == plane_row(blk + s_ // 8) + cnt):
+                            cnt += 1
+                        s0, d0 = plane_row(blk), plane_row(blk + s_ // 8)
+                        move(rsca[d0:d0 + cnt, m, gs, :], vsc[s0:s0 + cnt, gs, :])
+                        blk += cnt
 
-        def qk(n, u):
-            if not ok(n):
+        def rcol(g, m):
+            return 8 * (m % 2) + 4 * g + m // 2
+
+        def norm(b, j):
+            return b + j // NU, j % NU
+
+        def qk(b, j):
+            b, j = norm(b, j)
+            if not ok(b):
                 return
-            qt, kt = st[("qt", n)], st[("kt", n)]
-            s = ps.tile([P, N], F32, tag="s%d" % u, name="s")
+            kt = st[("kt", b)]
+            s = ps.tile([P, N], F32, tag="s%d" % ((NU * b + j) % NS), name="s")
             regs = []
             off = 0
-            for (x, a) in UNITS[u]:
-                w = 32 * (a + 1)
+            for (g, m) in UNITS[j]:
+                w = width(m)
                 flat = s[:, off:off + PACK * w]
                 reg = flat.rearrange("i (t p) -> i t p", t=PACK)
-                nc.tensor.matmul(out=reg, lhsT=qt[:, x, a, :], rhs=kt[:, :, 0:w], start=True, stop=False)
-                nc.tensor.matmul(out=reg[:, :, 32 * a:32 * a + 32], lhsT=ident[:], rhs=maskb[:],
-                                 start=False, stop=True)
-                regs.append((x, a, w, flat, reg))
+                nc.tensor.matmul(out=reg, lhsT=st[("qt", b, g)][:, m, :], rhs=kt[:, g, :, 0:w], start=True, stop=False)
+                nc.tensor.matmul(out=reg[:, :, w - SL:w], lhsT=ident[:], rhs=maskb[:], start=False, stop=True)
+                regs.append((w, flat, reg))
                 off += PACK * w
-            st[("s", n, u)] = (s, regs)
+            st[("s", b, j)] = (s, regs)
 
-        def red(n, u):
-            if not ok(n):
+        def red(b, j):
+            b, j = norm(b, j)
+            if not ok(b):
                 return
-            mx = sm(n)[0]
-            s, regs = st[("s", n, u)]
-            c0 = UCOL[u]
-            if u == 2:
-                nc.vector.tensor_reduce(out=mx[:, c0:c0 + 2], in_=s[:].rearrange("i (x c) -> i x c", x=2),
-                                        axis=AX.X, op=ALU.max)
+            mx = sm(b)[0]
+            s, regs = st[("s", b, j)]
+            c0 = UCOL[j]
+            if len(regs) == 2 and regs[0][0] == regs[1][0]:
+                nc.vector.tensor_reduce(out=mx[:, c0:c0 + 2], in_=s[:].rearrange("i (x c) -> i x c", x=2), axis=AX.X, op=ALU.max)
             else:
-                for i, (x, a, w, flat, reg) in enumerate(regs):
+                for i, (w, flat, reg) in enumerate(regs):
                     nc.vector.tensor_reduce(out=mx[:, c0 + i:c0 + i + 1], in_=flat, axis=AX.X, op=ALU.max)
-
-        def nb(n, u):
-            if not ok(n):
-                return
-            mx, nbt, rs = sm(n)
-            c0, c1 = UCOL[u], UCOL[u] + len(UNITS[u])
-            nc.gpsimd.tensor_scalar(out=nbt[:, c0:c1], in0=mx[:, c0:c1], scalar1=-SCALE, scalar2=0.0,
+            c1 = c0 + len(regs)
+            nc.gpsimd.tensor_scalar(out=sm(b)[1][:, c0:c1], in0=mx[:, c0:c1], scalar1=-SCALE, scalar2=0.0,
                                     op0=ALU.mult, op1=ALU.add)
 
-        def ex(n, u):
-            if not ok(n):
+        def ex(b, j):
+            if not ok(b):
                 return
-            mx, nbt, rs = sm(n)
-            et = ep.tile([P, 2, P, 2], BF16, name="et%d" % u)
-            c0 = UCOL[u]
-            for i, (x, a, w, flat, reg) in enumerate(st[("s", n, u)][1]):
-                col = ECOL[(x, a)]
-                r = RCOL[(x, a)]
-                nc.scalar.activation(out=et[:, :, col:col + w, :],
-                                     in_=reg.rearrange("i (h e) p -> i h p e", e=2), func=ACT.Exp,
-                                     bias=nbt[:, c0 + i:c0 + i + 1], scale=SCALE, accum_out=rs[:, r:r + 1])
-            st[("et", n, u)] = et
+            mx, nbt, rs, rinv = sm(b)
+            et = ep.tile([P, 2, P, 2], BF16, name="et")
+            regs = st[("s", b, j)][1]
+            c0 = UCOL[j]
+            for i, (w, flat, reg) in enumerate(regs):
+                col = regs[1][0] if (len(regs) == 2 and i == 0) else 0
+                nc.scalar.activation(out=et[:, :, col:col + w, :], in_=reg.rearrange("i (h e) p -> i h p e", e=2),
+                                     func=ACT.Exp, bias=nbt[:, c0 + i:c0 + i + 1], scale=SCALE,
+                                     accum_out=rs[:, rcol(*UNITS[j][i]):rcol(*UNITS[j][i]) + 1])
+            st[("et", b, j)] = et
 
-        def tr(n, bi):
-            if not ok(n):
+        def tr(b, gi):
+            if not ok(b):
                 return
             xt = ps.tile([P, 2, 2, P], F32, tag=ttag(), name="xt")
-            for sl, j in enumerate(BANKS[bi]):
-                words = st[("et", n, j)][:].rearrange("i h p e -> i (h p e)").bitcast(F32)
+            for sl, j in enumerate(GROUPS[gi]):
+                words = st[("et", b, j)][:].rearrange("i h p e -> i (h p e)").bitcast(F32)
                 for h in range(2):
                     nc.tensor.transpose(xt[:, sl, h, :], words[:, h * P:(h + 1) * P], identf[:])
-            st[("xt", n, bi)] = xt
+            st[("xt", b, gi)] = xt
 
-        def cp(n, bi):
-            if not ok(n):
+        def cp(b, gi):
+            if not ok(b):
                 return
-            cnt = len(BANKS[bi])
-            xt = st[("xt", n, bi)]
-            gr = gp.tile([P, 2, P, PACK], BF16, name="gr%d" % bi, align_bytes=64)
-            nc.scalar.copy(out=gr[:, 0:cnt].bitcast(F32), in_=xt[:, 0:cnt].rearrange("p s h i -> p s i h"))
-            st[("gr", n, bi)] = gr
+            cnt = len(GROUPS[gi])
+            qi = gi // 2
+            if gi % 2 == 0:
+                gr = gp.tile([P, 2 * len(QGROUP[qi]), P, PACK], BF16, name="gr%d" % qi, align_bytes=64)
+                st[("gr", b, qi)] = gr
+            gr = st[("gr", b, qi)]
+            lo = 2 * (gi % 2)
+            nc.scalar.copy(out=gr[:, lo:lo + cnt].bitcast(F32), in_=st[("xt", b, gi)][:, 0:cnt].rearrange("p s h i -> p s i h"))
 
-        def qz(n, bi):
-            if not ok(n):
+        def qz(b, qi):
+            if not ok(b):
                 return
-            cnt = len(BANKS[bi])
-            gr = st[("gr", n, bi)]
-            ec = cpl.tile([P, 2 * P], U32, name="ec%d" % bi, align_bytes=64)
-            esc = cpl.tile([P, 2 * P], U8, name="esc%d" % bi, align_bytes=64)
+            units = [j for gi in QGROUP[qi] for j in GROUPS[gi]]
+            cnt = len(units)
+            gr = st[("gr", b, qi)]
+            ec = cpl.tile([P, 4 * P], U32, name="ec%d" % qi, align_bytes=64)
+            esc = cpl.tile([P, 4 * P], U8, name="esc%d" % qi, align_bytes=64)
             nc.vector.quantize_mx(out=ec[:, 0:cnt * P].bitcast(FP8X4), scales=esc[:, 0:cnt * P],
                                   in_=gr[:, 0:cnt].rearrange("p s i t -> p (s i t)"))
-            for sl, j in enumerate(BANKS[bi]):
-                st[("c", n, j)] = (ec[:, sl * P:(sl + 1) * P], esc[:, sl * P:(sl + 1) * P])
+            for sl, j in enumerate(units):
+                st[("c", b, j)] = (ec[:, sl * P:(sl + 1) * P], esc[:, sl * P:(sl + 1) * P])
 
-        def pv(n, half):
-            if not ok(n):
+        def pv(b, oi):
+            if not ok(b):
                 return
-            vc, vsc, r20c, r20s, r11c, r11s = vsets[n % NV]
-            plan = [
-                [(0, 0, r20c, r20s, 2 * D), (1, 2 * D, r20c, r20s, 2 * D)],
-                [(2, 0, r11c, r11s, 2 * D), (3, 2 * D, vc, vsc, D), (4, 3 * D, vc, vsc, D)],
-            ]
-            o = ps.tile([P, NT, D], F32, tag="o", name="o")
-            oflat = o[:].rearrange("i a d -> i (a d)")
-            for (j, col, rc_, rsc, width) in plan[half]:
-                cod, sca = st[("c", n, j)]
-                nc.tensor.matmul_mx(
-                    out=oflat[:, col:col + width],
-                    lhsT=cod.bitcast(FP8X4), lhsT_scale=sca,
-                    rhs=rc_[:, 0:width].bitcast(FP8X4), rhs_scale=rsc[:, 0:width],
-                    start=True, stop=True,
-                )
-            st[("o", n, half)] = o
+            vc, vsc, rcod, rsca = vsets[b % NSETS]
+            o = ps.tile([P, 4, D], F32, tag=("o" if b < B - 1 else "s%d" % oi), name="o")
+            for j in OBANK[oi]:
+                cod, sca = st[("c", b, j)]
+                for i, (g, m) in enumerate(UNITS[j]):
+                    if 2 * (m % 2) + g != oi:
+                        continue
+                    shifted = len(UNITS[j]) == 2 and i == 0
+                    rhs = vc[:, g, :] if m == NM - 1 else rcod[:, m, g, :]
+                    rsc = rsca[:, m, g, :] if shifted else vsc[:, g, :]
+                    nc.tensor.matmul_mx(out=o[:, m // 2, :], lhsT=cod.bitcast(FP8X4), lhsT_scale=sca,
+                                        rhs=rhs.bitcast(FP8X4), rhs_scale=rsc, start=True, stop=True)
+            st[("o", b, oi)] = o
 
-        def rc(n):
-            if not ok(n):
+        def rc(b, half):
+            if not ok(b):
                 return
-            rinv = small.tile([P, 8], F32, name="rinv")
-            nc.vector.reciprocal(out=rinv[:], in_=sm(n)[2][:])
-            st[("rinv", n)] = rinv
+            mx, nbt, rs, rinv = sm(b)
+            nc.vector.reciprocal(out=rinv[:, 8 * half:8 * half + 8], in_=rs[:, 8 * half:8 * half + 8])
 
-        def nm(n, half):
-            if not ok(n):
+        def nm(b, oi):
+            if not ok(b):
                 return
-            b, g = divmod(n, KVH)
-            o = st[("o", n, half)]
-            rinv = st[("rinv", n)]
-            ob = obp.tile([P, NT, D], F32, name="ob")
-            nc.vector.tensor_tensor(
-                out=ob[:], in0=o[:],
-                in1=rinv[:, half * NT:(half + 1) * NT].unsqueeze(2).to_broadcast([P, NT, D]), op=ALU.mult)
-            for x in range(2):
-                dst = out[b, g + KVH * x].rearrange("(a p) d -> p a d", p=P)
-                if half == 0:
-                    nc.sync.dma_start(out=dst[:, 0:NT:2, :], in_=ob[:, 2 * x:2 * x + 2, :])
-                else:
-                    nc.sync.dma_start(out=dst[:, 1:NT:2, :], in_=ob[:, x:NT:2, :])
+            o = st[("o", b, oi)]
+            rinv = sm(b)[3]
+            g, par = oi % 2, oi // 2
+            if g == 0:
+                ob = obp.tile([P, KVH, 4, D], F32, name="ob")
+                st[("ob", b, par)] = ob
+            ob = st[("ob", b, par)]
+            nc.vector.tensor_tensor(out=ob[:, g], in0=o[:],
+                                    in1=rinv[:, 4 * oi:4 * oi + 4].unsqueeze(2).to_broadcast([P, 4, D]), op=ALU.mult)
+            if g == KVH - 1:
+                for x in range(2):
+                    dst = out[b, KVH * x:KVH * (x + 1)].rearrange("g (m i) d -> i (g m) d", i=HQ)
+                    nc.sync.dma_start(out=dst[:, par:KVH * NM:2, :],
+                                      in_=ob[HQ * x:HQ * (x + 1)].rearrange("i g a d -> i (g a) d"))
 
-        for n in range(-2, NP + 2):
-            if n % 2 == 0:
-                load(n // 2 + 2)
-            tr(n - 1, 1)
-            pv(n - 2, 1)
-            qk(n, 4)
-            ex(n, 0)
-            qtcp(n + 1)
-            qz(n - 1, 0)
-            red(n, 3)
-            nb(n, 3)
-            tr(n - 1, 2)
-            qk(n + 1, 0)
-            ex(n, 1)
-            cp(n - 1, 1)
-            nm(n - 2, 1)
-            red(n, 4)
-            nb(n, 4)
-            vrg(n + 2)
-            kttr(n + 2)
-            pv(n - 1, 0)
-            qk(n + 1, 1)
-            ex(n, 2)
-            cp(n - 1, 2)
-            rc(n - 1)
-            vqz(n + 1)
-            red(n + 1, 0)
-            nb(n + 1, 0)
-            tr(n, 0)
-            qk(n + 1, 2)
-            ex(n, 3)
-            ktcp(n + 2)
-            qz(n - 1, 1)
-            nm(n - 1, 0)
-            red(n + 1, 1)
-            nb(n + 1, 1)
-            qttr(n + 2)
-            qk(n + 1, 3)
-            ex(n, 4)
-            cp(n, 0)
-            qz(n - 1, 2)
-            red(n + 1, 2)
-            nb(n + 1, 2)
+        KTCP = nc.vector.tensor_copy
+
+        for b in range(-1, B):
+            load(b + 2)
+            kttr(b + 1)
+            qk(b, 4)
+            ex(b, 0)
+            nm(b - 2, 3)
+            rc(b - 1, 0)
+            red(b, 3)
+            qttr(b + 1, 0)
+            pv(b - 1, 0)
+            qk(b, 5)
+            ex(b, 1)
+            ktcp(b + 1)
+            red(b, 4)
+            tr(b - 1, 3)
+            qk(b, 6)
+            ex(b, 2)
+            qtcp(b + 1, 0)
+            nm(b - 1, 0)
+            red(b, 5)
+            tr(b - 1, 4)
+            pv(b - 1, 1)
+            qk(b, 7)
+            ex(b, 3)
+            cp(b - 1, 3)
+            vqz(b)
+            red(b, 6)
+            qttr(b + 1, 1)
+            qk(b, 8)
+            ex(b, 4)
+            cp(b - 1, 4)
+            nm(b - 1, 1)
+            rc(b - 1, 1)
+            red(b, 7)
+            vrg(b + 1, 0)
+            tr(b, 0)
+            qk(b, 9)
+            ex(b, 5)
+            qtcp(b + 1, 1)
+            qz(b - 1, 1)
+            qz(b - 1, 2)
+            red(b, 8)
+            tr(b, 1)
+            pv(b - 1, 2)
+            qk(b, 10)
+            ex(b, 6)
+            cp(b, 0)
+            red(b, 9)
+            vrg(b + 1, 1)
+            tr(b, 2)
+            qk(b, 11)
+            ex(b, 7)
+            cp(b, 1)
+            nm(b - 1, 2)
+            red(b, 10)
+            pv(b - 1, 3)
+            qk(b, 12)
+            ex(b, 8)
+            cp(b, 2)
+            qz(b, 0)
+            red(b, 11)
+
+        L = B - 1
+        tr(L, 3)
+        pv(L, 0)
+        pv(L, 1)
+        cp(L, 3)
+        tr(L, 4)
+        cp(L, 4)
+        nm(L - 1, 3)
+        rc(L, 0)
+        nm(L, 0)
+        nm(L, 1)
+        qz(L, 1)
+        qz(L, 2)
+        rc(L, 1)
+        pv(L, 2)
+        pv(L, 3)
+        nm(L, 2)
+        nm(L, 3)

@@ -84,7 +84,7 @@ def tile_attend_t_kernel(tc, q, k, v, out):
             kb, qb, vb = lds[b]
             nc.sync.dma_start(out=kb[:], in_=k[b].rearrange("g (p t) d -> p g (t d)", t=PACK))
             for x in range(2):
-                nc.sync.dma_start(out=qb[HQ * x:HQ * (x + 1)].rearrange("i g m d -> i (g m) d"),
+                nc.sync.dma_start(out=qb[x:P:2].rearrange("i g m d -> i (g m) d"),
                                   in_=q[b, KVH * x:KVH * (x + 1)].rearrange("g (m i) d -> i (g m) d", i=HQ))
             nc.sync.dma_start(out=vb[:], in_=v[b].rearrange("g (p t) d -> p g (t d)", t=PACK))
 
@@ -109,16 +109,14 @@ def tile_attend_t_kernel(tc, q, k, v, out):
         make_identity(nc, ident[:])
         identf = const.tile([P, P], F32, name="identf")
         make_identity(nc, identf[:])
-        m32 = const.tile([P, P], F32, name="m32")
+        m32 = const.tile([P, HQ], F32, name="m32")
         nc.gpsimd.memset(m32[:], 0.0)
         nc.gpsimd.affine_select(
             out=m32[:], in_=m32[:], compare_op=ALU.is_ge, fill=NEG, base=0,
-            pattern=[[-1, P]], channel_multiplier=1,
+            pattern=[[-2, PACK], [-2 * PACK, SL]], channel_multiplier=1,
         )
         maskb = const.tile([P, PACK, SL], BF16, name="maskb")
-        for x in range(2):
-            rows = slice(HQ * x, HQ * (x + 1))
-            nc.vector.tensor_copy(out=maskb[rows], in_=m32[rows, HQ * x:HQ * (x + 1)].rearrange("i (p t) -> i t p", t=PACK))
+        nc.vector.tensor_copy(out=maskb[:].rearrange("i t p -> i (t p)"), in_=m32[:])
 
         def move(dst, src):
             nc.sync.dma_start(out=dst.bitcast(I32), in_=src.bitcast(I32))
@@ -324,7 +322,7 @@ def tile_attend_t_kernel(tc, q, k, v, out):
                 for x in range(2):
                     dst = out[b, KVH * x:KVH * (x + 1)].rearrange("g (m i) d -> i (g m) d", i=HQ)
                     nc.sync.dma_start(out=dst[:, par:KVH * NM:2, :],
-                                      in_=ob[HQ * x:HQ * (x + 1)].rearrange("i g a d -> i (g a) d"))
+                                      in_=ob[x:P:2].rearrange("i g a d -> i (g a) d"))
 
         KTCP = nc.vector.tensor_copy
 

@@ -136,7 +136,7 @@ def tile_attend_t_kernel(tc, q, k, v, out):
             tk = ps.tile([P, KVH, PACK, P], BF16, tag=ttag(), name="tk")
             for g in range(KVH):
                 for t in range(PACK):
-                    nc.tensor.transpose(tk[:, g, t, :], lds[b][0][:, g, t * D:(t + 1) * D], ident[:])
+                    nc.tensor.matmul(out=tk[:, g, t, :], lhsT=lds[b][0][:, g, t * D:(t + 1) * D], rhs=ident[:], start=True, stop=True)
             st[("tk", b)] = tk
 
         def ktcp(b):
@@ -151,7 +151,7 @@ def tile_attend_t_kernel(tc, q, k, v, out):
                 return
             tq = ps.tile([P, NM, P], BF16, tag=ttag(), name="tq")
             for m in range(NM):
-                nc.tensor.transpose(tq[:, m, :], lds[b][1][:, g, m, :], ident[:])
+                nc.tensor.matmul(out=tq[:, m, :], lhsT=lds[b][1][:, g, m, :], rhs=ident[:], start=True, stop=True)
             st[("tq", b, g)] = tq
 
         def qtcp(b, g):
@@ -200,9 +200,11 @@ def tile_attend_t_kernel(tc, q, k, v, out):
         def norm(b, j):
             return b + j // NU, j % NU
 
-        def qk(b, j):
+        def qk(b, j, mid=None):
             b, j = norm(b, j)
             if not ok(b):
+                if mid is not None:
+                    mid()
                 return
             kt = st[("kt", b)]
             s = ps.tile([P, N], F32, tag="s%d" % ((NU * b + j) % NS), name="s")
@@ -213,7 +215,11 @@ def tile_attend_t_kernel(tc, q, k, v, out):
                 flat = s[:, off:off + PACK * w]
                 reg = flat.rearrange("i (t p) -> i t p", t=PACK)
                 nc.tensor.matmul(out=reg, lhsT=st[("qt", b, g)][:, m, :], rhs=kt[:, g, :, 0:w], start=True, stop=False)
+                if mid is not None and off == 0 and len(UNITS[j]) == 1:
+                    mid()
                 nc.tensor.matmul(out=reg[:, :, w - SL:w], lhsT=ident[:], rhs=maskb[:], start=False, stop=True)
+                if mid is not None and off == 0 and len(UNITS[j]) == 2:
+                    mid()
                 regs.append((w, flat, reg))
                 off += PACK * w
             st[("s", b, j)] = (s, regs)
@@ -347,8 +353,7 @@ def tile_attend_t_kernel(tc, q, k, v, out):
             nm(b - 1, 0)
             red(b, 5)
             tr(b - 1, 4)
-            pv(b - 1, 1)
-            qk(b, 7)
+            qk(b, 7, lambda: pv(b - 1, 1))
             ex(b, 3)
             cp(b - 1, 3)
             vqz(b)
@@ -369,8 +374,7 @@ def tile_attend_t_kernel(tc, q, k, v, out):
             qz(b - 1, 2)
             red(b, 8)
             tr(b, 1)
-            pv(b - 1, 2)
-            qk(b, 10)
+            qk(b, 10, lambda: pv(b - 1, 2))
             ex(b, 6)
             cp(b, 0)
             red(b, 9)

@@ -23,7 +23,7 @@ FLOPS = 4 * B * H * N * N * D
 HQ = 64
 NM = N // HQ
 SL = HQ // PACK
-NSETS = 2
+NSETS = 3
 
 UNITS = [[(0, 0), (0, 6)], [(0, 2), (0, 4)], [(1, 0), (1, 6)], [(1, 2), (1, 4)], [(0, 1), (0, 5)], [(0, 7)],
          [(1, 1), (1, 5)], [(1, 7)], [(0, 3), (1, 3)]]
@@ -58,7 +58,7 @@ def tile_attend_t_kernel(tc, q, k, v, out):
         gp = ctx.enter_context(tc.tile_pool(name="gp", bufs=2))
         cpl = ctx.enter_context(tc.tile_pool(name="cpl", bufs=2))
         small = ctx.enter_context(tc.tile_pool(name="small", bufs=4))
-        obp = ctx.enter_context(tc.tile_pool(name="obp", bufs=3))
+        obp = ctx.enter_context(tc.tile_pool(name="obp", bufs=4))
         ps = ctx.enter_context(tc.psum_pool(name="ps", bufs=1))
 
         st = {}
@@ -89,6 +89,7 @@ def tile_attend_t_kernel(tc, q, k, v, out):
             nc.sync.dma_start(out=vb[:], in_=v[b].rearrange("g (p t) d -> p g (t d)", t=PACK))
 
         load(0)
+        load(1)
 
         warm = const.tile([P, 2], F32, name="warm")
         nc.vector.memset(warm[:], 0.0)
@@ -332,8 +333,10 @@ def tile_attend_t_kernel(tc, q, k, v, out):
 
         KTCP = nc.vector.tensor_copy
 
+        vrg(0, 0)
+        vrg(0, 1)
         for b in range(-1, B):
-            load(b + 2)
+            load(b + 3)
             kttr(b + 1)
             qk(b, 4)
             ex(b, 0)
@@ -351,12 +354,13 @@ def tile_attend_t_kernel(tc, q, k, v, out):
             ex(b, 2)
             qtcp(b + 1, 0)
             nm(b - 1, 0)
+            if b < 0:
+                vqz(0)
             red(b, 5)
             tr(b - 1, 4)
             qk(b, 7, lambda: pv(b - 1, 1))
             ex(b, 3)
             cp(b - 1, 3)
-            vqz(b)
             red(b, 6)
             qttr(b + 1, 1)
             qk(b, 8)
@@ -365,7 +369,8 @@ def tile_attend_t_kernel(tc, q, k, v, out):
             nm(b - 1, 1)
             rc(b - 1, 1)
             red(b, 7)
-            vrg(b + 1, 0)
+            if b >= 0:
+                vrg(b + 1, 0)
             tr(b, 0)
             qk(b, 9)
             ex(b, 5)
@@ -378,7 +383,8 @@ def tile_attend_t_kernel(tc, q, k, v, out):
             ex(b, 6)
             cp(b, 0)
             red(b, 9)
-            vrg(b + 1, 1)
+            if b >= 0:
+                vrg(b + 1, 1)
             tr(b, 2)
             qk(b, 11)
             ex(b, 7)
@@ -390,21 +396,23 @@ def tile_attend_t_kernel(tc, q, k, v, out):
             ex(b, 8)
             cp(b, 2)
             qz(b, 0)
+            if b >= 0:
+                vqz(b + 1)
             red(b, 11)
 
         L = B - 1
         tr(L, 3)
+        tr(L, 4)
         pv(L, 0)
         pv(L, 1)
         cp(L, 3)
-        tr(L, 4)
         cp(L, 4)
         nm(L - 1, 3)
         rc(L, 0)
         nm(L, 0)
-        nm(L, 1)
         qz(L, 1)
         qz(L, 2)
+        nm(L, 1)
         rc(L, 1)
         pv(L, 2)
         pv(L, 3)

@@ -144,7 +144,8 @@ def tile_attend_t_kernel(tc, q, k, v, out):
             if not ok(b):
                 return
             kt = qtp.tile([P, KVH, PACK, P], BF16, name="kt")
-            KTCP(out=kt[:].rearrange("d g t p -> d (g t p)"), in_=st[("tk", b)][:].rearrange("d g t p -> d (g t p)"))
+            copy = nc.vector.tensor_copy if b % 2 == 0 else nc.scalar.copy
+            copy(out=kt[:].rearrange("d g t p -> d (g t p)"), in_=st[("tk", b)][:].rearrange("d g t p -> d (g t p)"))
             st[("kt", b)] = kt
 
         def qttr(b, g):
@@ -331,8 +332,6 @@ def tile_attend_t_kernel(tc, q, k, v, out):
                     nc.sync.dma_start(out=dst[:, par:KVH * NM:2, :],
                                       in_=ob[x:P:2].rearrange("i g a d -> i (g a) d"))
 
-        KTCP = nc.vector.tensor_copy
-
         vrg(0, 0)
         vrg(0, 1)
         for b in range(-1, B):
@@ -391,6 +390,8 @@ def tile_attend_t_kernel(tc, q, k, v, out):
             cp(b, 1)
             nm(b - 1, 2)
             red(b, 10)
+            if b == B - 1:
+                tr(b, 3)
             pv(b - 1, 3)
             qk(b, 12)
             ex(b, 8)
@@ -401,7 +402,6 @@ def tile_attend_t_kernel(tc, q, k, v, out):
             red(b, 11)
 
         L = B - 1
-        tr(L, 3)
         tr(L, 4)
         pv(L, 0)
         pv(L, 1)
@@ -409,9 +409,9 @@ def tile_attend_t_kernel(tc, q, k, v, out):
         cp(L, 4)
         nm(L - 1, 3)
         rc(L, 0)
-        nm(L, 0)
         qz(L, 1)
         qz(L, 2)
+        nm(L, 0)
         nm(L, 1)
         rc(L, 1)
         pv(L, 2)

@@ -23,7 +23,10 @@ FLOPS = 4 * B * H * N * N * D
 HQ = 64
 NM = N // HQ
 SL = HQ // PACK
-NSETS = 3
+NSETS = 2
+PB = 2
+CB = PB * 2 * D * 4
+VB = CB + PB * 2 * D
 
 UNITS = [[(0, 0), (0, 6)], [(0, 2), (0, 4)], [(1, 0), (1, 6)], [(1, 2), (1, 4)], [(0, 1), (0, 5)], [(0, 7)],
          [(1, 1), (1, 5)], [(1, 7)], [(0, 3), (1, 3)]]
@@ -71,25 +74,32 @@ def tile_attend_t_kernel(tc, q, k, v, out):
         def ok(b):
             return 0 <= b < B
 
-        lds = []
-        for b in range(B):
-            kb = const.tile([P, KVH, N], BF16, name="kb%d" % b)
-            qb = const.tile([P, KVH, NM, D], BF16, name="qb%d" % b)
-            vb = const.tile([P, KVH, N], BF16, name="vb%d" % b)
-            lds.append((kb, qb, vb))
+        kbs = [const.tile([P, PB, KVH, N], BF16, name="kb%d" % i) for i in range(B // PB)]
+        vbs = [const.tile([P, PB, KVH, N], BF16, name="vb%d" % i) for i in range(B // PB)]
+        qbs = [const.tile([P, KVH, NM, D], BF16, name="qb%d" % i) for i in range(B)]
 
-        def load(b):
-            if not ok(b):
-                return
-            kb, qb, vb = lds[b]
-            nc.sync.dma_start(out=kb[:], in_=k[b].rearrange("g (p t) d -> p g (t d)", t=PACK))
+        def load_q(b):
             for x in range(2):
-                nc.sync.dma_start(out=qb[x:P:2].rearrange("i g m d -> i (g m) d"),
+                nc.sync.dma_start(out=qbs[b][x:P:2].rearrange("i g m d -> i (g m) d"),
                                   in_=q[b, KVH * x:KVH * (x + 1)].rearrange("g (m i) d -> i (g m) d", i=HQ))
-            nc.sync.dma_start(out=vb[:], in_=v[b].rearrange("g (p t) d -> p g (t d)", t=PACK))
 
-        load(0)
-        load(1)
+        def load_kv(dst, src, b):
+            nc.sync.dma_start(out=dst[b // PB][:, b % PB], in_=src[b].rearrange("g (p t) d -> p g (t d)", t=PACK))
+
+        def load_pair(i):
+            if not 0 < i < B // PB:
+                return
+            nc.sync.dma_start(out=kbs[i][:].rearrange("p b g c -> p (b g) c"),
+                              in_=k[PB * i:PB * (i + 1)].rearrange("b g (p t) d -> p (b g) (t d)", t=PACK))
+            load_q(PB * i)
+            nc.sync.dma_start(out=vbs[i][:].rearrange("p b g c -> p (b g) c"),
+                              in_=v[PB * i:PB * (i + 1)].rearrange("b g (p t) d -> p (b g) (t d)", t=PACK))
+            load_q(PB * i + 1)
+
+        for b in range(PB):
+            load_kv(kbs, k, b)
+            load_q(b)
+            load_kv(vbs, v, b)
 
         warm = const.tile([P, 2], F32, name="warm")
         nc.vector.memset(warm[:], 0.0)
@@ -97,14 +107,13 @@ def tile_attend_t_kernel(tc, q, k, v, out):
 
         vsets = []
         for j in range(NSETS):
-            vc = const.tile([P, KVH, D], U32, name="vc%d" % j, align_bytes=64)
-            vsc = const.tile([P, KVH, D], U8, name="vsc%d" % j, align_bytes=64)
-            rcod = const.tile([P, NM, KVH, D], U32, name="rcod%d" % j, align_bytes=64)
-            rsca = const.tile([P, NM // 2, KVH, D], U8, name="rsca%d" % j, align_bytes=64)
-            nc.vector.memset(vsc[:].rearrange("p g d -> p (g d)").bitcast(I32), 0)
-            nc.vector.memset(rcod[:, 0:NM - 1].rearrange("p m g d -> p (m g d)").bitcast(I32), 0)
-            nc.vector.memset(rsca[:].rearrange("p m g d -> p (m g d)").bitcast(I32), 0)
-            vsets.append((vc, vsc, rcod, rsca))
+            vq = const.tile([P, VB], U8, name="vq%d" % j, align_bytes=64)
+            vsh = const.tile([P, NM // 2, VB], U8, name="vsh%d" % j, align_bytes=64)
+            vpl = const.tile([P, NM // 2, VB - CB], U8, name="vpl%d" % j, align_bytes=64)
+            nc.vector.memset(vq[:, CB:VB].bitcast(I32), 0)
+            nc.vector.memset(vsh[:].rearrange("p m c -> p (m c)").bitcast(I32), 0)
+            nc.vector.memset(vpl[:].rearrange("p m c -> p (m c)").bitcast(I32), 0)
+            vsets.append((vq, vsh, vpl))
 
         ident = const.tile([P, P], BF16, name="ident")
         make_identity(nc, ident[:])
@@ -137,7 +146,7 @@ def tile_attend_t_kernel(tc, q, k, v, out):
             tk = ps.tile([P, KVH, PACK, P], BF16, tag=ttag(), name="tk")
             for g in range(KVH):
                 for t in range(PACK):
-                    nc.tensor.matmul(out=tk[:, g, t, :], lhsT=lds[b][0][:, g, t * D:(t + 1) * D], rhs=ident[:], start=True, stop=True)
+                    nc.tensor.matmul(out=tk[:, g, t, :], lhsT=kbs[b // PB][:, b % PB, g, t * D:(t + 1) * D], rhs=ident[:], start=True, stop=True)
             st[("tk", b)] = tk
 
         def ktcp(b):
@@ -153,7 +162,7 @@ def tile_attend_t_kernel(tc, q, k, v, out):
                 return
             tq = ps.tile([P, NM, P], BF16, tag=ttag(), name="tq")
             for m in range(NM):
-                nc.tensor.matmul(out=tq[:, m, :], lhsT=lds[b][1][:, g, m, :], rhs=ident[:], start=True, stop=True)
+                nc.tensor.matmul(out=tq[:, m, :], lhsT=qbs[b][:, g, m, :], rhs=ident[:], start=True, stop=True)
             st[("tq", b, g)] = tq
 
         def qtcp(b, g):
@@ -166,35 +175,32 @@ def tile_attend_t_kernel(tc, q, k, v, out):
         def vrg(b, g):
             if not ok(b):
                 return
-            if g == 0:
-                vg = vgp.tile([P, KVH, D, PACK], BF16, name="vg", align_bytes=64)
-                st[("vg", b)] = vg
-            vg = st[("vg", b)]
-            nc.gpsimd.tensor_scalar(out=vg[:, g], in0=lds[b][2][:, g, :].rearrange("p (t d) -> p d t", t=PACK),
+            if b % PB == 0 and g == 0:
+                vg = vgp.tile([P, PB, KVH, D, PACK], BF16, name="vg", align_bytes=64)
+                st[("vg", b // PB)] = vg
+            vg = st[("vg", b // PB)]
+            nc.gpsimd.tensor_scalar(out=vg[:, b % PB, g], in0=vbs[b // PB][:, b % PB, g, :].rearrange("p (t d) -> p d t", t=PACK),
                                     scalar1=1.0, scalar2=0.0, op0=ALU.mult, op1=ALU.add)
 
-        def vqz(b):
-            if not ok(b):
+        def vqz(i):
+            if not 0 <= i < B // PB:
                 return
-            vc, vsc, rcod, rsca = vsets[b % NSETS]
-            nc.vector.quantize_mx(out=vc[:].rearrange("p g d -> p (g d)").bitcast(FP8X4),
-                                  scales=vsc[:].rearrange("p g d -> p (g d)"),
-                                  in_=st[("vg", b)][:].rearrange("p g d t -> p (g d t)"))
-            for m in range(NM - 1):
-                w = width(m)
-                sh = shift(m)
-                for gs in ((slice(0, KVH),) if m != 3 else (slice(0, 1), slice(1, 2))):
-                    s_ = sh if (m != 3 or gs.start == 0) else 0
-                    move(rcod[s_:s_ + w, m, gs, :], vc[0:w, gs, :])
-                    blk = 0
-                    while s_ > 0 and blk < w // 8:
-                        cnt = 1
-                        while (blk + cnt < w // 8 and plane_row(blk + cnt) == plane_row(blk) + cnt
-                               and plane_row(blk + cnt + s_ // 8) == plane_row(blk + s_ // 8) + cnt):
-                            cnt += 1
-                        s0, d0 = plane_row(blk), plane_row(blk + s_ // 8)
-                        move(rsca[d0:d0 + cnt, m, gs, :], vsc[s0:s0 + cnt, gs, :])
-                        blk += cnt
+            vq, vsh, vpl = vsets[i % NSETS]
+            nc.vector.quantize_mx(out=vq[:, 0:CB].bitcast(FP8X4), scales=vq[:, CB:VB],
+                                  in_=st[("vg", i)][:].rearrange("p b g d t -> p (b g d t)"))
+            move(vsh[112:128, 0, 0:CB], vq[0:16, 0:CB])
+            move(vsh[98:100, 0, CB:VB], vq[0:2, CB:VB])
+            move(vsh[96:128, 1], vq[0:32])
+            move(vsh[80:112, 2, 0:CB], vq[0:32, 0:CB])
+            move(vsh[112:128, 2, 0:CB], vq[32:48, 0:CB])
+            move(vsh[66:68, 2, CB:VB], vq[0:2, CB:VB])
+            move(vsh[96:98, 2, CB:VB], vq[2:4, CB:VB])
+            move(vsh[98:100, 2, CB:VB], vq[32:34, CB:VB])
+            move(vsh[64:128, 3], vq[0:64])
+            for lo, cnt, m0 in ((0, 64, 0), (64, 2, 1), (66, 2, 2), (96, 2, 3)):
+                rows = slice(lo, lo + cnt)
+                nc.sync.dma_start(out=vpl[rows, m0:NM // 2].bitcast(I32),
+                                  in_=vq[rows, CB:VB].bitcast(I32).unsqueeze(1).to_broadcast([cnt, NM // 2 - m0, (VB - CB) // 4]))
 
         def rcol(g, m):
             return 8 * (m % 2) + 4 * g + m // 2
@@ -294,7 +300,7 @@ def tile_attend_t_kernel(tc, q, k, v, out):
         def pv(b, oi):
             if not ok(b):
                 return
-            vc, vsc, rcod, rsca = vsets[b % NSETS]
+            vq, vsh, vpl = vsets[b // PB % NSETS]
             o = ps.tile([P, 4, D], F32, tag=("o" if b < B - 1 else "s%d" % oi), name="o")
             for j in OBANK[oi]:
                 cod, sca = st[("c", b, j)]
@@ -302,8 +308,14 @@ def tile_attend_t_kernel(tc, q, k, v, out):
                     if 2 * (m % 2) + g != oi:
                         continue
                     shifted = len(UNITS[j]) == 2 and i == 0
-                    rhs = vc[:, g, :] if m == NM - 1 else rcod[:, m, g, :]
-                    rsc = rsca[:, m, g, :] if shifted else vsc[:, g, :]
+                    i0 = (b % PB * KVH + g) * D
+                    rhs = vsh[:, m, PACK * i0:PACK * (i0 + D)] if shifted else vq[:, PACK * i0:PACK * (i0 + D)]
+                    if shifted:
+                        rsc = vsh[:, m, CB + i0:CB + i0 + D]
+                    elif m < NM - 1:
+                        rsc = vpl[:, m - 3, i0:i0 + D]
+                    else:
+                        rsc = vq[:, CB + i0:CB + i0 + D]
                     nc.tensor.matmul_mx(out=o[:, m // 2, :], lhsT=cod.bitcast(FP8X4), lhsT_scale=sca,
                                         rhs=rhs.bitcast(FP8X4), rhs_scale=rsc, start=True, stop=True)
             st[("o", b, oi)] = o
@@ -335,7 +347,7 @@ def tile_attend_t_kernel(tc, q, k, v, out):
         vrg(0, 0)
         vrg(0, 1)
         for b in range(-1, B):
-            load(b + 3)
+            load_pair(b + 2)
             kttr(b + 1)
             qk(b, 4)
             ex(b, 0)
@@ -353,8 +365,6 @@ def tile_attend_t_kernel(tc, q, k, v, out):
             ex(b, 2)
             qtcp(b + 1, 0)
             nm(b - 1, 0)
-            if b < 0:
-                vqz(0)
             red(b, 5)
             tr(b - 1, 4)
             qk(b, 7, lambda: pv(b - 1, 1))
@@ -368,8 +378,7 @@ def tile_attend_t_kernel(tc, q, k, v, out):
             nm(b - 1, 1)
             rc(b - 1, 1)
             red(b, 7)
-            if b >= 0:
-                vrg(b + 1, 0)
+            vrg(b + 2, 0)
             tr(b, 0)
             qk(b, 9)
             ex(b, 5)
@@ -382,8 +391,7 @@ def tile_attend_t_kernel(tc, q, k, v, out):
             ex(b, 6)
             cp(b, 0)
             red(b, 9)
-            if b >= 0:
-                vrg(b + 1, 1)
+            vrg(b + 2, 1)
             tr(b, 2)
             qk(b, 11)
             ex(b, 7)
@@ -397,8 +405,8 @@ def tile_attend_t_kernel(tc, q, k, v, out):
             ex(b, 8)
             cp(b, 2)
             qz(b, 0)
-            if b >= 0:
-                vqz(b + 1)
+            if b % PB == 1:
+                vqz((b + 1) // PB)
             red(b, 11)
 
         L = B - 1

@@ -36,6 +36,7 @@ GROUPS = [[0, 1], [2, 3], [4, 5], [6, 7], [8]]
 QGROUP = [[0, 1], [2, 3], [4]]
 OBANK = [[0, 1], [2, 3], [4, 5, 8], [6, 7, 8]]
 NS = 5
+OTAG = {(B - 2, 3): "s2", (B - 1, 0): "s3", (B - 1, 1): "s4", (B - 1, 2): "s0"}
 
 
 def width(m):
@@ -86,34 +87,57 @@ def tile_attend_t_kernel(tc, q, k, v, out):
         def load_kv(dst, src, b):
             nc.sync.dma_start(out=dst[b // PB][:, b % PB], in_=src[b].rearrange("g (p t) d -> p g (t d)", t=PACK))
 
-        def load_pair(i):
-            if not 0 < i < B // PB:
-                return
-            nc.sync.dma_start(out=kbs[i][:].rearrange("p b g c -> p (b g) c"),
-                              in_=k[PB * i:PB * (i + 1)].rearrange("b g (p t) d -> p (b g) (t d)", t=PACK))
-            load_q(PB * i)
-            nc.sync.dma_start(out=vbs[i][:].rearrange("p b g c -> p (b g) c"),
-                              in_=v[PB * i:PB * (i + 1)].rearrange("b g (p t) d -> p (b g) (t d)", t=PACK))
-            load_q(PB * i + 1)
+        def load_pair(dst, src, i):
+            nc.sync.dma_start(out=dst[i][:].rearrange("p b g c -> p (b g) c"),
+                              in_=src[PB * i:PB * (i + 1)].rearrange("b g (p t) d -> p (b g) (t d)", t=PACK))
 
-        for b in range(PB):
-            load_kv(kbs, k, b)
-            load_q(b)
-            load_kv(vbs, v, b)
+        def load_first(i):
+            if 0 < i < B // PB:
+                load_pair(kbs, k, i)
+                load_q(PB * i)
+                load_pair(vbs, v, i)
+
+        def load_rest(i):
+            if 0 < i < B // PB:
+                load_q(PB * i + 1)
+
+        for g in range(KVH):
+            nc.sync.dma_start(out=kbs[0][:, 0, g], in_=k[0, g].rearrange("(p t) d -> p (t d)", t=PACK))
+            for x in range(2):
+                nc.sync.dma_start(out=qbs[0][x:P:2, g], in_=q[0, KVH * x + g].rearrange("(m i) d -> i m d", i=HQ))
+        load_kv(kbs, k, 1)
+        load_kv(vbs, v, 0)
+        load_q(1)
+        load_kv(vbs, v, 1)
+        load_first(1)
 
         warm = const.tile([P, 2], F32, name="warm")
         nc.vector.memset(warm[:], 0.0)
         nc.scalar.activation(out=warm[:, 1:2], in_=warm[:, 0:1], func=ACT.Exp)
+
+        zero = const.tile([P, N], BF16, name="zero")
+        nc.vector.memset(zero[:], 0.0)
+        for i in range(4):
+            dummy = ps.tile([P, N], F32, tag="s%d" % i, name="dummy")
+            nc.tensor.matmul(out=dummy[:], lhsT=zero[:, 0:P], rhs=zero[:], start=True, stop=True)
 
         vsets = []
         for j in range(NSETS):
             vq = const.tile([P, VB], U8, name="vq%d" % j, align_bytes=64)
             vsh = const.tile([P, NM // 2, VB], U8, name="vsh%d" % j, align_bytes=64)
             vpl = const.tile([P, NM // 2, VB - CB], U8, name="vpl%d" % j, align_bytes=64)
-            nc.vector.memset(vq[:, CB:VB].bitcast(I32), 0)
-            nc.vector.memset(vsh[:].rearrange("p m c -> p (m c)").bitcast(I32), 0)
-            nc.vector.memset(vpl[:].rearrange("p m c -> p (m c)").bitcast(I32), 0)
             vsets.append((vq, vsh, vpl))
+
+        def clear(j, part, memset, dt, value):
+            vq, vsh, vpl = vsets[j]
+            if part < NM // 2:
+                memset(vsh[:, part].bitcast(dt), value)
+            else:
+                memset(vq[:, CB:VB].bitcast(dt), value)
+                memset(vpl[:].rearrange("p m c -> p (m c)").bitcast(dt), value)
+
+        for part in range(NM // 2 + 1):
+            clear(0, part, nc.vector.memset, I32, 0)
 
         ident = const.tile([P, P], BF16, name="ident")
         make_identity(nc, ident[:])
@@ -140,37 +164,41 @@ def tile_attend_t_kernel(tc, q, k, v, out):
                 st[("sm", b)] = (mx, nbt, rs, rinv)
             return st[("sm", b)]
 
-        def kttr(b):
+        def kttr(b, gs=(0, 1)):
             if not ok(b):
                 return
             tk = ps.tile([P, KVH, PACK, P], BF16, tag=ttag(), name="tk")
-            for g in range(KVH):
+            for g in gs:
                 for t in range(PACK):
                     nc.tensor.matmul(out=tk[:, g, t, :], lhsT=kbs[b // PB][:, b % PB, g, t * D:(t + 1) * D], rhs=ident[:], start=True, stop=True)
             st[("tk", b)] = tk
 
-        def ktcp(b):
+        def ktcp(b, gs=(0, 1)):
             if not ok(b):
                 return
-            kt = qtp.tile([P, KVH, PACK, P], BF16, name="kt")
+            if gs[0] == 0:
+                kt = qtp.tile([P, KVH, PACK, P], BF16, name="kt")
+                st[("kt", b)] = kt
+            kt = st[("kt", b)]
             copy = nc.vector.tensor_copy if b % 2 == 0 else nc.scalar.copy
-            copy(out=kt[:].rearrange("d g t p -> d (g t p)"), in_=st[("tk", b)][:].rearrange("d g t p -> d (g t p)"))
-            st[("kt", b)] = kt
+            ends = slice(gs[0], gs[-1] + 1)
+            copy(out=kt[:, ends].rearrange("d g t p -> d (g t p)"), in_=st[("tk", b)][:, ends].rearrange("d g t p -> d (g t p)"))
 
-        def qttr(b, g):
+        def qttr(b, g, ms=slice(0, NM), tag=None):
             if not ok(b):
                 return
-            tq = ps.tile([P, NM, P], BF16, tag=ttag(), name="tq")
-            for m in range(NM):
+            tq = ps.tile([P, NM, P], BF16, tag=tag or ttag(), name="tq")
+            for m in range(ms.start, ms.stop, ms.step or 1):
                 nc.tensor.matmul(out=tq[:, m, :], lhsT=qbs[b][:, g, m, :], rhs=ident[:], start=True, stop=True)
-            st[("tq", b, g)] = tq
+            st[("tq", b, g, ms.start)] = tq
 
-        def qtcp(b, g):
+        def qtcp(b, g, ms=slice(0, NM)):
             if not ok(b):
                 return
-            qt = qtp.tile([P, NM, P], BF16, name="qt%d" % g)
-            nc.scalar.copy(out=qt[:].rearrange("d m i -> d (m i)"), in_=st[("tq", b, g)][:].rearrange("d m i -> d (m i)"))
-            st[("qt", b, g)] = qt
+            if ms.start == 0:
+                qt = qtp.tile([P, NM, P], BF16, name="qt%d" % g)
+                st[("qt", b, g)] = qt
+            nc.scalar.copy(out=st[("qt", b, g)][:, ms], in_=st[("tq", b, g, ms.start)][:, ms])
 
         def vrg(b, g):
             if not ok(b):
@@ -301,7 +329,7 @@ def tile_attend_t_kernel(tc, q, k, v, out):
             if not ok(b):
                 return
             vq, vsh, vpl = vsets[b // PB % NSETS]
-            o = ps.tile([P, 4, D], F32, tag=("o" if b < B - 1 else "s%d" % oi), name="o")
+            o = ps.tile([P, 4, D], F32, tag=OTAG.get((b, oi), "o"), name="o")
             for j in OBANK[oi]:
                 cod, sca = st[("c", b, j)]
                 for i, (g, m) in enumerate(UNITS[j]):
@@ -336,41 +364,79 @@ def tile_attend_t_kernel(tc, q, k, v, out):
                 ob = obp.tile([P, KVH, 4, D], F32, name="ob")
                 st[("ob", b, par)] = ob
             ob = st[("ob", b, par)]
-            nc.vector.tensor_tensor(out=ob[:, g], in0=o[:],
-                                    in1=rinv[:, 4 * oi:4 * oi + 4].unsqueeze(2).to_broadcast([P, 4, D]), op=ALU.mult)
-            if g == KVH - 1:
+            if (b, oi) == (B - 1, 3):
+                for a in range(4):
+                    nc.scalar.activation(out=ob[:, g, a], in_=o[:, a], func=ACT.Copy, scale=rinv[:, 4 * oi + a:4 * oi + a + 1])
+            else:
+                nc.vector.tensor_tensor(out=ob[:, g], in0=o[:],
+                                        in1=rinv[:, 4 * oi:4 * oi + 4].unsqueeze(2).to_broadcast([P, 4, D]), op=ALU.mult)
+            if b == B - 1 or (b, par) == (B - 2, 1):
+                for x in range(2):
+                    nc.sync.dma_start(out=out[b, KVH * x + g].rearrange("(m i) d -> i m d", i=HQ)[:, par:NM:2, :], in_=ob[x:P:2, g])
+            elif g == KVH - 1:
                 for x in range(2):
                     dst = out[b, KVH * x:KVH * (x + 1)].rearrange("g (m i) d -> i (g m) d", i=HQ)
                     nc.sync.dma_start(out=dst[:, par:KVH * NM:2, :],
                                       in_=ob[x:P:2].rearrange("i g a d -> i (g a) d"))
 
+        kttr(0, (0,))
+        ktcp(0, (0,))
+        HEAD = (slice(0, 7, 6), slice(2, 5, 2), slice(1, 8, 2))
+        for ms, tag in zip(HEAD, ("s2", "s3", "s4")):
+            qttr(0, 0, ms, tag)
+            qtcp(0, 0, ms)
+        kttr(0, (1,))
+        qk(0, 0)
+        qk(0, 1)
+        ktcp(0, (1,))
+        red(0, 0)
+        qttr(0, 1)
+        qtcp(0, 1)
+        red(0, 1)
         vrg(0, 0)
+        qk(0, 2)
+        qk(0, 3)
+        red(0, 2)
         vrg(0, 1)
-        for b in range(-1, B):
-            load_pair(b + 2)
+
+        for b in range(B - 1):
+            if b % PB == 1:
+                load_first((b + 3) // PB)
+                load_rest((b + 3) // PB)
             kttr(b + 1)
             qk(b, 4)
             ex(b, 0)
             nm(b - 2, 3)
             rc(b - 1, 0)
             red(b, 3)
+            if b == 0:
+                vrg(1, 0)
             qttr(b + 1, 0)
             pv(b - 1, 0)
             qk(b, 5)
             ex(b, 1)
             ktcp(b + 1)
             red(b, 4)
+            if b == 0:
+                vrg(1, 1)
             tr(b - 1, 3)
             qk(b, 6)
             ex(b, 2)
             qtcp(b + 1, 0)
             nm(b - 1, 0)
             red(b, 5)
+            if b == 0:
+                vqz(0)
+                load_rest(1)
+            if b == 0:
+                clear(1, 4, nc.gpsimd.memset, F32, 0.0)
             tr(b - 1, 4)
             qk(b, 7, lambda: pv(b - 1, 1))
             ex(b, 3)
             cp(b - 1, 3)
             red(b, 6)
+            if b == 0:
+                clear(1, 0, nc.gpsimd.memset, F32, 0.0)
             qttr(b + 1, 1)
             qk(b, 8)
             ex(b, 4)
@@ -386,6 +452,8 @@ def tile_attend_t_kernel(tc, q, k, v, out):
             qz(b - 1, 1)
             qz(b - 1, 2)
             red(b, 8)
+            if b == 0:
+                clear(1, 1, nc.gpsimd.memset, F32, 0.0)
             tr(b, 1)
             qk(b, 10, lambda: pv(b - 1, 2))
             ex(b, 6)
@@ -398,8 +466,8 @@ def tile_attend_t_kernel(tc, q, k, v, out):
             cp(b, 1)
             nm(b - 1, 2)
             red(b, 10)
-            if b == B - 1:
-                tr(b, 3)
+            if b == 0:
+                clear(1, 2, nc.gpsimd.memset, F32, 0.0)
             pv(b - 1, 3)
             qk(b, 12)
             ex(b, 8)
@@ -408,20 +476,66 @@ def tile_attend_t_kernel(tc, q, k, v, out):
             if b % PB == 1:
                 vqz((b + 1) // PB)
             red(b, 11)
+            if b == 0:
+                clear(1, 3, nc.gpsimd.memset, F32, 0.0)
 
         L = B - 1
-        tr(L, 4)
+        M = B - 2
+        qk(L, 4)
+        ex(L, 0)
+        nm(M - 1, 3)
+        rc(M, 0)
+        red(L, 3)
+        pv(M, 0)
+        tr(M, 3)
+        qk(L, 5)
+        ex(L, 1)
+        cp(M, 3)
+        red(L, 4)
+        nm(M, 0)
+        tr(M, 4)
+        qk(L, 6)
+        ex(L, 2)
+        cp(M, 4)
+        red(L, 5)
+        rc(M, 1)
+        tr(L, 0)
+        qk(L, 7, lambda: pv(M, 1))
+        ex(L, 3)
+        qz(M, 1)
+        red(L, 6)
+        nm(M, 1)
+        qk(L, 8)
+        ex(L, 4)
+        cp(L, 0)
+        qz(M, 2)
+        red(L, 7)
+        tr(L, 1)
+        pv(M, 2)
+        ex(L, 5)
+        cp(L, 1)
+        red(L, 8)
+        nm(M, 2)
+        pv(M, 3)
+        tr(L, 2)
+        ex(L, 6)
+        cp(L, 2)
+        qz(L, 0)
+        nm(M, 3)
         pv(L, 0)
         pv(L, 1)
-        cp(L, 3)
-        cp(L, 4)
-        nm(L - 1, 3)
+        ex(L, 7)
         rc(L, 0)
-        qz(L, 1)
-        qz(L, 2)
         nm(L, 0)
+        tr(L, 3)
+        ex(L, 8)
+        cp(L, 3)
         nm(L, 1)
+        tr(L, 4)
+        cp(L, 4)
+        qz(L, 1)
         rc(L, 1)
+        qz(L, 2)
         pv(L, 2)
         pv(L, 3)
         nm(L, 2)

@@ -22,6 +22,7 @@ NEG = -1.0e30
 FLOPS = 4 * B * H * N * N * D
 HQ = 64
 NM = N // HQ
+QROW = N // HQ
 SL = HQ // PACK
 NSETS = 2
 PB = 2
@@ -77,12 +78,11 @@ def tile_attend_t_kernel(tc, q, k, v, out):
 
         kbs = [const.tile([P, PB, KVH, N], BF16, name="kb%d" % i) for i in range(B // PB)]
         vbs = [const.tile([P, PB, KVH, N], BF16, name="vb%d" % i) for i in range(B // PB)]
-        qbs = [const.tile([P, KVH, NM, D], BF16, name="qb%d" % i) for i in range(B)]
+        qbs = [const.tile([P, KVH, QROW * D], BF16, name="qb%d" % i) for i in range(B)]
 
         def load_q(b):
             for x in range(2):
-                nc.sync.dma_start(out=qbs[b][x:P:2].rearrange("i g m d -> i (g m) d"),
-                                  in_=q[b, KVH * x:KVH * (x + 1)].rearrange("g (m i) d -> i (g m) d", i=HQ))
+                nc.sync.dma_start(out=qbs[b][x:P:2], in_=q[b, KVH * x:KVH * (x + 1)].rearrange("g (p t) d -> p g (t d)", t=QROW))
 
         def load_kv(dst, src, b):
             nc.sync.dma_start(out=dst[b // PB][:, b % PB], in_=src[b].rearrange("g (p t) d -> p g (t d)", t=PACK))
@@ -104,7 +104,7 @@ def tile_attend_t_kernel(tc, q, k, v, out):
         for g in range(KVH):
             nc.sync.dma_start(out=kbs[0][:, 0, g], in_=k[0, g].rearrange("(p t) d -> p (t d)", t=PACK))
             for x in range(2):
-                nc.sync.dma_start(out=qbs[0][x:P:2, g], in_=q[0, KVH * x + g].rearrange("(m i) d -> i m d", i=HQ))
+                nc.sync.dma_start(out=qbs[0][x:P:2, g], in_=q[0, KVH * x + g].rearrange("(p t) d -> p (t d)", t=QROW))
         load_kv(kbs, k, 1)
         load_kv(vbs, v, 0)
         load_q(1)
@@ -184,13 +184,15 @@ def tile_attend_t_kernel(tc, q, k, v, out):
             ends = slice(gs[0], gs[-1] + 1)
             copy(out=kt[:, ends].rearrange("d g t p -> d (g t p)"), in_=st[("tk", b)][:, ends].rearrange("d g t p -> d (g t p)"))
 
-        def qttr(b, g, ms=slice(0, NM), tag=None):
+        def qttr(b, g):
             if not ok(b):
                 return
-            tq = ps.tile([P, NM, P], BF16, tag=tag or ttag(), name="tq")
-            for m in range(ms.start, ms.stop, ms.step or 1):
-                nc.tensor.matmul(out=tq[:, m, :], lhsT=qbs[b][:, g, m, :], rhs=ident[:], start=True, stop=True)
-            st[("tq", b, g, ms.start)] = tq
+            tq = ps.tile([P, NM, P], BF16, tag=ttag(), name="tq")
+            cols = tq[:].rearrange("d m (j t x) -> d (m j) t x", t=QROW, x=2)
+            for t in range(QROW):
+                nc.tensor.matmul(out=cols[:, :, t, :], lhsT=qbs[b][:, g, t * D:(t + 1) * D],
+                                 rhs=ident[:].rearrange("p (i x) -> p i x", x=2), start=True, stop=True)
+            st[("tq", b, g)] = tq
 
         def qtcp(b, g, ms=slice(0, NM)):
             if not ok(b):
@@ -198,7 +200,7 @@ def tile_attend_t_kernel(tc, q, k, v, out):
             if ms.start == 0:
                 qt = qtp.tile([P, NM, P], BF16, name="qt%d" % g)
                 st[("qt", b, g)] = qt
-            nc.scalar.copy(out=st[("qt", b, g)][:, ms], in_=st[("tq", b, g, ms.start)][:, ms])
+            nc.scalar.copy(out=st[("qt", b, g)][:, ms], in_=st[("tq", b, g)][:, ms])
 
         def vrg(b, g):
             if not ok(b):
@@ -382,8 +384,8 @@ def tile_attend_t_kernel(tc, q, k, v, out):
         kttr(0, (0,))
         ktcp(0, (0,))
         HEAD = (slice(0, 7, 6), slice(2, 5, 2), slice(1, 8, 2))
-        for ms, tag in zip(HEAD, ("s2", "s3", "s4")):
-            qttr(0, 0, ms, tag)
+        qttr(0, 0)
+        for ms in HEAD:
             qtcp(0, 0, ms)
         kttr(0, (1,))
         qk(0, 0)

@@ -37,7 +37,7 @@ GROUPS = [[0, 1], [2, 3], [4, 5], [6, 7], [8]]
 QGROUP = [[0, 1], [2, 3], [4]]
 OBANK = [[0, 1], [2, 3], [4, 5, 8], [6, 7, 8]]
 NS = 5
-OTAG = {(B - 2, 3): "s2", (B - 1, 0): "s3", (B - 1, 1): "s4", (B - 1, 2): "s0"}
+OTAG = {(B - 1, 0): "s2", (B - 1, 1): "s3", (B - 1, 2): "s4", (B - 1, 3): "s0"}
 
 
 def width(m):
@@ -128,16 +128,13 @@ def tile_attend_t_kernel(tc, q, k, v, out):
             vpl = const.tile([P, NM // 2, VB - CB], U8, name="vpl%d" % j, align_bytes=64)
             vsets.append((vq, vsh, vpl))
 
-        def clear(j, part, memset, dt, value):
-            vq, vsh, vpl = vsets[j]
-            if part < NM // 2:
-                memset(vsh[:, part].bitcast(dt), value)
-            else:
-                memset(vq[:, CB:VB].bitcast(dt), value)
-                memset(vpl[:].rearrange("p m c -> p (m c)").bitcast(dt), value)
+        def clear(tile):
+            nc.vector.memset(tile.bitcast(I32), 0)
 
-        for part in range(NM // 2 + 1):
-            clear(0, part, nc.vector.memset, I32, 0)
+        for vq, vsh, vpl in vsets:
+            clear(vq[:, CB:VB])
+            clear(vsh[:].rearrange("p m c -> p (m c)"))
+            clear(vpl[:].rearrange("p m c -> p (m c)"))
 
         ident = const.tile([P, P], BF16, name="ident")
         make_identity(nc, ident[:])
@@ -401,7 +398,7 @@ def tile_attend_t_kernel(tc, q, k, v, out):
         red(0, 2)
         vrg(0, 1)
 
-        for b in range(B - 1):
+        for b in range(B):
             if b % PB == 1:
                 load_first((b + 3) // PB)
                 load_rest((b + 3) // PB)
@@ -411,16 +408,12 @@ def tile_attend_t_kernel(tc, q, k, v, out):
             nm(b - 2, 3)
             rc(b - 1, 0)
             red(b, 3)
-            if b == 0:
-                vrg(1, 0)
             qttr(b + 1, 0)
             pv(b - 1, 0)
             qk(b, 5)
             ex(b, 1)
             ktcp(b + 1)
             red(b, 4)
-            if b == 0:
-                vrg(1, 1)
             tr(b - 1, 3)
             qk(b, 6)
             ex(b, 2)
@@ -428,17 +421,14 @@ def tile_attend_t_kernel(tc, q, k, v, out):
             nm(b - 1, 0)
             red(b, 5)
             if b == 0:
-                vqz(0)
-                load_rest(1)
-            if b == 0:
-                clear(1, 4, nc.gpsimd.memset, F32, 0.0)
+                vrg(1, 0)
             tr(b - 1, 4)
             qk(b, 7, lambda: pv(b - 1, 1))
             ex(b, 3)
             cp(b - 1, 3)
             red(b, 6)
             if b == 0:
-                clear(1, 0, nc.gpsimd.memset, F32, 0.0)
+                vrg(1, 1)
             qttr(b + 1, 1)
             qk(b, 8)
             ex(b, 4)
@@ -446,7 +436,11 @@ def tile_attend_t_kernel(tc, q, k, v, out):
             nm(b - 1, 1)
             rc(b - 1, 1)
             red(b, 7)
-            vrg(b + 2, 0)
+            if b == 0:
+                vqz(0)
+                load_rest(1)
+            if b > 0:
+                vrg(b + 2, 0)
             tr(b, 0)
             qk(b, 9)
             ex(b, 5)
@@ -454,22 +448,20 @@ def tile_attend_t_kernel(tc, q, k, v, out):
             qz(b - 1, 1)
             qz(b - 1, 2)
             red(b, 8)
-            if b == 0:
-                clear(1, 1, nc.gpsimd.memset, F32, 0.0)
             tr(b, 1)
             qk(b, 10, lambda: pv(b - 1, 2))
             ex(b, 6)
             cp(b, 0)
             red(b, 9)
-            vrg(b + 2, 1)
+            vrg(b + 2, 0 if b == 0 else 1)
             tr(b, 2)
             qk(b, 11)
             ex(b, 7)
             cp(b, 1)
             nm(b - 1, 2)
             red(b, 10)
-            if b == 0:
-                clear(1, 2, nc.gpsimd.memset, F32, 0.0)
+            if b == B - 1:
+                tr(b, 3)
             pv(b - 1, 3)
             qk(b, 12)
             ex(b, 8)
@@ -479,65 +471,21 @@ def tile_attend_t_kernel(tc, q, k, v, out):
                 vqz((b + 1) // PB)
             red(b, 11)
             if b == 0:
-                clear(1, 3, nc.gpsimd.memset, F32, 0.0)
+                vrg(2, 1)
 
         L = B - 1
-        M = B - 2
-        qk(L, 4)
-        ex(L, 0)
-        nm(M - 1, 3)
-        rc(M, 0)
-        red(L, 3)
-        pv(M, 0)
-        tr(M, 3)
-        qk(L, 5)
-        ex(L, 1)
-        cp(M, 3)
-        red(L, 4)
-        nm(M, 0)
-        tr(M, 4)
-        qk(L, 6)
-        ex(L, 2)
-        cp(M, 4)
-        red(L, 5)
-        rc(M, 1)
-        tr(L, 0)
-        qk(L, 7, lambda: pv(M, 1))
-        ex(L, 3)
-        qz(M, 1)
-        red(L, 6)
-        nm(M, 1)
-        qk(L, 8)
-        ex(L, 4)
-        cp(L, 0)
-        qz(M, 2)
-        red(L, 7)
-        tr(L, 1)
-        pv(M, 2)
-        ex(L, 5)
-        cp(L, 1)
-        red(L, 8)
-        nm(M, 2)
-        pv(M, 3)
-        tr(L, 2)
-        ex(L, 6)
-        cp(L, 2)
-        qz(L, 0)
-        nm(M, 3)
+        tr(L, 4)
         pv(L, 0)
         pv(L, 1)
-        ex(L, 7)
-        rc(L, 0)
-        nm(L, 0)
-        tr(L, 3)
-        ex(L, 8)
         cp(L, 3)
-        nm(L, 1)
-        tr(L, 4)
         cp(L, 4)
+        nm(L - 1, 3)
+        rc(L, 0)
         qz(L, 1)
-        rc(L, 1)
         qz(L, 2)
+        nm(L, 0)
+        nm(L, 1)
+        rc(L, 1)
         pv(L, 2)
         pv(L, 3)
         nm(L, 2)

@@ -36,8 +36,6 @@ UCOL = [0, 2, 4, 6, 8, 10, 11, 13, 14]
 GROUPS = [[0, 1], [2, 3], [4, 5], [6, 7], [8]]
 QGROUP = [[0, 1], [2, 3], [4]]
 OBANK = [[0, 1], [2, 3], [4, 5, 8], [6, 7, 8]]
-NS = 5
-OTAG = {(B - 1, 0): "s2", (B - 1, 1): "s3", (B - 1, 2): "s4", (B - 1, 3): "s0"}
 
 
 def width(m):
@@ -67,11 +65,18 @@ def tile_attend_t_kernel(tc, q, k, v, out):
         ps = ctx.enter_context(tc.psum_pool(name="ps", bufs=1))
 
         st = {}
-        turns = []
+        free = ["b%d" % i for i in range(8)]
 
-        def ttag():
-            turns.append(0)
-            return "t%d" % (len(turns) % 2)
+        def take(key, shape, dt):
+            tag = free[0]
+            free.remove(tag)
+            tile = ps.tile(shape, dt, tag=tag, name="bank")
+            st[key] = tile
+            st[("tag", key)] = tag
+            return tile
+
+        def give(key):
+            free.append(st[("tag", key)])
 
         def ok(b):
             return 0 <= b < B
@@ -118,8 +123,9 @@ def tile_attend_t_kernel(tc, q, k, v, out):
         zero = const.tile([P, N], BF16, name="zero")
         nc.vector.memset(zero[:], 0.0)
         for i in range(4):
-            dummy = ps.tile([P, N], F32, tag="s%d" % i, name="dummy")
+            dummy = take("dummy", [P, N], F32)
             nc.tensor.matmul(out=dummy[:], lhsT=zero[:, 0:P], rhs=zero[:], start=True, stop=True)
+            give("dummy")
 
         vsets = []
         for j in range(NSETS):
@@ -131,10 +137,9 @@ def tile_attend_t_kernel(tc, q, k, v, out):
         def clear(tile):
             nc.vector.memset(tile.bitcast(I32), 0)
 
-        for vq, vsh, vpl in vsets:
-            clear(vq[:, CB:VB])
-            clear(vsh[:].rearrange("p m c -> p (m c)"))
-            clear(vpl[:].rearrange("p m c -> p (m c)"))
+        clear(vsets[0][0][:, CB:VB])
+        clear(vsets[0][1][:].rearrange("p m c -> p (m c)"))
+        clear(vsets[0][2][:].rearrange("p m c -> p (m c)"))
 
         ident = const.tile([P, P], BF16, name="ident")
         make_identity(nc, ident[:])
@@ -164,11 +169,10 @@ def tile_attend_t_kernel(tc, q, k, v, out):
         def kttr(b, gs=(0, 1)):
             if not ok(b):
                 return
-            tk = ps.tile([P, KVH, PACK, P], BF16, tag=ttag(), name="tk")
+            tk = take(("tk", b, gs[0]), [P, KVH, PACK, P], BF16)
             for g in gs:
                 for t in range(PACK):
                     nc.tensor.matmul(out=tk[:, g, t, :], lhsT=kbs[b // PB][:, b % PB, g, t * D:(t + 1) * D], rhs=ident[:], start=True, stop=True)
-            st[("tk", b)] = tk
 
         def ktcp(b, gs=(0, 1)):
             if not ok(b):
@@ -179,25 +183,27 @@ def tile_attend_t_kernel(tc, q, k, v, out):
             kt = st[("kt", b)]
             copy = nc.vector.tensor_copy if b % 2 == 0 else nc.scalar.copy
             ends = slice(gs[0], gs[-1] + 1)
-            copy(out=kt[:, ends].rearrange("d g t p -> d (g t p)"), in_=st[("tk", b)][:, ends].rearrange("d g t p -> d (g t p)"))
+            copy(out=kt[:, ends].rearrange("d g t p -> d (g t p)"), in_=st[("tk", b, gs[0])][:, ends].rearrange("d g t p -> d (g t p)"))
+            give(("tk", b, gs[0]))
 
         def qttr(b, g):
             if not ok(b):
                 return
-            tq = ps.tile([P, NM, P], BF16, tag=ttag(), name="tq")
+            tq = take(("tq", b, g), [P, NM, P], BF16)
             cols = tq[:].rearrange("d m (j t x) -> d (m j) t x", t=QROW, x=2)
             for t in range(QROW):
                 nc.tensor.matmul(out=cols[:, :, t, :], lhsT=qbs[b][:, g, t * D:(t + 1) * D],
                                  rhs=ident[:].rearrange("p (i x) -> p i x", x=2), start=True, stop=True)
-            st[("tq", b, g)] = tq
 
-        def qtcp(b, g, ms=slice(0, NM)):
+        def qtcp(b, g, ms=slice(0, NM), last=True):
             if not ok(b):
                 return
             if ms.start == 0:
                 qt = qtp.tile([P, NM, P], BF16, name="qt%d" % g)
                 st[("qt", b, g)] = qt
             nc.scalar.copy(out=st[("qt", b, g)][:, ms], in_=st[("tq", b, g)][:, ms])
+            if last:
+                give(("tq", b, g))
 
         def vrg(b, g):
             if not ok(b):
@@ -206,8 +212,11 @@ def tile_attend_t_kernel(tc, q, k, v, out):
                 vg = vgp.tile([P, PB, KVH, D, PACK], BF16, name="vg", align_bytes=64)
                 st[("vg", b // PB)] = vg
             vg = st[("vg", b // PB)]
-            nc.gpsimd.tensor_scalar(out=vg[:, b % PB, g], in0=vbs[b // PB][:, b % PB, g, :].rearrange("p (t d) -> p d t", t=PACK),
-                                    scalar1=1.0, scalar2=0.0, op0=ALU.mult, op1=ALU.add)
+            src = vbs[b // PB][:, b % PB, g, :].rearrange("p (t d) -> p d t", t=PACK)
+            if b < PB:
+                nc.vector.tensor_copy(out=vg[:, b % PB, g], in_=src)
+            else:
+                nc.gpsimd.tensor_scalar(out=vg[:, b % PB, g], in0=src, scalar1=1.0, scalar2=0.0, op0=ALU.mult, op1=ALU.add)
 
         def vqz(i):
             if not 0 <= i < B // PB:
@@ -242,7 +251,7 @@ def tile_attend_t_kernel(tc, q, k, v, out):
                     mid()
                 return
             kt = st[("kt", b)]
-            s = ps.tile([P, N], F32, tag="s%d" % ((NU * b + j) % NS), name="s")
+            s = take(("s", b, j), [P, N], F32)
             regs = []
             off = 0
             for (g, m) in UNITS[j]:
@@ -257,14 +266,14 @@ def tile_attend_t_kernel(tc, q, k, v, out):
                     mid()
                 regs.append((w, flat, reg))
                 off += PACK * w
-            st[("s", b, j)] = (s, regs)
+            st[("regs", b, j)] = regs
 
         def red(b, j):
             b, j = norm(b, j)
             if not ok(b):
                 return
             mx = sm(b)[0]
-            s, regs = st[("s", b, j)]
+            s, regs = st[("s", b, j)], st[("regs", b, j)]
             c0 = UCOL[j]
             if len(regs) == 2 and regs[0][0] == regs[1][0]:
                 nc.vector.tensor_reduce(out=mx[:, c0:c0 + 2], in_=s[:].rearrange("i (x c) -> i x c", x=2), axis=AX.X, op=ALU.max)
@@ -280,24 +289,24 @@ def tile_attend_t_kernel(tc, q, k, v, out):
                 return
             mx, nbt, rs, rinv = sm(b)
             et = ep.tile([P, 2, P, 2], BF16, name="et")
-            regs = st[("s", b, j)][1]
+            regs = st[("regs", b, j)]
             c0 = UCOL[j]
             for i, (w, flat, reg) in enumerate(regs):
                 col = regs[1][0] if (len(regs) == 2 and i == 0) else 0
                 nc.scalar.activation(out=et[:, :, col:col + w, :], in_=reg.rearrange("i (h e) p -> i h p e", e=2),
                                      func=ACT.Exp, bias=nbt[:, c0 + i:c0 + i + 1], scale=SCALE,
                                      accum_out=rs[:, rcol(*UNITS[j][i]):rcol(*UNITS[j][i]) + 1])
+            give(("s", b, j))
             st[("et", b, j)] = et
 
         def tr(b, gi):
             if not ok(b):
                 return
-            xt = ps.tile([P, 2, 2, P], F32, tag=ttag(), name="xt")
+            xt = take(("xt", b, gi), [P, 2, 2, P], F32)
             for sl, j in enumerate(GROUPS[gi]):
                 words = st[("et", b, j)][:].rearrange("i h p e -> i (h p e)").bitcast(F32)
                 for h in range(2):
                     nc.tensor.transpose(xt[:, sl, h, :], words[:, h * P:(h + 1) * P], identf[:])
-            st[("xt", b, gi)] = xt
 
         def cp(b, gi):
             if not ok(b):
@@ -309,7 +318,9 @@ def tile_attend_t_kernel(tc, q, k, v, out):
                 st[("gr", b, qi)] = gr
             gr = st[("gr", b, qi)]
             lo = 2 * (gi % 2)
-            nc.scalar.copy(out=gr[:, lo:lo + cnt].bitcast(F32), in_=st[("xt", b, gi)][:, 0:cnt].rearrange("p s h i -> p s i h"))
+            copy = nc.vector.tensor_copy if gi == 4 and b < B - 1 else nc.scalar.copy
+            copy(out=gr[:, lo:lo + cnt].bitcast(F32), in_=st[("xt", b, gi)][:, 0:cnt].rearrange("p s h i -> p s i h"))
+            give(("xt", b, gi))
 
         def qz(b, qi):
             if not ok(b):
@@ -328,7 +339,7 @@ def tile_attend_t_kernel(tc, q, k, v, out):
             if not ok(b):
                 return
             vq, vsh, vpl = vsets[b // PB % NSETS]
-            o = ps.tile([P, 4, D], F32, tag=OTAG.get((b, oi), "o"), name="o")
+            o = take(("o", b, oi), [P, 4, D], F32)
             for j in OBANK[oi]:
                 cod, sca = st[("c", b, j)]
                 for i, (g, m) in enumerate(UNITS[j]):
@@ -345,7 +356,6 @@ def tile_attend_t_kernel(tc, q, k, v, out):
                         rsc = vq[:, CB + i0:CB + i0 + D]
                     nc.tensor.matmul_mx(out=o[:, m // 2, :], lhsT=cod.bitcast(FP8X4), lhsT_scale=sca,
                                         rhs=rhs.bitcast(FP8X4), rhs_scale=rsc, start=True, stop=True)
-            st[("o", b, oi)] = o
 
         def rc(b, half):
             if not ok(b):
@@ -369,6 +379,7 @@ def tile_attend_t_kernel(tc, q, k, v, out):
             else:
                 nc.vector.tensor_tensor(out=ob[:, g], in0=o[:],
                                         in1=rinv[:, 4 * oi:4 * oi + 4].unsqueeze(2).to_broadcast([P, 4, D]), op=ALU.mult)
+            give(("o", b, oi))
             if b == B - 1 or (b, par) == (B - 2, 1):
                 for x in range(2):
                     nc.sync.dma_start(out=out[b, KVH * x + g].rearrange("(m i) d -> i m d", i=HQ)[:, par:NM:2, :], in_=ob[x:P:2, g])
@@ -383,7 +394,7 @@ def tile_attend_t_kernel(tc, q, k, v, out):
         HEAD = (slice(0, 7, 6), slice(2, 5, 2), slice(1, 8, 2))
         qttr(0, 0)
         for ms in HEAD:
-            qtcp(0, 0, ms)
+            qtcp(0, 0, ms, ms.start == 1)
         kttr(0, (1,))
         qk(0, 0)
         qk(0, 1)
@@ -392,11 +403,9 @@ def tile_attend_t_kernel(tc, q, k, v, out):
         qttr(0, 1)
         qtcp(0, 1)
         red(0, 1)
-        vrg(0, 0)
         qk(0, 2)
         qk(0, 3)
         red(0, 2)
-        vrg(0, 1)
 
         for b in range(B):
             if b % PB == 1:
@@ -408,12 +417,18 @@ def tile_attend_t_kernel(tc, q, k, v, out):
             nm(b - 2, 3)
             rc(b - 1, 0)
             red(b, 3)
+            if b == 0:
+                vrg(0, 0)
+                vrg(0, 1)
             qttr(b + 1, 0)
             pv(b - 1, 0)
             qk(b, 5)
             ex(b, 1)
             ktcp(b + 1)
             red(b, 4)
+            if b == 0:
+                vrg(1, 0)
+                vrg(1, 1)
             tr(b - 1, 3)
             qk(b, 6)
             ex(b, 2)
@@ -421,14 +436,15 @@ def tile_attend_t_kernel(tc, q, k, v, out):
             nm(b - 1, 0)
             red(b, 5)
             if b == 0:
-                vrg(1, 0)
+                vqz(0)
+                load_rest(1)
             tr(b - 1, 4)
             qk(b, 7, lambda: pv(b - 1, 1))
             ex(b, 3)
             cp(b - 1, 3)
             red(b, 6)
             if b == 0:
-                vrg(1, 1)
+                clear(vsets[1][1][:, 0])
             qttr(b + 1, 1)
             qk(b, 8)
             ex(b, 4)
@@ -437,10 +453,8 @@ def tile_attend_t_kernel(tc, q, k, v, out):
             rc(b - 1, 1)
             red(b, 7)
             if b == 0:
-                vqz(0)
-                load_rest(1)
-            if b > 0:
-                vrg(b + 2, 0)
+                clear(vsets[1][1][:, 1])
+            vrg(b + 2, 0)
             tr(b, 0)
             qk(b, 9)
             ex(b, 5)
@@ -448,18 +462,25 @@ def tile_attend_t_kernel(tc, q, k, v, out):
             qz(b - 1, 1)
             qz(b - 1, 2)
             red(b, 8)
+            if b == 0:
+                clear(vsets[1][1][:, 2])
             tr(b, 1)
             qk(b, 10, lambda: pv(b - 1, 2))
             ex(b, 6)
             cp(b, 0)
             red(b, 9)
-            vrg(b + 2, 0 if b == 0 else 1)
+            if b == 0:
+                clear(vsets[1][1][:, 3])
+                clear(vsets[1][0][:, CB:VB])
+            vrg(b + 2, 1)
             tr(b, 2)
             qk(b, 11)
             ex(b, 7)
             cp(b, 1)
             nm(b - 1, 2)
             red(b, 10)
+            if b == 0:
+                clear(vsets[1][2][:].rearrange("p m c -> p (m c)"))
             if b == B - 1:
                 tr(b, 3)
             pv(b - 1, 3)
@@ -470,8 +491,6 @@ def tile_attend_t_kernel(tc, q, k, v, out):
             if b % PB == 1:
                 vqz((b + 1) // PB)
             red(b, 11)
-            if b == 0:
-                vrg(2, 1)
 
         L = B - 1
         tr(L, 4)

@@ -186,24 +186,25 @@ def tile_attend_t_kernel(tc, q, k, v, out):
             copy(out=kt[:, ends].rearrange("d g t p -> d (g t p)"), in_=st[("tk", b, gs[0])][:, ends].rearrange("d g t p -> d (g t p)"))
             give(("tk", b, gs[0]))
 
-        def qttr(b, g):
+        def qttr(b, g, parts=(slice(0, NM),)):
             if not ok(b):
                 return
-            tq = take(("tq", b, g), [P, NM, P], BF16)
-            cols = tq[:].rearrange("d m (j t x) -> d (m j) t x", t=QROW, x=2)
-            for t in range(QROW):
-                nc.tensor.matmul(out=cols[:, :, t, :], lhsT=qbs[b][:, g, t * D:(t + 1) * D],
-                                 rhs=ident[:].rearrange("p (i x) -> p i x", x=2), start=True, stop=True)
+            tq = take(("tq", b, g, parts[0]), [P, NM, P], BF16)
+            cols = tq[:].rearrange("d m (j t x) -> d m j t x", t=QROW, x=2)
+            for ms in parts:
+                for t in range(QROW):
+                    nc.tensor.matmul(out=cols[:, ms, :, t, :], lhsT=qbs[b][:, g, t * D:(t + 1) * D],
+                                     rhs=ident[:].rearrange("p (m j x) -> p m j x", m=NM, x=2)[:, ms], start=True, stop=True)
 
-        def qtcp(b, g, ms=slice(0, NM), last=True):
+        def qtcp(b, g, parts=(slice(0, NM),), copy=nc.scalar.copy):
             if not ok(b):
                 return
-            if ms.start == 0:
+            if ("qt", b, g) not in st:
                 qt = qtp.tile([P, NM, P], BF16, name="qt%d" % g)
                 st[("qt", b, g)] = qt
-            nc.scalar.copy(out=st[("qt", b, g)][:, ms], in_=st[("tq", b, g)][:, ms])
-            if last:
-                give(("tq", b, g))
+            for ms in parts:
+                copy(out=st[("qt", b, g)][:, ms], in_=st[("tq", b, g, parts[0])][:, ms])
+            give(("tq", b, g, parts[0]))
 
         def vrg(b, g):
             if not ok(b):
@@ -373,7 +374,7 @@ def tile_attend_t_kernel(tc, q, k, v, out):
                 ob = obp.tile([P, KVH, 4, D], F32, name="ob")
                 st[("ob", b, par)] = ob
             ob = st[("ob", b, par)]
-            if (b, oi) == (B - 1, 3):
+            if (b, oi) in ((B - 1, 0), (B - 1, 3)):
                 for a in range(4):
                     nc.scalar.activation(out=ob[:, g, a], in_=o[:, a], func=ACT.Copy, scale=rinv[:, 4 * oi + a:4 * oi + a + 1])
             else:
@@ -389,19 +390,21 @@ def tile_attend_t_kernel(tc, q, k, v, out):
                     nc.sync.dma_start(out=dst[:, par:KVH * NM:2, :],
                                       in_=ob[x:P:2].rearrange("i g a d -> i (g a) d"))
 
+        FIRST = (slice(0, 7, 6),)
+        NEXT = (slice(2, 5, 2), slice(1, 8, 2))
         kttr(0, (0,))
         ktcp(0, (0,))
-        HEAD = (slice(0, 7, 6), slice(2, 5, 2), slice(1, 8, 2))
-        qttr(0, 0)
-        for ms in HEAD:
-            qtcp(0, 0, ms, ms.start == 1)
+        qttr(0, 0, FIRST)
+        qtcp(0, 0, FIRST)
+        qttr(0, 0, NEXT)
+        qtcp(0, 0, NEXT)
         kttr(0, (1,))
-        qk(0, 0)
-        qk(0, 1)
         ktcp(0, (1,))
-        red(0, 0)
         qttr(0, 1)
         qtcp(0, 1)
+        qk(0, 0)
+        qk(0, 1)
+        red(0, 0)
         red(0, 1)
         qk(0, 2)
         qk(0, 3)
@@ -494,17 +497,17 @@ def tile_attend_t_kernel(tc, q, k, v, out):
 
         L = B - 1
         tr(L, 4)
-        pv(L, 0)
-        pv(L, 1)
         cp(L, 3)
         cp(L, 4)
-        nm(L - 1, 3)
+        pv(L, 0)
+        pv(L, 1)
         rc(L, 0)
+        rc(L, 1)
+        nm(L - 1, 3)
         qz(L, 1)
         qz(L, 2)
         nm(L, 0)
         nm(L, 1)
-        rc(L, 1)
         pv(L, 2)
         pv(L, 3)
         nm(L, 2)

@@ -432,6 +432,8 @@ def tile_attend_t_kernel(tc, q, k, v, out):
             if b == 0:
                 vrg(1, 0)
                 vrg(1, 1)
+            else:
+                vrg(b + 2, 0)
             tr(b - 1, 3)
             qk(b, 6)
             ex(b, 2)
@@ -441,6 +443,8 @@ def tile_attend_t_kernel(tc, q, k, v, out):
             if b == 0:
                 vqz(0)
                 load_rest(1)
+            else:
+                vrg(b + 2, 1)
             tr(b - 1, 4)
             qk(b, 7, lambda: pv(b - 1, 1))
             ex(b, 3)
@@ -457,7 +461,6 @@ def tile_attend_t_kernel(tc, q, k, v, out):
             red(b, 7)
             if b == 0:
                 clear(vsets[1][1][:, 1])
-            vrg(b + 2, 0)
             tr(b, 0)
             qk(b, 9)
             ex(b, 5)
@@ -475,7 +478,8 @@ def tile_attend_t_kernel(tc, q, k, v, out):
             if b == 0:
                 clear(vsets[1][1][:, 3])
                 clear(vsets[1][0][:, CB:VB])
-            vrg(b + 2, 1)
+            if b == 0:
+                vrg(2, 0)
             tr(b, 2)
             qk(b, 11)
             ex(b, 7)
@@ -484,6 +488,7 @@ def tile_attend_t_kernel(tc, q, k, v, out):
             red(b, 10)
             if b == 0:
                 clear(vsets[1][2][:].rearrange("p m c -> p (m c)"))
+                vrg(2, 1)
             if b == B - 1:
                 tr(b, 3)
             pv(b - 1, 3)

@@ -319,8 +319,7 @@ def tile_attend_t_kernel(tc, q, k, v, out):
                 st[("gr", b, qi)] = gr
             gr = st[("gr", b, qi)]
             lo = 2 * (gi % 2)
-            copy = nc.vector.tensor_copy if gi == 4 and b < B - 1 else nc.scalar.copy
-            copy(out=gr[:, lo:lo + cnt].bitcast(F32), in_=st[("xt", b, gi)][:, 0:cnt].rearrange("p s h i -> p s i h"))
+            nc.scalar.copy(out=gr[:, lo:lo + cnt].bitcast(F32), in_=st[("xt", b, gi)][:, 0:cnt].rearrange("p s h i -> p s i h"))
             give(("xt", b, gi))
 
         def qz(b, qi):
@@ -475,6 +474,8 @@ def tile_attend_t_kernel(tc, q, k, v, out):
             ex(b, 6)
             cp(b, 0)
             red(b, 9)
+            if b % PB == 1:
+                vqz((b + 1) // PB)
             if b == 0:
                 clear(vsets[1][1][:, 3])
                 clear(vsets[1][0][:, CB:VB])
@@ -495,10 +496,8 @@ def tile_attend_t_kernel(tc, q, k, v, out):
             qk(b, 12)
             ex(b, 8)
             cp(b, 2)
-            qz(b, 0)
-            if b % PB == 1:
-                vqz((b + 1) // PB)
             red(b, 11)
+            qz(b, 0)
 
         L = B - 1
         tr(L, 4)

@@ -181,7 +181,7 @@ def tile_attend_t_kernel(tc, q, k, v, out):
                 kt = qtp.tile([P, KVH, PACK, P], BF16, name="kt")
                 st[("kt", b)] = kt
             kt = st[("kt", b)]
-            copy = nc.vector.tensor_copy if b % 2 == 0 else nc.scalar.copy
+            copy = nc.vector.tensor_copy if b == 0 else nc.scalar.copy
             ends = slice(gs[0], gs[-1] + 1)
             copy(out=kt[:, ends].rearrange("d g t p -> d (g t p)"), in_=st[("tk", b, gs[0])][:, ends].rearrange("d g t p -> d (g t p)"))
             give(("tk", b, gs[0]))

@@ -357,11 +357,11 @@ def tile_attend_t_kernel(tc, q, k, v, out):
                     nc.tensor.matmul_mx(out=o[:, m // 2, :], lhsT=cod.bitcast(FP8X4), lhsT_scale=sca,
                                         rhs=rhs.bitcast(FP8X4), rhs_scale=rsc, start=True, stop=True)
 
-        def rc(b, half):
+        def rc(b):
             if not ok(b):
                 return
             mx, nbt, rs, rinv = sm(b)
-            nc.vector.reciprocal(out=rinv[:, 8 * half:8 * half + 8], in_=rs[:, 8 * half:8 * half + 8])
+            nc.vector.reciprocal(out=rinv[:], in_=rs[:])
 
         def nm(b, oi):
             if not ok(b):
@@ -417,7 +417,6 @@ def tile_attend_t_kernel(tc, q, k, v, out):
             qk(b, 4)
             ex(b, 0)
             nm(b - 2, 3)
-            rc(b - 1, 0)
             red(b, 3)
             if b == 0:
                 vrg(0, 0)
@@ -426,6 +425,7 @@ def tile_attend_t_kernel(tc, q, k, v, out):
             pv(b - 1, 0)
             qk(b, 5)
             ex(b, 1)
+            rc(b - 1)
             ktcp(b + 1)
             red(b, 4)
             if b == 0:
@@ -445,7 +445,8 @@ def tile_attend_t_kernel(tc, q, k, v, out):
             else:
                 vrg(b + 2, 1)
             tr(b - 1, 4)
-            qk(b, 7, lambda: pv(b - 1, 1))
+            pv(b - 1, 1)
+            qk(b, 7)
             ex(b, 3)
             cp(b - 1, 3)
             red(b, 6)
@@ -456,7 +457,6 @@ def tile_attend_t_kernel(tc, q, k, v, out):
             ex(b, 4)
             cp(b - 1, 4)
             nm(b - 1, 1)
-            rc(b - 1, 1)
             red(b, 7)
             if b == 0:
                 clear(vsets[1][1][:, 1])
@@ -470,7 +470,8 @@ def tile_attend_t_kernel(tc, q, k, v, out):
             if b == 0:
                 clear(vsets[1][1][:, 2])
             tr(b, 1)
-            qk(b, 10, lambda: pv(b - 1, 2))
+            pv(b - 1, 2)
+            qk(b, 10)
             ex(b, 6)
             cp(b, 0)
             red(b, 9)
@@ -505,8 +506,7 @@ def tile_attend_t_kernel(tc, q, k, v, out):
         cp(L, 4)
         pv(L, 0)
         pv(L, 1)
-        rc(L, 0)
-        rc(L, 1)
+        rc(L)
         nm(L - 1, 3)
         qz(L, 1)
         qz(L, 2)

import math
from contextlib import ExitStack

import concourse.mybir as mybir
from concourse.masks import make_identity

BF16 = mybir.dt.bfloat16
F32 = mybir.dt.float32
I32 = mybir.dt.int32
U32 = mybir.dt.uint32
U8 = mybir.dt.uint8
FP8X4 = mybir.dt.float8_e4m3fn_x4
ALU = mybir.AluOpType
ACT = mybir.ActivationFunctionType
AX = mybir.AxisListType

B, H, KVH, N, D = 8, 4, 2, 512, 128
P = 128
PACK = 4
SCALE = 1.0 / math.sqrt(D)
NEG = -1.0e30
FLOPS = 4 * B * H * N * N * D
HQ = 64
NM = N // HQ
QROW = N // HQ
SL = HQ // PACK
NSETS = 2
PB = 2
CB = PB * 2 * D * 4
VB = CB + PB * 2 * D

UNITS = [[(0, 0), (0, 6)], [(0, 2), (0, 4)], [(1, 0), (1, 6)], [(1, 2), (1, 4)], [(0, 1), (0, 5)], [(0, 7)],
         [(1, 1), (1, 5)], [(1, 7)], [(0, 3), (1, 3)]]
NU = len(UNITS)
UCOL = [0, 2, 4, 6, 8, 10, 11, 13, 14]
GROUPS = [[0, 1], [2, 3], [4, 5], [6, 7], [8]]
QGROUP = [[0, 1], [2, 3], [4]]
OBANK = [[0, 1], [2, 3], [4, 5, 8], [6, 7, 8]]


def width(m):
    return SL * (m + 1)


def shift(m):
    return P - width(m) if m <= 3 else 0


def plane_row(blk):
    return 32 * (blk // 4) + blk % 4


def tile_attend_t_kernel(tc, q, k, v, out):
    nc = tc.nc
    with ExitStack() as ctx:
        ctx.enter_context(tc.manual_schedule())
        const = ctx.enter_context(tc.tile_pool(name="const", bufs=1))
        qtp = ctx.enter_context(tc.tile_pool(name="qtp", bufs=2))
        vgp = ctx.enter_context(tc.tile_pool(name="vgp", bufs=2))
        ep = ctx.enter_context(tc.tile_pool(name="ep", bufs=8))
        gp = ctx.enter_context(tc.tile_pool(name="gp", bufs=2))
        cpl = ctx.enter_context(tc.tile_pool(name="cpl", bufs=2))
        small = ctx.enter_context(tc.tile_pool(name="small", bufs=4))
        obp = ctx.enter_context(tc.tile_pool(name="obp", bufs=4))
        ps = ctx.enter_context(tc.psum_pool(name="ps", bufs=1))

        st = {}
        free = ["b%d" % i for i in range(8)]

        def take(key, shape, dt):
            tag = free[0]
            free.remove(tag)
            tile = ps.tile(shape, dt, tag=tag, name="bank")
            st[key] = tile
            st[("tag", key)] = tag
            return tile

        def give(key):
            free.append(st[("tag", key)])

        def ok(b):
            return 0 <= b < B

        kbs = [const.tile([P, PB, KVH, N], BF16, name="kb%d" % i) for i in range(B // PB)]
        vbs = [const.tile([P, PB, KVH, N], BF16, name="vb%d" % i) for i in range(B // PB)]
        qbs = [const.tile([P, KVH, QROW * D], BF16, name="qb%d" % i) for i in range(B)]

        def load_q(b):
            for x in range(2):
                nc.sync.dma_start(out=qbs[b][x:P:2], in_=q[b, KVH * x:KVH * (x + 1)].rearrange("g (p t) d -> p g (t d)", t=QROW))

        def load_kv(dst, src, b):
            nc.sync.dma_start(out=dst[b // PB][:, b % PB], in_=src[b].rearrange("g (p t) d -> p g (t d)", t=PACK))

        def load_pair(dst, src, i):
            nc.sync.dma_start(out=dst[i][:].rearrange("p b g c -> p (b g) c"),
                              in_=src[PB * i:PB * (i + 1)].rearrange("b g (p t) d -> p (b g) (t d)", t=PACK))

        def load_first(i):
            if 0 < i < B // PB:
                load_pair(kbs, k, i)
                load_q(PB * i)
                load_pair(vbs, v, i)

        def load_rest(i):
            if 0 < i < B // PB:
                load_q(PB * i + 1)

        for g in range(KVH):
            nc.sync.dma_start(out=kbs[0][:, 0, g], in_=k[0, g].rearrange("(p t) d -> p (t d)", t=PACK))
            for x in range(2):
                nc.sync.dma_start(out=qbs[0][x:P:2, g], in_=q[0, KVH * x + g].rearrange("(p t) d -> p (t d)", t=QROW))
        load_kv(kbs, k, 1)
        load_kv(vbs, v, 0)
        load_q(1)
        load_kv(vbs, v, 1)
        load_first(1)

        warm = const.tile([P, 2], F32, name="warm")
        nc.vector.memset(warm[:], 0.0)
        nc.scalar.activation(out=warm[:, 1:2], in_=warm[:, 0:1], func=ACT.Exp)

        zero = const.tile([P, N], BF16, name="zero")
        nc.vector.memset(zero[:], 0.0)
        for i in range(4):
            dummy = take("dummy", [P, N], F32)
            nc.tensor.matmul(out=dummy[:], lhsT=zero[:, 0:P], rhs=zero[:], start=True, stop=True)
            give("dummy")

        vsets = []
        for j in range(NSETS):
            vq = const.tile([P, VB], U8, name="vq%d" % j, align_bytes=64)
            vsh = const.tile([P, NM // 2, VB], U8, name="vsh%d" % j, align_bytes=64)
            vpl = const.tile([P, NM // 2, VB - CB], U8, name="vpl%d" % j, align_bytes=64)
            vsets.append((vq, vsh, vpl))

        def clear(tile):
            nc.vector.memset(tile.bitcast(I32), 0)

        clear(vsets[0][0][:, CB:VB])
        clear(vsets[0][1][:].rearrange("p m c -> p (m c)"))
        clear(vsets[0][2][:].rearrange("p m c -> p (m c)"))

        ident = const.tile([P, P], BF16, name="ident")
        make_identity(nc, ident[:])
        identf = const.tile([P, P], F32, name="identf")
        make_identity(nc, identf[:])
        m32 = const.tile([P, HQ], F32, name="m32")
        nc.gpsimd.memset(m32[:], 0.0)
        nc.gpsimd.affine_select(
            out=m32[:], in_=m32[:], compare_op=ALU.is_ge, fill=NEG, base=0,
            pattern=[[-2, PACK], [-2 * PACK, SL]], channel_multiplier=1,
        )
        maskb = const.tile([P, PACK, SL], BF16, name="maskb")
        nc.vector.tensor_copy(out=maskb[:].rearrange("i t p -> i (t p)"), in_=m32[:])

        def move(dst, src):
            nc.sync.dma_start(out=dst.bitcast(I32), in_=src.bitcast(I32))

        def sm(b):
            if ("sm", b) not in st:
                mx = small.tile([P, 16], F32, name="mx")
                nbt = small.tile([P, 16], F32, name="nbt")
                rs = small.tile([P, 16], F32, name="rs")
                rinv = small.tile([P, 16], F32, name="rinv")
                st[("sm", b)] = (mx, nbt, rs, rinv)
            return st[("sm", b)]

        def kttr(b, gs=(0, 1)):
            if not ok(b):
                return
            tk = take(("tk", b, gs[0]), [P, KVH, PACK, P], BF16)
            for g in gs:
                for t in range(PACK):
                    nc.tensor.matmul(out=tk[:, g, t, :], lhsT=kbs[b // PB][:, b % PB, g, t * D:(t + 1) * D], rhs=ident[:], start=True, stop=True)

        def ktcp(b, gs=(0, 1)):
            if not ok(b):
                return
            if gs[0] == 0:
                kt = qtp.tile([P, KVH, PACK, P], BF16, name="kt")
                st[("kt", b)] = kt
            kt = st[("kt", b)]
            copy = nc.vector.tensor_copy if b == 0 else nc.scalar.copy
            ends = slice(gs[0], gs[-1] + 1)
            copy(out=kt[:, ends].rearrange("d g t p -> d (g t p)"), in_=st[("tk", b, gs[0])][:, ends].rearrange("d g t p -> d (g t p)"))
            give(("tk", b, gs[0]))

        def qttr(b, g, parts=(slice(0, NM),)):
            if not ok(b):
                return
            tq = take(("tq", b, g, parts[0]), [P, NM, P], BF16)
            cols = tq[:].rearrange("d m (j t x) -> d m j t x", t=QROW, x=2)
            for ms in parts:
                for t in range(QROW):
                    nc.tensor.matmul(out=cols[:, ms, :, t, :], lhsT=qbs[b][:, g, t * D:(t + 1) * D],
                                     rhs=ident[:].rearrange("p (m j x) -> p m j x", m=NM, x=2)[:, ms], start=True, stop=True)

        def qtcp(b, g, parts=(slice(0, NM),), copy=nc.scalar.copy):
            if not ok(b):
                return
            if ("qt", b, g) not in st:
                qt = qtp.tile([P, NM, P], BF16, name="qt%d" % g)
                st[("qt", b, g)] = qt
            for ms in parts:
                copy(out=st[("qt", b, g)][:, ms], in_=st[("tq", b, g, parts[0])][:, ms])
            give(("tq", b, g, parts[0]))

        def vrg(b, g):
            if not ok(b):
                return
            if b % PB == 0 and g == 0:
                vg = vgp.tile([P, PB, KVH, D, PACK], BF16, name="vg", align_bytes=64)
                st[("vg", b // PB)] = vg
            vg = st[("vg", b // PB)]
            src = vbs[b // PB][:, b % PB, g, :].rearrange("p (t d) -> p d t", t=PACK)
            if b < PB:
                nc.vector.tensor_copy(out=vg[:, b % PB, g], in_=src)
            else:
                nc.gpsimd.tensor_scalar(out=vg[:, b % PB, g], in0=src, scalar1=1.0, scalar2=0.0, op0=ALU.mult, op1=ALU.add)

        def vqz(i):
            if not 0 <= i < B // PB:
                return
            vq, vsh, vpl = vsets[i % NSETS]
            nc.vector.quantize_mx(out=vq[:, 0:CB].bitcast(FP8X4), scales=vq[:, CB:VB],
                                  in_=st[("vg", i)][:].rearrange("p b g d t -> p (b g d t)"))
            move(vsh[112:128, 0, 0:CB], vq[0:16, 0:CB])
            move(vsh[98:100, 0, CB:VB], vq[0:2, CB:VB])
            move(vsh[96:128, 1], vq[0:32])
            move(vsh[80:112, 2, 0:CB], vq[0:32, 0:CB])
            move(vsh[112:128, 2, 0:CB], vq[32:48, 0:CB])
            move(vsh[66:68, 2, CB:VB], vq[0:2, CB:VB])
            move(vsh[96:98, 2, CB:VB], vq[2:4, CB:VB])
            move(vsh[98:100, 2, CB:VB], vq[32:34, CB:VB])
            move(vsh[64:128, 3], vq[0:64])
            for lo, cnt, m0 in ((0, 64, 0), (64, 2, 1), (66, 2, 2), (96, 2, 3)):
                rows = slice(lo, lo + cnt)
                nc.sync.dma_start(out=vpl[rows, m0:NM // 2].bitcast(I32),
                                  in_=vq[rows, CB:VB].bitcast(I32).unsqueeze(1).to_broadcast([cnt, NM // 2 - m0, (VB - CB) // 4]))

        def rcol(g, m):
            return 8 * (m % 2) + 4 * g + m // 2

        def norm(b, j):
            return b + j // NU, j % NU

        def qk(b, j, mid=None):
            b, j = norm(b, j)
            if not ok(b):
                if mid is not None:
                    mid()
                return
            kt = st[("kt", b)]
            s = take(("s", b, j), [P, N], F32)
            regs = []
            off = 0
            for (g, m) in UNITS[j]:
                w = width(m)
                flat = s[:, off:off + PACK * w]
                reg = flat.rearrange("i (t p) -> i t p", t=PACK)
                nc.tensor.matmul(out=reg, lhsT=st[("qt", b, g)][:, m, :], rhs=kt[:, g, :, 0:w], start=True, stop=False)
                if mid is not None and off == 0 and len(UNITS[j]) == 1:
                    mid()
                nc.tensor.matmul(out=reg[:, :, w - SL:w], lhsT=ident[:], rhs=maskb[:], start=False, stop=True)
                if mid is not None and off == 0 and len(UNITS[j]) == 2:
                    mid()
                regs.append((w, flat, reg))
                off += PACK * w
            st[("regs", b, j)] = regs

        def red(b, j):
            b, j = norm(b, j)
            if not ok(b):
                return
            mx = sm(b)[0]
            s, regs = st[("s", b, j)], st[("regs", b, j)]
            c0 = UCOL[j]
            if len(regs) == 2 and regs[0][0] == regs[1][0]:
                nc.vector.tensor_reduce(out=mx[:, c0:c0 + 2], in_=s[:].rearrange("i (x c) -> i x c", x=2), axis=AX.X, op=ALU.max)
            else:
                for i, (w, flat, reg) in enumerate(regs):
                    nc.vector.tensor_reduce(out=mx[:, c0 + i:c0 + i + 1], in_=flat, axis=AX.X, op=ALU.max)
            c1 = c0 + len(regs)
            nc.gpsimd.tensor_scalar(out=sm(b)[1][:, c0:c1], in0=mx[:, c0:c1], scalar1=-SCALE, scalar2=0.0,
                                    op0=ALU.mult, op1=ALU.add)

        def ex(b, j):
            if not ok(b):
                return
            mx, nbt, rs, rinv = sm(b)
            et = ep.tile([P, 2, P, 2], BF16, name="et")
            regs = st[("regs", b, j)]
            c0 = UCOL[j]
            for i, (w, flat, reg) in enumerate(regs):
                col = regs[1][0] if (len(regs) == 2 and i == 0) else 0
                nc.scalar.activation(out=et[:, :, col:col + w, :], in_=reg.rearrange("i (h e) p -> i h p e", e=2),
                                     func=ACT.Exp, bias=nbt[:, c0 + i:c0 + i + 1], scale=SCALE,
                                     accum_out=rs[:, rcol(*UNITS[j][i]):rcol(*UNITS[j][i]) + 1])
            give(("s", b, j))
            st[("et", b, j)] = et

        def tr(b, gi):
            if not ok(b):
                return
            xt = take(("xt", b, gi), [P, 2, 2, P], F32)
            for sl, j in enumerate(GROUPS[gi]):
                words = st[("et", b, j)][:].rearrange("i h p e -> i (h p e)").bitcast(F32)
                for h in range(2):
                    nc.tensor.transpose(xt[:, sl, h, :], words[:, h * P:(h + 1) * P], identf[:])

        def cp(b, gi):
            if not ok(b):
                return
            cnt = len(GROUPS[gi])
            qi = gi // 2
            if gi % 2 == 0:
                gr = gp.tile([P, 2 * len(QGROUP[qi]), P, PACK], BF16, name="gr%d" % qi, align_bytes=64)
                st[("gr", b, qi)] = gr
            gr = st[("gr", b, qi)]
            lo = 2 * (gi % 2)
            nc.scalar.copy(out=gr[:, lo:lo + cnt].bitcast(F32), in_=st[("xt", b, gi)][:, 0:cnt].rearrange("p s h i -> p s i h"))
            give(("xt", b, gi))

        def qz(b, qi):
            if not ok(b):
                return
            units = [j for gi in QGROUP[qi] for j in GROUPS[gi]]
            cnt = len(units)
            gr = st[("gr", b, qi)]
            ec = cpl.tile([P, 4 * P], U32, name="ec%d" % qi, align_bytes=64)
            esc = cpl.tile([P, 4 * P], U8, name="esc%d" % qi, align_bytes=64)
            nc.vector.quantize_mx(out=ec[:, 0:cnt * P].bitcast(FP8X4), scales=esc[:, 0:cnt * P],
                                  in_=gr[:, 0:cnt].rearrange("p s i t -> p (s i t)"))
            for sl, j in enumerate(units):
                st[("c", b, j)] = (ec[:, sl * P:(sl + 1) * P], esc[:, sl * P:(sl + 1) * P])

        def pv(b, oi):
            if not ok(b):
                return
            vq, vsh, vpl = vsets[b // PB % NSETS]
            o = take(("o", b, oi), [P, 4, D], F32)
            for j in OBANK[oi]:
                cod, sca = st[("c", b, j)]
                for i, (g, m) in enumerate(UNITS[j]):
                    if 2 * (m % 2) + g != oi:
                        continue
                    shifted = len(UNITS[j]) == 2 and i == 0
                    i0 = (b % PB * KVH + g) * D
                    rhs = vsh[:, m, PACK * i0:PACK * (i0 + D)] if shifted else vq[:, PACK * i0:PACK * (i0 + D)]
                    if shifted:
                        rsc = vsh[:, m, CB + i0:CB + i0 + D]
                    elif m < NM - 1:
                        rsc = vpl[:, m - 3, i0:i0 + D]
                    else:
                        rsc = vq[:, CB + i0:CB + i0 + D]
                    nc.tensor.matmul_mx(out=o[:, m // 2, :], lhsT=cod.bitcast(FP8X4), lhsT_scale=sca,
                                        rhs=rhs.bitcast(FP8X4), rhs_scale=rsc, start=True, stop=True)

        def rc(b):
            if not ok(b):
                return
            mx, nbt, rs, rinv = sm(b)
            nc.vector.reciprocal(out=rinv[:], in_=rs[:])

        def nm(b, oi):
            if not ok(b):
                return
            o = st[("o", b, oi)]
            rinv = sm(b)[3]
            g, par = oi % 2, oi // 2
            if g == 0:
                ob = obp.tile([P, KVH, 4, D], F32, name="ob")
                st[("ob", b, par)] = ob
            ob = st[("ob", b, par)]
            if (b, oi) in ((B - 1, 0), (B - 1, 3)):
                for a in range(4):
                    nc.scalar.activation(out=ob[:, g, a], in_=o[:, a], func=ACT.Copy, scale=rinv[:, 4 * oi + a:4 * oi + a + 1])
            else:
                nc.vector.tensor_tensor(out=ob[:, g], in0=o[:],
                                        in1=rinv[:, 4 * oi:4 * oi + 4].unsqueeze(2).to_broadcast([P, 4, D]), op=ALU.mult)
            give(("o", b, oi))
            if b == B - 1 or (b, par) == (B - 2, 1):
                for x in range(2):
                    nc.sync.dma_start(out=out[b, KVH * x + g].rearrange("(m i) d -> i m d", i=HQ)[:, par:NM:2, :], in_=ob[x:P:2, g])
            elif g == KVH - 1:
                for x in range(2):
                    dst = out[b, KVH * x:KVH * (x + 1)].rearrange("g (m i) d -> i (g m) d", i=HQ)
                    nc.sync.dma_start(out=dst[:, par:KVH * NM:2, :],
                                      in_=ob[x:P:2].rearrange("i g a d -> i (g a) d"))

        FIRST = (slice(0, 7, 6),)
        NEXT = (slice(2, 5, 2), slice(1, 8, 2))
        kttr(0, (0,))
        ktcp(0, (0,))
        qttr(0, 0, FIRST)
        qtcp(0, 0, FIRST)
        qttr(0, 0, NEXT)
        qtcp(0, 0, NEXT)
        kttr(0, (1,))
        ktcp(0, (1,))
        qttr(0, 1)
        qtcp(0, 1)
        qk(0, 0)
        qk(0, 1)
        red(0, 0)
        red(0, 1)
        qk(0, 2)
        qk(0, 3)
        red(0, 2)

        for b in range(B):
            if b % PB == 1:
                load_first((b + 3) // PB)
                load_rest((b + 3) // PB)
            kttr(b + 1)
            qk(b, 4)
            ex(b, 0)
            nm(b - 2, 3)
            red(b, 3)
            if b == 0:
                vrg(0, 0)
                vrg(0, 1)
            qttr(b + 1, 0)
            pv(b - 1, 0)
            qk(b, 5)
            ex(b, 1)
            rc(b - 1)
            ktcp(b + 1)
            red(b, 4)
            if b == 0:
                vrg(1, 0)
                vrg(1, 1)
            else:
                vrg(b + 2, 0)
            tr(b - 1, 3)
            qk(b, 6)
            ex(b, 2)
            qtcp(b + 1, 0)
            nm(b - 1, 0)
            red(b, 5)
            if b == 0:
                vqz(0)
                load_rest(1)
            else:
                vrg(b + 2, 1)
            tr(b - 1, 4)
            pv(b - 1, 1)
            qk(b, 7)
            ex(b, 3)
            cp(b - 1, 3)
            red(b, 6)
            if b == 0:
                clear(vsets[1][1][:, 0])
            qttr(b + 1, 1)
            qk(b, 8)
            ex(b, 4)
            cp(b - 1, 4)
            nm(b - 1, 1)
            red(b, 7)
            if b == 0:
                clear(vsets[1][1][:, 1])
            tr(b, 0)
            qk(b, 9)
            ex(b, 5)
            qtcp(b + 1, 1)
            qz(b - 1, 1)
            qz(b - 1, 2)
            red(b, 8)
            if b == 0:
                clear(vsets[1][1][:, 2])
            tr(b, 1)
            pv(b - 1, 2)
            qk(b, 10)
            ex(b, 6)
            cp(b, 0)
            red(b, 9)
            if b % PB == 1:
                vqz((b + 1) // PB)
            if b == 0:
                clear(vsets[1][1][:, 3])
                clear(vsets[1][0][:, CB:VB])
            if b == 0:
                vrg(2, 0)
            tr(b, 2)
            qk(b, 11)
            ex(b, 7)
            cp(b, 1)
            nm(b - 1, 2)
            red(b, 10)
            if b == 0:
                clear(vsets[1][2][:].rearrange("p m c -> p (m c)"))
                vrg(2, 1)
            if b == B - 1:
                tr(b, 3)
            pv(b - 1, 3)
            qk(b, 12)
            ex(b, 8)
            cp(b, 2)
            red(b, 11)
            qz(b, 0)

        L = B - 1
        tr(L, 4)
        cp(L, 3)
        cp(L, 4)
        pv(L, 0)
        pv(L, 1)
        rc(L)
        nm(L - 1, 3)
        qz(L, 1)
        qz(L, 2)
        nm(L, 0)
        nm(L, 1)
        pv(L, 2)
        pv(L, 3)
        nm(L, 2)
        nm(L, 3)
